import numpy as np
import ml_dtypes


def mxq(x, axis, fmt="e4m3"):
    dtype, down = {"e4m3": (ml_dtypes.float8_e4m3fn, 7), "e5m2": (ml_dtypes.float8_e5m2, 14)}[fmt]
    v = np.moveaxis(np.asarray(x, np.float32).astype(ml_dtypes.bfloat16).astype(np.float64), axis, -1)
    blocks = v.reshape(v.shape[:-1] + (-1, 32))
    amax = np.abs(blocks).max(-1, keepdims=True)
    byte = np.maximum(np.where(amax > 0, np.frexp(amax)[1] - 1 + 127, 0) - down, 1)
    scale = np.exp2(byte - 127.0)
    codes = (blocks / scale).astype(np.float32).astype(dtype).astype(np.float64)
    return np.moveaxis((codes * scale).reshape(v.shape), -1, axis)


WIDE = False


def mx_kscale(k):
    if not WIDE:
        return np.ones(k)
    levels = np.array([10, -10, 5, -5, 0])
    a = np.random.permutation(np.resize(levels, k // 512 * 4)).reshape(k // 512, 4)
    idx = np.arange(k)
    return np.exp2(a[idx // 512, idx % 128 // 32])


BF16 = ml_dtypes.bfloat16


def bf(x):
    return np.asarray(x, np.float32).astype(BF16)


def f64(x):
    return np.asarray(x).astype(np.float64)


E2M1 = np.array([0.0, 0.5, 1.0, 1.5, 2.0, 3.0, 4.0, 6.0, -0.0, -0.5, -1.0, -1.5, -2.0, -3.0, -4.0, -6.0])


def pack_weight(w, fmt):
    k, n = w.shape
    w = f64(bf(w)).reshape(k // 32, 32, n)
    amax = np.abs(w).max(1)
    if fmt == "e4m3":
        byte = np.frexp(amax)[1] - 1 + 127 - 7
    else:
        mant, ex = np.frexp(amax / 6.0)
        byte = np.where(mant > 0.5, ex, ex - 1) + 127
    byte = np.clip(np.where(amax > 0, byte, 1), 1, 254)
    scaled = (w * np.exp2(127.0 - byte)[:, None, :]).reshape(k, n).astype(np.float32)
    by_word = np.ascontiguousarray(scaled.reshape(k // 512, 128, 4, n).transpose(0, 1, 3, 2))
    if fmt == "e4m3":
        words = by_word.astype(ml_dtypes.float8_e4m3fn).view(np.uint8)
    else:
        c = by_word.astype(ml_dtypes.float4_e2m1fn).view(np.uint8) & 0xF
        words = c[..., 0::2] | (c[..., 1::2] << 4)
    return np.ascontiguousarray(words), np.ascontiguousarray(byte.astype(np.uint8).reshape(k // 512, 16, n))


def unpack_weight(words, scales, fmt):
    g, p, n, _ = words.shape
    if fmt == "e4m3":
        vals = np.ascontiguousarray(words).view(ml_dtypes.float8_e4m3fn).astype(np.float64)
    else:
        nib = np.empty((g, p, n, 4), np.uint8)
        nib[..., 0::2] = words & 0xF
        nib[..., 1::2] = words >> 4
        vals = E2M1[nib]
    vals = vals * np.repeat(np.exp2(scales.astype(np.float64) - 127.0), 8, axis=1)[..., None]
    return vals.transpose(0, 1, 3, 2).reshape(g * 512, n)


B, T, E, Q = 4, 512, 512, 2048
EPS_RMS = 1.1920929e-07


def silu(t):
    return t * (1.0 / (1.0 + np.exp(-t)))


def rms_norm(t):
    return t * (1.0 / np.sqrt(np.mean(t * t, axis=-1, keepdims=True) + EPS_RMS))


def w_norm(w, n):
    target_std = n ** (-0.5)
    return w * (target_std / (np.std(w, ddof=1) + 1e-08))


def setup_inputs():
    s = mx_kscale(E)
    u = s / s.min()
    row = np.where(u > 1.0, np.sqrt(EPS_RMS) / u, np.sqrt(T / (B * E)) * np.exp2(np.random.uniform(-1.0, 1.0, E)))
    ao = bf(np.random.standard_normal((E, E)) * row[:, None])
    w_swiglu = bf((np.random.standard_normal((E, 2 * Q)) / np.sqrt(Q) * u[:, None]).reshape(2 * E, Q))
    w_out = bf(np.random.standard_normal((E, E)) / np.sqrt(E) * u)
    out_w = (np.random.standard_normal((E, E)) * np.sqrt(E) + 2.0) / E * u[:, None]
    out_w_words, out_w_scales = pack_weight(np.ascontiguousarray(out_w.T), "e4m3")
    tao = bf(np.random.uniform(0.5, 1.5, (2, 1)) * np.random.choice([-1.0, 1.0], (2, 1)))
    return {"ao": ao,
            "w_swiglu": w_swiglu,
            "w_out": w_out,
            "out_w_words": out_w_words,
            "out_w_scales": out_w_scales,
            "tao": tao}


def reference(ao, w_swiglu, w_out, out_w_words, out_w_scales, tao):
    ws, wo = f64(w_swiglu), f64(w_out)
    g = np.clip(np.abs(f64(tao)), 1e-08, 1.0)
    beta, gamma = g[0], g[1]
    aoq = mxq(rms_norm(f64(ao)), 0, "e4m3")
    owq = unpack_weight(out_w_words, out_w_scales, "e4m3")
    n2 = silu(mxq(ws.reshape(E, 2 * Q).T, 1, "e4m3") @ aoq)
    n2 = mxq(n2, 1, "e4m3") @ owq
    ws_new = w_norm(ws + n2.T.reshape(2 * E, Q), Q) * beta
    n3 = silu(mxq(wo, 1, "e4m3") @ aoq)
    wo_new = w_norm(wo + (mxq(n3, 1, "e4m3") @ owq), Q) * gamma
    return ws_new, wo_new

@@ -1,0 +1,301 @@
+from contextlib import ExitStack
+
+import concourse.mybir as mybir
+from concourse.masks import make_identity
+
+F32 = mybir.dt.float32
+BF16 = mybir.dt.bfloat16
+I32 = mybir.dt.int32
+U32 = mybir.dt.uint32
+U8 = mybir.dt.uint8
+FP8X4 = mybir.dt.float8_e4m3fn_x4
+ACT = mybir.ActivationFunctionType
+ALU = mybir.AluOpType
+
+P = 128
+PACK = 4
+E = P * PACK
+HALVES = 2
+Q = 2048
+BLOCK = 512
+BLOCKS_PER_HALF = Q // BLOCK
+V_BLOCKS = HALVES * BLOCKS_PER_HALF
+COUNT_1 = E * HALVES * Q
+COUNT_2 = E * E
+PARTS = V_BLOCKS * PACK
+EPS_RMS = 1.1920929e-07
+EPS_STD = 1e-08
+TARGET_STD = 2048.0**-0.5
+BLOCKS_GROUPED_BY_SCALAR = 2
+AHEAD = 2
+
+FLOPS = 2 * 2 * E * E * (HALVES * Q + E)
+
+
+def first_stage(nc, psum_first, stage, a_codes, a_scales, x_codes, x_scales):
+    h_grouped = stage.tile([P, BLOCK, PACK], BF16, align_bytes=64)
+    for s in range(BLOCK // P):
+        cols = slice(s * P, (s + 1) * P)
+        bank = psum_first.tile([P, PACK, P], F32)
+        for t in range(PACK):
+            e_slice = slice(t * P, (t + 1) * P)
+            nc.tensor.matmul_mx(
+                out=bank[:, t, :],
+                lhsT=a_codes[:, e_slice].bitcast(FP8X4),
+                lhsT_scale=a_scales[:, e_slice],
+                rhs=x_codes[:, cols].bitcast(FP8X4),
+                rhs_scale=x_scales[:, cols],
+                start=True,
+                stop=True,
+            )
+        nc.scalar.activation(
+            out=h_grouped[:, cols, :], in_=bank[:].rearrange("p t j -> p j t"), func=ACT.Silu
+        )
+    h_codes = stage.tile([P, BLOCK], U32, align_bytes=64)
+    h_scales = stage.tile([P, BLOCK], U8, align_bytes=64)
+    nc.vector.quantize_mx(
+        out=h_codes[:].bitcast(FP8X4),
+        scales=h_scales[:],
+        in_=h_grouped[:].rearrange("p j t -> p (j t)"),
+    )
+    return h_codes, h_scales
+
+
+def add_weight_and_measure(nc, stage, z, product, weight, stats, part):
+    nc.vector.scalar_tensor_tensor(
+        out=z,
+        in0=product,
+        scalar=1.0,
+        in1=weight,
+        op0=ALU.mult,
+        op1=ALU.add,
+        accum_out=stats[:, 0, part : part + 1],
+    )
+    squares = stage.tile([P, BLOCK], BF16)
+    nc.scalar.activation(
+        out=squares[:], in_=z, func=ACT.Square, accum_out=stats[:, 1, part : part + 1]
+    )
+
+
+def norm_factor(nc, psum_second, keep, stats, mean_of, count, inv_gate, name):
+    spread = psum_second.tile([P, 2 * PARTS], F32, tag="product")
+    nc.tensor.matmul(
+        out=spread[:], lhsT=mean_of[:], rhs=stats[:].rearrange("p s k -> p (s k)"), start=True, stop=True
+    )
+    moments = keep.tile([P, 2], F32, name=name + "_moments")
+    nc.vector.tensor_reduce(
+        out=moments[:],
+        in_=spread[:].rearrange("p (s k) -> p s k", s=2),
+        axis=mybir.AxisListType.X,
+        op=ALU.add,
+    )
+    minus_var = keep.tile([P, 1], F32, name=name + "_minus_var")
+    nc.vector.scalar_tensor_tensor(
+        out=minus_var[:],
+        in0=moments[:, 0:1],
+        scalar=moments[:, 0:1],
+        in1=moments[:, 1:2],
+        op0=ALU.mult,
+        op1=ALU.subtract,
+    )
+    std = keep.tile([P, 1], F32, name=name + "_std")
+    nc.scalar.activation(out=std[:], in_=minus_var[:], func=ACT.Sqrt, scale=-count / (count - 1.0))
+    factor = keep.tile([P, 1], F32, name=name + "_factor")
+    nc.vector.tensor_scalar(
+        out=factor[:], in0=std[:], scalar1=EPS_STD, scalar2=inv_gate, op0=ALU.add, op1=ALU.mult
+    )
+    nc.vector.reciprocal(out=factor[:], in_=factor[:])
+    return factor
+
+
+def tile_retentionmechanism_pc_t_kernel(
+    tc, ao, w_swiglu, w_out, out_w_words, out_w_scales, tao, out_0, out_1
+):
+    nc = tc.nc
+    v_dram = w_swiglu.rearrange("(t p h) q -> p t h q", p=P, h=HALVES)
+    out1_dram = out_0.rearrange("(t p h) q -> p t h q", p=P, h=HALVES)
+    out2_dram = out_1.rearrange("(c p) n -> p c n", p=P)
+
+    with ExitStack() as ctx:
+        keep = ctx.enter_context(tc.tile_pool(name="keep", bufs=1))
+        stage = ctx.enter_context(tc.tile_pool(name="stage", bufs=3))
+        psum_first = ctx.enter_context(tc.psum_pool(name="psum_first", bufs=4))
+        psum_second = ctx.enter_context(tc.psum_pool(name="psum_second", bufs=4))
+
+        ao_sb = keep.tile([P, PACK, E], BF16)
+        v_sb = keep.tile([P, PACK, HALVES, Q], BF16)
+        wo_sb = keep.tile([P, PACK, E], BF16)
+        tao_sb = keep.tile([P, 2], BF16)
+        w_codes = keep.tile([P, E], U32, align_bytes=64)
+        w_scales = keep.tile([P, E], U8, align_bytes=64)
+        a_codes = keep.tile([P, E], U32, align_bytes=64)
+        a_scales = keep.tile([P, E], U8, align_bytes=64)
+        v_codes = keep.tile([P, V_BLOCKS, BLOCK], U32, align_bytes=64)
+        v_scales = keep.tile([P, V_BLOCKS, BLOCK], U8, align_bytes=64)
+        wo_codes = keep.tile([P, E], U32, align_bytes=64)
+        wo_scales = keep.tile([P, E], U8, align_bytes=64)
+        z1 = keep.tile([P, PACK, HALVES, Q], F32)
+        z2 = keep.tile([P, PACK, E], F32)
+        stats_1 = keep.tile([P, 2, PARTS], F32)
+        stats_2 = keep.tile([P, 2, PARTS], F32)
+
+        nc.vector.memset(w_scales[:].bitcast(I32), 0)
+        nc.vector.memset(stats_1[:], 0.0)
+        nc.vector.memset(stats_2[:], 0.0)
+        one = keep.tile([P, 1], F32)
+        nc.vector.memset(one[:], 1.0)
+        nc.scalar.activation(out=one[:], in_=one[:], func=ACT.Sqrt)
+        ident = keep.tile([P, P], BF16)
+        make_identity(nc, ident[:])
+        mean_of_1 = keep.tile([P, P], F32)
+        nc.gpsimd.memset(mean_of_1[:], 1.0 / COUNT_1)
+        mean_of_2 = keep.tile([P, P], F32)
+        nc.gpsimd.memset(mean_of_2[:], 1.0 / COUNT_2)
+
+        def load_v_block(b):
+            h, q0 = b // BLOCKS_PER_HALF, (b % BLOCKS_PER_HALF) * BLOCK
+            nc.sync.dma_start(out=v_sb[:, :, h, q0 : q0 + BLOCK], in_=v_dram[:, :, h, q0 : q0 + BLOCK])
+
+        nc.sync.dma_start(out=ao_sb[:], in_=ao.rearrange("(t p) e -> p t e", p=P))
+        load_v_block(0)
+        nc.sync.dma_start(out=wo_sb[:], in_=w_out.rearrange("(c p) d -> p c d", p=P))
+        load_v_block(1)
+        nc.sync.dma_start(
+            out=w_codes[:].bitcast(I32),
+            in_=out_w_words.rearrange("g p n t -> (g p) (n t)").bitcast(I32),
+        )
+        scale_rows = out_w_scales.rearrange("g s n -> (g s) n").bitcast(I32)
+        for r in range(PACK):
+            nc.sync.dma_start(out=w_scales[r:P:32, :].bitcast(I32), in_=scale_rows[r : 4 * PACK : PACK, :])
+        for b in range(2, V_BLOCKS):
+            load_v_block(b)
+        nc.scalar.dma_start(out=tao_sb[:], in_=tao.rearrange("a b -> (a b)").partition_broadcast(P))
+
+        sum_sq = keep.tile([P, PACK], F32)
+        for t in range(PACK):
+            squares = stage.tile([P, BLOCK], BF16)
+            nc.scalar.activation(
+                out=squares[:], in_=ao_sb[:, t, :], func=ACT.Square, accum_out=sum_sq[:, t : t + 1]
+            )
+        rms = keep.tile([P, PACK], F32)
+        nc.vector.tensor_scalar(
+            out=rms[:], in0=sum_sq[:], scalar1=1.0 / E, scalar2=EPS_RMS, op0=ALU.mult, op1=ALU.add
+        )
+        nc.scalar.activation(out=rms[:], in_=rms[:], func=ACT.Sqrt)
+        inv_rms = keep.tile([P, PACK], F32)
+        nc.vector.reciprocal(out=inv_rms[:], in_=rms[:])
+        a_grouped = keep.tile([P, E, PACK], BF16, align_bytes=64)
+        for u in range(PACK):
+            nc.vector.tensor_tensor(
+                out=a_grouped[:, u * P : (u + 1) * P, :],
+                in0=ao_sb[:, :, u:E:PACK].rearrange("p t c -> p c t"),
+                in1=inv_rms[:].unsqueeze(1).to_broadcast([P, P, PACK]),
+                op=ALU.mult,
+            )
+        nc.vector.quantize_mx(
+            out=a_codes[:].bitcast(FP8X4),
+            scales=a_scales[:],
+            in_=a_grouped[:].rearrange("p c t -> p (c t)"),
+        )
+
+        wo_grouped = keep.tile([P, E, PACK], BF16, align_bytes=64)
+        for c in range(PACK):
+            flipped = psum_first.tile([P, PACK, P], BF16, tag="bank")
+            for t in range(PACK):
+                nc.tensor.transpose(flipped[:, t, :], wo_sb[:, c, t * P : (t + 1) * P], ident[:])
+            nc.scalar.copy(
+                out=wo_grouped[:, c * P : (c + 1) * P, :], in_=flipped[:].rearrange("p t i -> p i t")
+            )
+        nc.vector.quantize_mx(
+            out=wo_codes[:].bitcast(FP8X4),
+            scales=wo_scales[:],
+            in_=wo_grouped[:].rearrange("p i t -> p (i t)"),
+        )
+
+        gate = keep.tile([P, 2], F32)
+        inv_gate = keep.tile([P, 2], F32)
+        nc.vector.tensor_scalar(out=gate[:], in0=tao_sb[:], scalar1=-1.0, scalar2=None, op0=ALU.mult)
+        nc.vector.tensor_tensor(out=gate[:], in0=gate[:], in1=tao_sb[:], op=ALU.max)
+        nc.vector.tensor_scalar(
+            out=gate[:], in0=gate[:], scalar1=1e-08, scalar2=1.0, op0=ALU.max, op1=ALU.min
+        )
+        nc.vector.tensor_scalar(out=gate[:], in0=gate[:], scalar1=TARGET_STD, scalar2=None, op0=ALU.mult)
+        nc.vector.reciprocal(out=inv_gate[:], in_=gate[:])
+
+        def quantise_v_block(b):
+            h, q0 = b // BLOCKS_PER_HALF, (b % BLOCKS_PER_HALF) * BLOCK
+            v_grouped = stage.tile([P, BLOCK, PACK], BF16, align_bytes=64)
+            dst = v_grouped[:].rearrange("p (c i) t -> p c t i", i=4)
+            src = v_sb[:, :, h, q0 : q0 + BLOCK].rearrange("p t (c i) -> p c t i", i=4)
+            if b < BLOCKS_GROUPED_BY_SCALAR:
+                nc.scalar.copy(out=dst, in_=src)
+            else:
+                nc.vector.tensor_copy(out=dst, in_=src)
+            nc.vector.quantize_mx(
+                out=v_codes[:, b, :].bitcast(FP8X4),
+                scales=v_scales[:, b, :],
+                in_=v_grouped[:].rearrange("p j t -> p (j t)"),
+            )
+
+        for b in range(AHEAD):
+            quantise_v_block(b)
+        for b in range(V_BLOCKS):
+            if b + AHEAD < V_BLOCKS:
+                quantise_v_block(b + AHEAD)
+            h, q0 = b // BLOCKS_PER_HALF, (b % BLOCKS_PER_HALF) * BLOCK
+            h_codes, h_scales = first_stage(
+                nc, psum_first, stage, a_codes, a_scales, v_codes[:, b, :], v_scales[:, b, :]
+            )
+            for c in range(PACK):
+                n_slice = slice(c * P, (c + 1) * P)
+                product = psum_second.tile([P, BLOCK], F32)
+                nc.tensor.matmul_mx(
+                    out=product[:],
+                    lhsT=w_codes[:, n_slice].bitcast(FP8X4),
+                    lhsT_scale=w_scales[:, n_slice],
+                    rhs=h_codes[:].bitcast(FP8X4),
+                    rhs_scale=h_scales[:],
+                    start=True,
+                    stop=True,
+                )
+                add_weight_and_measure(
+                    nc,
+                    stage,
+                    z1[:, c, h, q0 : q0 + BLOCK],
+                    product[:],
+                    v_sb[:, c, h, q0 : q0 + BLOCK],
+                    stats_1,
+                    b * PACK + c,
+                )
+
+        h_codes, h_scales = first_stage(nc, psum_first, stage, a_codes, a_scales, wo_codes, wo_scales)
+
+        factor_1 = norm_factor(
+            nc, psum_second, keep, stats_1, mean_of_1, COUNT_1, inv_gate[:, 0:1], "first"
+        )
+
+        for c in range(PACK):
+            i_slice = slice(c * P, (c + 1) * P)
+            product = psum_second.tile([P, BLOCK], F32)
+            nc.tensor.matmul_mx(
+                out=product[:],
+                lhsT=h_codes[:, i_slice].bitcast(FP8X4),
+                lhsT_scale=h_scales[:, i_slice],
+                rhs=w_codes[:].bitcast(FP8X4),
+                rhs_scale=w_scales[:],
+                start=True,
+                stop=True,
+            )
+            add_weight_and_measure(nc, stage, z2[:, c, :], product[:], wo_sb[:, c, :], stats_2, c)
+        factor_2 = norm_factor(
+            nc, psum_second, keep, stats_2, mean_of_2, COUNT_2, inv_gate[:, 1:2], "second"
+        )
+
+        for c in range(PACK):
+            for h in range(HALVES):
+                nc.vector.tensor_scalar(
+                    out=z1[:, c, h, :], in0=z1[:, c, h, :], scalar1=factor_1[:], scalar2=None, op0=ALU.mult
+                )
+                nc.sync.dma_start(out=out1_dram[:, c, h, :], in_=z1[:, c, h, :])
+        nc.scalar.activation(out=z2[:], in_=z2[:], func=ACT.Copy, scale=factor_2[:])
+        nc.sync.dma_start(out=out2_dram, in_=z2[:])

@@ -26,92 +26,15 @@ PARTS = V_BLOCKS * PACK
 EPS_RMS = 1.1920929e-07
 EPS_STD = 1e-08
 TARGET_STD = 2048.0**-0.5
-BLOCKS_GROUPED_BY_SCALAR = 2
-AHEAD = 2
 
 FLOPS = 2 * 2 * E * E * (HALVES * Q + E)
-
-
-def first_stage(nc, psum_first, stage, a_codes, a_scales, x_codes, x_scales):
-    h_grouped = stage.tile([P, BLOCK, PACK], BF16, align_bytes=64)
-    for s in range(BLOCK // P):
-        cols = slice(s * P, (s + 1) * P)
-        bank = psum_first.tile([P, PACK, P], F32)
-        for t in range(PACK):
-            e_slice = slice(t * P, (t + 1) * P)
-            nc.tensor.matmul_mx(
-                out=bank[:, t, :],
-                lhsT=a_codes[:, e_slice].bitcast(FP8X4),
-                lhsT_scale=a_scales[:, e_slice],
-                rhs=x_codes[:, cols].bitcast(FP8X4),
-                rhs_scale=x_scales[:, cols],
-                start=True,
-                stop=True,
-            )
-        nc.scalar.activation(
-            out=h_grouped[:, cols, :], in_=bank[:].rearrange("p t j -> p j t"), func=ACT.Silu
-        )
-    h_codes = stage.tile([P, BLOCK], U32, align_bytes=64)
-    h_scales = stage.tile([P, BLOCK], U8, align_bytes=64)
-    nc.vector.quantize_mx(
-        out=h_codes[:].bitcast(FP8X4),
-        scales=h_scales[:],
-        in_=h_grouped[:].rearrange("p j t -> p (j t)"),
-    )
-    return h_codes, h_scales
-
-
-def add_weight_and_measure(nc, stage, z, product, weight, stats, part):
-    nc.vector.scalar_tensor_tensor(
-        out=z,
-        in0=product,
-        scalar=1.0,
-        in1=weight,
-        op0=ALU.mult,
-        op1=ALU.add,
-        accum_out=stats[:, 0, part : part + 1],
-    )
-    squares = stage.tile([P, BLOCK], BF16)
-    nc.scalar.activation(
-        out=squares[:], in_=z, func=ACT.Square, accum_out=stats[:, 1, part : part + 1]
-    )
-
-
-def norm_factor(nc, psum_second, keep, stats, mean_of, count, inv_gate, name):
-    spread = psum_second.tile([P, 2 * PARTS], F32, tag="product")
-    nc.tensor.matmul(
-        out=spread[:], lhsT=mean_of[:], rhs=stats[:].rearrange("p s k -> p (s k)"), start=True, stop=True
-    )
-    moments = keep.tile([P, 2], F32, name=name + "_moments")
-    nc.vector.tensor_reduce(
-        out=moments[:],
-        in_=spread[:].rearrange("p (s k) -> p s k", s=2),
-        axis=mybir.AxisListType.X,
-        op=ALU.add,
-    )
-    minus_var = keep.tile([P, 1], F32, name=name + "_minus_var")
-    nc.vector.scalar_tensor_tensor(
-        out=minus_var[:],
-        in0=moments[:, 0:1],
-        scalar=moments[:, 0:1],
-        in1=moments[:, 1:2],
-        op0=ALU.mult,
-        op1=ALU.subtract,
-    )
-    std = keep.tile([P, 1], F32, name=name + "_std")
-    nc.scalar.activation(out=std[:], in_=minus_var[:], func=ACT.Sqrt, scale=-count / (count - 1.0))
-    factor = keep.tile([P, 1], F32, name=name + "_factor")
-    nc.vector.tensor_scalar(
-        out=factor[:], in0=std[:], scalar1=EPS_STD, scalar2=inv_gate, op0=ALU.add, op1=ALU.mult
-    )
-    nc.vector.reciprocal(out=factor[:], in_=factor[:])
-    return factor
 
 
 def tile_retentionmechanism_pc_t_kernel(
     tc, ao, w_swiglu, w_out, out_w_words, out_w_scales, tao, out_0, out_1
 ):
     nc = tc.nc
+    ao_dram = ao.rearrange("(t p) e -> p t e", p=P)
     v_dram = w_swiglu.rearrange("(t p h) q -> p t h q", p=P, h=HALVES)
     out1_dram = out_0.rearrange("(t p h) q -> p t h q", p=P, h=HALVES)
     out2_dram = out_1.rearrange("(c p) n -> p c n", p=P)
@@ -139,64 +62,259 @@ def tile_retentionmechanism_pc_t_kernel(
         stats_1 = keep.tile([P, 2, PARTS], F32)
         stats_2 = keep.tile([P, 2, PARTS], F32)
 
-        nc.vector.memset(w_scales[:].bitcast(I32), 0)
-        nc.vector.memset(stats_1[:], 0.0)
-        nc.vector.memset(stats_2[:], 0.0)
-        one = keep.tile([P, 1], F32)
-        nc.vector.memset(one[:], 1.0)
-        nc.scalar.activation(out=one[:], in_=one[:], func=ACT.Sqrt)
-        ident = keep.tile([P, P], BF16)
-        make_identity(nc, ident[:])
-        mean_of_1 = keep.tile([P, P], F32)
-        nc.gpsimd.memset(mean_of_1[:], 1.0 / COUNT_1)
-        mean_of_2 = keep.tile([P, P], F32)
-        nc.gpsimd.memset(mean_of_2[:], 1.0 / COUNT_2)
+        def columns_of(b):
+            q0 = (b % BLOCKS_PER_HALF) * BLOCK
+            return b // BLOCKS_PER_HALF, slice(q0, q0 + BLOCK)
 
         def load_v_block(b):
-            h, q0 = b // BLOCKS_PER_HALF, (b % BLOCKS_PER_HALF) * BLOCK
-            nc.sync.dma_start(out=v_sb[:, :, h, q0 : q0 + BLOCK], in_=v_dram[:, :, h, q0 : q0 + BLOCK])
+            half, cols = columns_of(b)
+            nc.sync.dma_start(out=v_sb[:, :, half, cols], in_=v_dram[:, :, half, cols])
 
-        nc.sync.dma_start(out=ao_sb[:], in_=ao.rearrange("(t p) e -> p t e", p=P))
-        load_v_block(0)
-        nc.sync.dma_start(out=wo_sb[:], in_=w_out.rearrange("(c p) d -> p c d", p=P))
-        load_v_block(1)
-        nc.sync.dma_start(
-            out=w_codes[:].bitcast(I32),
-            in_=out_w_words.rearrange("g p n t -> (g p) (n t)").bitcast(I32),
-        )
-        scale_rows = out_w_scales.rearrange("g s n -> (g s) n").bitcast(I32)
-        for r in range(PACK):
-            nc.sync.dma_start(out=w_scales[r:P:32, :].bitcast(I32), in_=scale_rows[r : 4 * PACK : PACK, :])
-        for b in range(2, V_BLOCKS):
-            load_v_block(b)
-        nc.scalar.dma_start(out=tao_sb[:], in_=tao.rearrange("a b -> (a b)").partition_broadcast(P))
+        def group_v_block(b, copy):
+            half, cols = columns_of(b)
+            v_grouped = stage.tile([P, BLOCK, PACK], BF16, align_bytes=64)
+            copy(
+                out=v_grouped[:].rearrange("p (c i) t -> p c t i", i=4),
+                in_=v_sb[:, :, half, cols].rearrange("p t (c i) -> p c t i", i=4),
+            )
+            return v_grouped
 
-        sum_sq = keep.tile([P, PACK], F32)
-        for t in range(PACK):
+        def quantise_v_block(b, v_grouped):
+            nc.vector.quantize_mx(
+                out=v_codes[:, b, :].bitcast(FP8X4),
+                scales=v_scales[:, b, :],
+                in_=v_grouped[:].rearrange("p j t -> p (j t)"),
+            )
+
+        def multiply_and_silu(x_codes, x_scales):
+            h_grouped = stage.tile([P, BLOCK, PACK], BF16, align_bytes=64)
+            for s in range(BLOCK // P):
+                cols = slice(s * P, (s + 1) * P)
+                bank = psum_first.tile([P, PACK, P], F32)
+                for t in range(PACK):
+                    e_slice = slice(t * P, (t + 1) * P)
+                    nc.tensor.matmul_mx(
+                        out=bank[:, t, :],
+                        lhsT=a_codes[:, e_slice].bitcast(FP8X4),
+                        lhsT_scale=a_scales[:, e_slice],
+                        rhs=x_codes[:, cols].bitcast(FP8X4),
+                        rhs_scale=x_scales[:, cols],
+                        start=True,
+                        stop=True,
+                    )
+                nc.scalar.activation(
+                    out=h_grouped[:, cols, :], in_=bank[:].rearrange("p t j -> p j t"), func=ACT.Silu
+                )
+            return h_grouped
+
+        def quantise_h(h_grouped):
+            h_codes = stage.tile([P, BLOCK], U32, align_bytes=64)
+            h_scales = stage.tile([P, BLOCK], U8, align_bytes=64)
+            nc.vector.quantize_mx(
+                out=h_codes[:].bitcast(FP8X4),
+                scales=h_scales[:],
+                in_=h_grouped[:].rearrange("p j t -> p (j t)"),
+            )
+            return h_codes, h_scales
+
+        def add_weight_and_measure(z, product, weight, stats, part):
+            nc.vector.scalar_tensor_tensor(
+                out=z,
+                in0=product,
+                scalar=1.0,
+                in1=weight,
+                op0=ALU.mult,
+                op1=ALU.add,
+                accum_out=stats[:, 0, part : part + 1],
+            )
             squares = stage.tile([P, BLOCK], BF16)
             nc.scalar.activation(
-                out=squares[:], in_=ao_sb[:, t, :], func=ACT.Square, accum_out=sum_sq[:, t : t + 1]
+                out=squares[:], in_=z, func=ACT.Square, accum_out=stats[:, 1, part : part + 1]
             )
-        rms = keep.tile([P, PACK], F32)
-        nc.vector.tensor_scalar(
-            out=rms[:], in0=sum_sq[:], scalar1=1.0 / E, scalar2=EPS_RMS, op0=ALU.mult, op1=ALU.add
-        )
-        nc.scalar.activation(out=rms[:], in_=rms[:], func=ACT.Sqrt)
-        inv_rms = keep.tile([P, PACK], F32)
-        nc.vector.reciprocal(out=inv_rms[:], in_=rms[:])
-        a_grouped = keep.tile([P, E, PACK], BF16, align_bytes=64)
-        for u in range(PACK):
-            nc.vector.tensor_tensor(
-                out=a_grouped[:, u * P : (u + 1) * P, :],
-                in0=ao_sb[:, :, u:E:PACK].rearrange("p t c -> p c t"),
-                in1=inv_rms[:].unsqueeze(1).to_broadcast([P, P, PACK]),
-                op=ALU.mult,
+
+        def update_first_weight(b, h_codes, h_scales):
+            half, cols = columns_of(b)
+            for c in range(PACK):
+                n_slice = slice(c * P, (c + 1) * P)
+                product = psum_second.tile([P, BLOCK], F32)
+                nc.tensor.matmul_mx(
+                    out=product[:],
+                    lhsT=w_codes[:, n_slice].bitcast(FP8X4),
+                    lhsT_scale=w_scales[:, n_slice],
+                    rhs=h_codes[:].bitcast(FP8X4),
+                    rhs_scale=h_scales[:],
+                    start=True,
+                    stop=True,
+                )
+                add_weight_and_measure(
+                    z1[:, c, half, cols], product[:], v_sb[:, c, half, cols], stats_1, b * PACK + c
+                )
+
+        def update_second_weight(h_codes, h_scales):
+            for c in range(PACK):
+                i_slice = slice(c * P, (c + 1) * P)
+                product = psum_second.tile([P, BLOCK], F32)
+                nc.tensor.matmul_mx(
+                    out=product[:],
+                    lhsT=h_codes[:, i_slice].bitcast(FP8X4),
+                    lhsT_scale=h_scales[:, i_slice],
+                    rhs=w_codes[:].bitcast(FP8X4),
+                    rhs_scale=w_scales[:],
+                    start=True,
+                    stop=True,
+                )
+                add_weight_and_measure(z2[:, c, :], product[:], wo_sb[:, c, :], stats_2, c)
+
+        def norm_factor(stats, mean_of, slope, offset, name):
+            spread = psum_second.tile([P, 2 * PARTS], F32, tag="product")
+            nc.tensor.matmul(
+                out=spread[:],
+                lhsT=mean_of[:],
+                rhs=stats[:].rearrange("p s k -> p (s k)"),
+                start=True,
+                stop=True,
             )
-        nc.vector.quantize_mx(
-            out=a_codes[:].bitcast(FP8X4),
-            scales=a_scales[:],
-            in_=a_grouped[:].rearrange("p c t -> p (c t)"),
-        )
+            moments = keep.tile([P, 2], F32, name=name + "_moments")
+            nc.vector.tensor_reduce(
+                out=moments[:],
+                in_=spread[:].rearrange("p (s k) -> p s k", s=2),
+                axis=mybir.AxisListType.X,
+                op=ALU.add,
+            )
+            spread_of_z = keep.tile([P, 1], F32, name=name + "_spread")
+            nc.vector.scalar_tensor_tensor(
+                out=spread_of_z[:],
+                in0=moments[:, 0:1],
+                scalar=moments[:, 0:1],
+                in1=moments[:, 1:2],
+                op0=ALU.mult,
+                op1=ALU.subtract,
+                reverse1=True,
+            )
+            nc.gpsimd.tensor_tensor(out=spread_of_z[:], in0=spread_of_z[:], in1=half_power[:], op=ALU.pow)
+            factor = keep.tile([P, 1], F32, name=name + "_factor")
+            nc.vector.tensor_scalar(
+                out=factor[:], in0=spread_of_z[:], scalar1=slope, scalar2=offset, op0=ALU.mult, op1=ALU.add
+            )
+            nc.vector.reciprocal(out=factor[:], in_=factor[:])
+            return factor
+
+        with tc.manual_schedule():
+            nc.vector.memset(w_scales[:].bitcast(I32), 0)
+            nc.vector.memset(stats_2[:], 0.0)
+            one = keep.tile([P, 1], F32)
+            nc.vector.memset(one[:], 1.0)
+            nc.scalar.activation(out=one[:], in_=one[:], func=ACT.Sqrt)
+            half_power = keep.tile([P, 1], F32)
+            nc.gpsimd.memset(half_power[:], 0.5)
+            mean_of_1 = keep.tile([P, P], F32)
+            nc.gpsimd.memset(mean_of_1[:], 1.0 / COUNT_1)
+            mean_of_2 = keep.tile([P, P], F32)
+            nc.gpsimd.memset(mean_of_2[:], 1.0 / COUNT_2)
+            ident = keep.tile([P, P], BF16)
+            make_identity(nc, ident[:])
+
+            nc.sync.dma_start(out=tao_sb[:], in_=tao.rearrange("a b -> (a b)").partition_broadcast(P))
+            for t in range(PACK):
+                nc.sync.dma_start(out=ao_sb[:, t, :], in_=ao_dram[:, t, :])
+            load_v_block(0)
+            load_v_block(1)
+            nc.sync.dma_start(
+                out=w_codes[:].bitcast(I32),
+                in_=out_w_words.rearrange("g p n t -> (g p) (n t)").bitcast(I32),
+            )
+            scale_rows = out_w_scales.rearrange("g s n -> (g s) n").bitcast(I32)
+            for r in range(PACK):
+                nc.sync.dma_start(
+                    out=w_scales[r:P:32, :].bitcast(I32), in_=scale_rows[r : 4 * PACK : PACK, :]
+                )
+            for b in range(2, V_BLOCKS):
+                load_v_block(b)
+            nc.sync.dma_start(out=wo_sb[:], in_=w_out.rearrange("(c p) d -> p c d", p=P))
+
+            gate = keep.tile([P, 2], F32)
+            inv_gate = keep.tile([P, 2], F32)
+            slope = keep.tile([P, 2], F32)
+            offset = keep.tile([P, 2], F32)
+            nc.vector.tensor_scalar(out=gate[:], in0=tao_sb[:], scalar1=-1.0, scalar2=None, op0=ALU.mult)
+            nc.vector.tensor_tensor(out=gate[:], in0=gate[:], in1=tao_sb[:], op=ALU.max)
+            nc.vector.tensor_scalar(
+                out=gate[:], in0=gate[:], scalar1=1e-08, scalar2=1.0, op0=ALU.max, op1=ALU.min
+            )
+            nc.vector.tensor_scalar(
+                out=gate[:], in0=gate[:], scalar1=TARGET_STD, scalar2=None, op0=ALU.mult
+            )
+            nc.vector.reciprocal(out=inv_gate[:], in_=gate[:])
+            for w, count in enumerate((COUNT_1, COUNT_2)):
+                nc.vector.tensor_scalar(
+                    out=slope[:, w : w + 1],
+                    in0=inv_gate[:, w : w + 1],
+                    scalar1=(count / (count - 1.0)) ** 0.5,
+                    scalar2=None,
+                    op0=ALU.mult,
+                )
+            nc.vector.tensor_scalar(
+                out=offset[:], in0=inv_gate[:], scalar1=EPS_STD, scalar2=None, op0=ALU.mult
+            )
+
+            sum_sq_s = keep.tile([P, 2], F32)
+            sum_sq_v = keep.tile([P, 2], F32)
+            for t in range(2):
+                squares = stage.tile([P, BLOCK], BF16)
+                nc.scalar.activation(
+                    out=squares[:], in_=ao_sb[:, t, :], func=ACT.Square, accum_out=sum_sq_s[:, t : t + 1]
+                )
+                squares_v = stage.tile([P, BLOCK], F32)
+                nc.vector.scalar_tensor_tensor(
+                    out=squares_v[:],
+                    in0=ao_sb[:, 2 + t, :],
+                    scalar=1.0,
+                    in1=ao_sb[:, 2 + t, :],
+                    op0=ALU.mult,
+                    op1=ALU.mult,
+                    accum_out=sum_sq_v[:, t : t + 1],
+                )
+            rms = keep.tile([P, PACK], F32)
+            nc.vector.tensor_scalar(
+                out=rms[:, 0:2], in0=sum_sq_s[:], scalar1=1.0 / E, scalar2=EPS_RMS, op0=ALU.mult, op1=ALU.add
+            )
+            nc.vector.tensor_scalar(
+                out=rms[:, 2:4], in0=sum_sq_v[:], scalar1=1.0 / E, scalar2=EPS_RMS, op0=ALU.mult, op1=ALU.add
+            )
+            nc.scalar.activation(out=rms[:], in_=rms[:], func=ACT.Sqrt)
+            inv_rms = keep.tile([P, PACK], F32)
+            nc.vector.reciprocal(out=inv_rms[:], in_=rms[:])
+            grouped = {0: group_v_block(0, nc.scalar.copy)}
+            a_grouped = keep.tile([P, E, PACK], BF16, align_bytes=64)
+            for u in range(PACK):
+                nc.vector.tensor_tensor(
+                    out=a_grouped[:, u * P : (u + 1) * P, :],
+                    in0=ao_sb[:, :, u:E:PACK].rearrange("p t c -> p c t"),
+                    in1=inv_rms[:].unsqueeze(1).to_broadcast([P, P, PACK]),
+                    op=ALU.mult,
+                )
+            quantise_v_block(0, grouped[0])
+            nc.vector.quantize_mx(
+                out=a_codes[:].bitcast(FP8X4),
+                scales=a_scales[:],
+                in_=a_grouped[:].rearrange("p c t -> p (c t)"),
+            )
+
+            silu = {0: multiply_and_silu(v_codes[:, 0, :], v_scales[:, 0, :])}
+            grouped[1] = group_v_block(1, nc.vector.tensor_copy)
+            grouped[2] = group_v_block(2, nc.vector.tensor_copy)
+            quantise_v_block(1, grouped[1])
+            for b in range(V_BLOCKS):
+                if b + 1 < V_BLOCKS:
+                    silu[b + 1] = multiply_and_silu(v_codes[:, b + 1, :], v_scales[:, b + 1, :])
+                h_codes, h_scales = quantise_h(silu[b])
+                if b + 2 < V_BLOCKS:
+                    quantise_v_block(b + 2, grouped[b + 2])
+                if b + 3 < V_BLOCKS:
+                    grouped[b + 3] = group_v_block(b + 3, nc.vector.tensor_copy)
+                update_first_weight(b, h_codes, h_scales)
+
+        factor_1 = norm_factor(stats_1, mean_of_1, slope[:, 0:1], offset[:, 0:1], "first")
 
         wo_grouped = keep.tile([P, E, PACK], BF16, align_bytes=64)
         for c in range(PACK):
@@ -211,91 +329,19 @@ def tile_retentionmechanism_pc_t_kernel(
             scales=wo_scales[:],
             in_=wo_grouped[:].rearrange("p i t -> p (i t)"),
         )
-
-        gate = keep.tile([P, 2], F32)
-        inv_gate = keep.tile([P, 2], F32)
-        nc.vector.tensor_scalar(out=gate[:], in0=tao_sb[:], scalar1=-1.0, scalar2=None, op0=ALU.mult)
-        nc.vector.tensor_tensor(out=gate[:], in0=gate[:], in1=tao_sb[:], op=ALU.max)
-        nc.vector.tensor_scalar(
-            out=gate[:], in0=gate[:], scalar1=1e-08, scalar2=1.0, op0=ALU.max, op1=ALU.min
-        )
-        nc.vector.tensor_scalar(out=gate[:], in0=gate[:], scalar1=TARGET_STD, scalar2=None, op0=ALU.mult)
-        nc.vector.reciprocal(out=inv_gate[:], in_=gate[:])
-
-        def quantise_v_block(b):
-            h, q0 = b // BLOCKS_PER_HALF, (b % BLOCKS_PER_HALF) * BLOCK
-            v_grouped = stage.tile([P, BLOCK, PACK], BF16, align_bytes=64)
-            dst = v_grouped[:].rearrange("p (c i) t -> p c t i", i=4)
-            src = v_sb[:, :, h, q0 : q0 + BLOCK].rearrange("p t (c i) -> p c t i", i=4)
-            if b < BLOCKS_GROUPED_BY_SCALAR:
-                nc.scalar.copy(out=dst, in_=src)
-            else:
-                nc.vector.tensor_copy(out=dst, in_=src)
-            nc.vector.quantize_mx(
-                out=v_codes[:, b, :].bitcast(FP8X4),
-                scales=v_scales[:, b, :],
-                in_=v_grouped[:].rearrange("p j t -> p (j t)"),
-            )
-
-        for b in range(AHEAD):
-            quantise_v_block(b)
-        for b in range(V_BLOCKS):
-            if b + AHEAD < V_BLOCKS:
-                quantise_v_block(b + AHEAD)
-            h, q0 = b // BLOCKS_PER_HALF, (b % BLOCKS_PER_HALF) * BLOCK
-            h_codes, h_scales = first_stage(
-                nc, psum_first, stage, a_codes, a_scales, v_codes[:, b, :], v_scales[:, b, :]
-            )
-            for c in range(PACK):
-                n_slice = slice(c * P, (c + 1) * P)
-                product = psum_second.tile([P, BLOCK], F32)
-                nc.tensor.matmul_mx(
-                    out=product[:],
-                    lhsT=w_codes[:, n_slice].bitcast(FP8X4),
-                    lhsT_scale=w_scales[:, n_slice],
-                    rhs=h_codes[:].bitcast(FP8X4),
-                    rhs_scale=h_scales[:],
-                    start=True,
-                    stop=True,
-                )
-                add_weight_and_measure(
-                    nc,
-                    stage,
-                    z1[:, c, h, q0 : q0 + BLOCK],
-                    product[:],
-                    v_sb[:, c, h, q0 : q0 + BLOCK],
-                    stats_1,
-                    b * PACK + c,
-                )
-
-        h_codes, h_scales = first_stage(nc, psum_first, stage, a_codes, a_scales, wo_codes, wo_scales)
-
-        factor_1 = norm_factor(
-            nc, psum_second, keep, stats_1, mean_of_1, COUNT_1, inv_gate[:, 0:1], "first"
-        )
+        h_codes, h_scales = quantise_h(multiply_and_silu(wo_codes, wo_scales))
+        update_second_weight(h_codes, h_scales)
+        factor_2 = norm_factor(stats_2, mean_of_2, slope[:, 1:2], offset[:, 1:2], "second")
 
         for c in range(PACK):
-            i_slice = slice(c * P, (c + 1) * P)
-            product = psum_second.tile([P, BLOCK], F32)
-            nc.tensor.matmul_mx(
-                out=product[:],
-                lhsT=h_codes[:, i_slice].bitcast(FP8X4),
-                lhsT_scale=h_scales[:, i_slice],
-                rhs=w_codes[:].bitcast(FP8X4),
-                rhs_scale=w_scales[:],
-                start=True,
-                stop=True,
-            )
-            add_weight_and_measure(nc, stage, z2[:, c, :], product[:], wo_sb[:, c, :], stats_2, c)
-        factor_2 = norm_factor(
-            nc, psum_second, keep, stats_2, mean_of_2, COUNT_2, inv_gate[:, 1:2], "second"
-        )
-
-        for c in range(PACK):
-            for h in range(HALVES):
+            for half in range(HALVES):
                 nc.vector.tensor_scalar(
-                    out=z1[:, c, h, :], in0=z1[:, c, h, :], scalar1=factor_1[:], scalar2=None, op0=ALU.mult
+                    out=z1[:, c, half, :],
+                    in0=z1[:, c, half, :],
+                    scalar1=factor_1[:],
+                    scalar2=None,
+                    op0=ALU.mult,
                 )
-                nc.sync.dma_start(out=out1_dram[:, c, h, :], in_=z1[:, c, h, :])
+                nc.sync.dma_start(out=out1_dram[:, c, half, :], in_=z1[:, c, half, :])
         nc.scalar.activation(out=z2[:], in_=z2[:], func=ACT.Copy, scale=factor_2[:])
         nc.sync.dma_start(out=out2_dram, in_=z2[:])

@@ -42,11 +42,13 @@ def tile_retentionmechanism_pc_t_kernel(
     with ExitStack() as ctx:
         keep = ctx.enter_context(tc.tile_pool(name="keep", bufs=1))
         stage = ctx.enter_context(tc.tile_pool(name="stage", bufs=3))
+        unread = ctx.enter_context(tc.tile_pool(name="unread", bufs=2))
+        outbound = ctx.enter_context(tc.tile_pool(name="outbound", bufs=4))
         psum_first = ctx.enter_context(tc.psum_pool(name="psum_first", bufs=4))
         psum_second = ctx.enter_context(tc.psum_pool(name="psum_second", bufs=4))
 
         ao_sb = keep.tile([P, PACK, E], BF16)
-        v_sb = keep.tile([P, PACK, HALVES, Q], BF16)
+        v_sb = keep.tile([P, V_BLOCKS, PACK, BLOCK], BF16)
         wo_sb = keep.tile([P, PACK, E], BF16)
         tao_sb = keep.tile([P, 2], BF16)
         w_codes = keep.tile([P, E], U32, align_bytes=64)
@@ -57,7 +59,7 @@ def tile_retentionmechanism_pc_t_kernel(
         v_scales = keep.tile([P, V_BLOCKS, BLOCK], U8, align_bytes=64)
         wo_codes = keep.tile([P, E], U32, align_bytes=64)
         wo_scales = keep.tile([P, E], U8, align_bytes=64)
-        z1 = keep.tile([P, PACK, HALVES, Q], F32)
+        z1 = keep.tile([P, V_BLOCKS, PACK, BLOCK], F32)
         z2 = keep.tile([P, PACK, E], F32)
         stats_1 = keep.tile([P, 2, PARTS], F32)
         stats_2 = keep.tile([P, 2, PARTS], F32)
@@ -68,15 +70,27 @@ def tile_retentionmechanism_pc_t_kernel(
 
         def load_v_block(b):
             half, cols = columns_of(b)
-            nc.sync.dma_start(out=v_sb[:, :, half, cols], in_=v_dram[:, :, half, cols])
+            nc.sync.dma_start(out=v_sb[:, b, :, :], in_=v_dram[:, :, half, cols])
 
-        def group_v_block(b, copy):
-            half, cols = columns_of(b)
+        def group_v_block(b):
             v_grouped = stage.tile([P, BLOCK, PACK], BF16, align_bytes=64)
-            copy(
-                out=v_grouped[:].rearrange("p (c i) t -> p c t i", i=4),
-                in_=v_sb[:, :, half, cols].rearrange("p t (c i) -> p c t i", i=4),
-            )
+            rows = v_sb[:, b, :, :]
+            if b == 0:
+                nc.scalar.copy(
+                    out=v_grouped[:].rearrange("p (c i) t -> p c t i", i=4),
+                    in_=rows.rearrange("p t (c i) -> p c t i", i=4),
+                )
+            else:
+                for s in range(BLOCK // P):
+                    cols_s = slice(s * P, (s + 1) * P)
+                    nc.gpsimd.tensor_scalar(
+                        out=v_grouped[:, cols_s, :],
+                        in0=rows[:, :, cols_s].rearrange("p t j -> p j t"),
+                        scalar1=1.0,
+                        scalar2=0.0,
+                        op0=ALU.mult,
+                        op1=ALU.add,
+                    )
             return v_grouped
 
         def quantise_v_block(b, v_grouped):
@@ -117,7 +131,7 @@ def tile_retentionmechanism_pc_t_kernel(
             )
             return h_codes, h_scales
 
-        def add_weight_and_measure(z, product, weight, stats, part):
+        def add_weight(z, product, weight, stats, part):
             nc.vector.scalar_tensor_tensor(
                 out=z,
                 in0=product,
@@ -127,13 +141,15 @@ def tile_retentionmechanism_pc_t_kernel(
                 op1=ALU.add,
                 accum_out=stats[:, 0, part : part + 1],
             )
-            squares = stage.tile([P, BLOCK], BF16)
+
+        def sum_squares(z, slices, stats, part):
+            squares = unread.tile([P, PACK, BLOCK], BF16)
             nc.scalar.activation(
-                out=squares[:], in_=z, func=ACT.Square, accum_out=stats[:, 1, part : part + 1]
+                out=squares[:, 0:slices, :], in_=z, func=ACT.Square, accum_out=stats[:, 1, part : part + 1]
             )
 
         def update_first_weight(b, h_codes, h_scales):
-            half, cols = columns_of(b)
+            last = b == V_BLOCKS - 1
             for c in range(PACK):
                 n_slice = slice(c * P, (c + 1) * P)
                 product = psum_second.tile([P, BLOCK], F32)
@@ -146,9 +162,11 @@ def tile_retentionmechanism_pc_t_kernel(
                     start=True,
                     stop=True,
                 )
-                add_weight_and_measure(
-                    z1[:, c, half, cols], product[:], v_sb[:, c, half, cols], stats_1, b * PACK + c
-                )
+                add_weight(z1[:, b, c, :], product[:], v_sb[:, b, c, :], stats_1, b * PACK + c)
+                if last:
+                    sum_squares(z1[:, b, c : c + 1, :], 1, stats_1, b * PACK + c)
+            if not last:
+                sum_squares(z1[:, b, :, :], PACK, stats_1, b * PACK)
 
         def update_second_weight(h_codes, h_scales):
             for c in range(PACK):
@@ -163,7 +181,8 @@ def tile_retentionmechanism_pc_t_kernel(
                     start=True,
                     stop=True,
                 )
-                add_weight_and_measure(z2[:, c, :], product[:], wo_sb[:, c, :], stats_2, c)
+                add_weight(z2[:, c, :], product[:], wo_sb[:, c, :], stats_2, c)
+                sum_squares(z2[:, c : c + 1, :], 1, stats_2, c)
 
         def norm_factor(stats, mean_of, slope, offset, name):
             spread = psum_second.tile([P, 2 * PARTS], F32, tag="product")
@@ -201,6 +220,7 @@ def tile_retentionmechanism_pc_t_kernel(
 
         with tc.manual_schedule():
             nc.vector.memset(w_scales[:].bitcast(I32), 0)
+            nc.vector.memset(stats_1[:], 0.0)
             nc.vector.memset(stats_2[:], 0.0)
             one = keep.tile([P, 1], F32)
             nc.vector.memset(one[:], 1.0)
@@ -214,7 +234,6 @@ def tile_retentionmechanism_pc_t_kernel(
             ident = keep.tile([P, P], BF16)
             make_identity(nc, ident[:])
 
-            nc.sync.dma_start(out=tao_sb[:], in_=tao.rearrange("a b -> (a b)").partition_broadcast(P))
             for t in range(PACK):
                 nc.sync.dma_start(out=ao_sb[:, t, :], in_=ao_dram[:, t, :])
             load_v_block(0)
@@ -231,6 +250,62 @@ def tile_retentionmechanism_pc_t_kernel(
             for b in range(2, V_BLOCKS):
                 load_v_block(b)
             nc.sync.dma_start(out=wo_sb[:], in_=w_out.rearrange("(c p) d -> p c d", p=P))
+            nc.sync.dma_start(out=tao_sb[:], in_=tao.rearrange("a b -> (a b)").partition_broadcast(P))
+
+            sum_sq_s = keep.tile([P, 2], F32)
+            sum_sq_v = keep.tile([P, 2], F32)
+            for t in range(2):
+                squares_s = unread.tile([P, BLOCK], BF16)
+                nc.scalar.activation(
+                    out=squares_s[:], in_=ao_sb[:, t, :], func=ACT.Square, accum_out=sum_sq_s[:, t : t + 1]
+                )
+                squares_v = unread.tile([P, BLOCK], F32)
+                nc.vector.scalar_tensor_tensor(
+                    out=squares_v[:],
+                    in0=ao_sb[:, 2 + t, :],
+                    scalar=1.0,
+                    in1=ao_sb[:, 2 + t, :],
+                    op0=ALU.mult,
+                    op1=ALU.mult,
+                    accum_out=sum_sq_v[:, t : t + 1],
+                )
+            rms = keep.tile([P, PACK], F32)
+            nc.vector.tensor_scalar(
+                out=rms[:, 0:2], in0=sum_sq_s[:], scalar1=1.0 / E, scalar2=EPS_RMS, op0=ALU.mult, op1=ALU.add
+            )
+            nc.vector.tensor_scalar(
+                out=rms[:, 2:4], in0=sum_sq_v[:], scalar1=1.0 / E, scalar2=EPS_RMS, op0=ALU.mult, op1=ALU.add
+            )
+            nc.scalar.activation(out=rms[:], in_=rms[:], func=ACT.Sqrt)
+            inv_rms = keep.tile([P, PACK], F32)
+            nc.vector.reciprocal(out=inv_rms[:], in_=rms[:])
+            grouped = {0: group_v_block(0), 1: group_v_block(1), 2: group_v_block(2)}
+            a_grouped = keep.tile([P, E, PACK], BF16, align_bytes=64)
+            for u in range(PACK):
+                nc.vector.tensor_tensor(
+                    out=a_grouped[:, u * P : (u + 1) * P, :],
+                    in0=ao_sb[:, :, u:E:PACK].rearrange("p t c -> p c t"),
+                    in1=inv_rms[:].unsqueeze(1).to_broadcast([P, P, PACK]),
+                    op=ALU.mult,
+                )
+            nc.vector.quantize_mx(
+                out=a_codes[:].bitcast(FP8X4),
+                scales=a_scales[:],
+                in_=a_grouped[:].rearrange("p c t -> p (c t)"),
+            )
+            quantise_v_block(0, grouped[0])
+
+            silu = {0: multiply_and_silu(v_codes[:, 0, :], v_scales[:, 0, :])}
+            quantise_v_block(1, grouped[1])
+            for b in range(V_BLOCKS):
+                if b + 1 < V_BLOCKS:
+                    silu[b + 1] = multiply_and_silu(v_codes[:, b + 1, :], v_scales[:, b + 1, :])
+                h_codes, h_scales = quantise_h(silu[b])
+                if b + 2 < V_BLOCKS:
+                    quantise_v_block(b + 2, grouped[b + 2])
+                if b + 3 < V_BLOCKS:
+                    grouped[b + 3] = group_v_block(b + 3)
+                update_first_weight(b, h_codes, h_scales)
 
             gate = keep.tile([P, 2], F32)
             inv_gate = keep.tile([P, 2], F32)
@@ -257,63 +332,6 @@ def tile_retentionmechanism_pc_t_kernel(
                 out=offset[:], in0=inv_gate[:], scalar1=EPS_STD, scalar2=None, op0=ALU.mult
             )
 
-            sum_sq_s = keep.tile([P, 2], F32)
-            sum_sq_v = keep.tile([P, 2], F32)
-            for t in range(2):
-                squares = stage.tile([P, BLOCK], BF16)
-                nc.scalar.activation(
-                    out=squares[:], in_=ao_sb[:, t, :], func=ACT.Square, accum_out=sum_sq_s[:, t : t + 1]
-                )
-                squares_v = stage.tile([P, BLOCK], F32)
-                nc.vector.scalar_tensor_tensor(
-                    out=squares_v[:],
-                    in0=ao_sb[:, 2 + t, :],
-                    scalar=1.0,
-                    in1=ao_sb[:, 2 + t, :],
-                    op0=ALU.mult,
-                    op1=ALU.mult,
-                    accum_out=sum_sq_v[:, t : t + 1],
-                )
-            rms = keep.tile([P, PACK], F32)
-            nc.vector.tensor_scalar(
-                out=rms[:, 0:2], in0=sum_sq_s[:], scalar1=1.0 / E, scalar2=EPS_RMS, op0=ALU.mult, op1=ALU.add
-            )
-            nc.vector.tensor_scalar(
-                out=rms[:, 2:4], in0=sum_sq_v[:], scalar1=1.0 / E, scalar2=EPS_RMS, op0=ALU.mult, op1=ALU.add
-            )
-            nc.scalar.activation(out=rms[:], in_=rms[:], func=ACT.Sqrt)
-            inv_rms = keep.tile([P, PACK], F32)
-            nc.vector.reciprocal(out=inv_rms[:], in_=rms[:])
-            grouped = {0: group_v_block(0, nc.scalar.copy)}
-            a_grouped = keep.tile([P, E, PACK], BF16, align_bytes=64)
-            for u in range(PACK):
-                nc.vector.tensor_tensor(
-                    out=a_grouped[:, u * P : (u + 1) * P, :],
-                    in0=ao_sb[:, :, u:E:PACK].rearrange("p t c -> p c t"),
-                    in1=inv_rms[:].unsqueeze(1).to_broadcast([P, P, PACK]),
-                    op=ALU.mult,
-                )
-            quantise_v_block(0, grouped[0])
-            nc.vector.quantize_mx(
-                out=a_codes[:].bitcast(FP8X4),
-                scales=a_scales[:],
-                in_=a_grouped[:].rearrange("p c t -> p (c t)"),
-            )
-
-            silu = {0: multiply_and_silu(v_codes[:, 0, :], v_scales[:, 0, :])}
-            grouped[1] = group_v_block(1, nc.vector.tensor_copy)
-            grouped[2] = group_v_block(2, nc.vector.tensor_copy)
-            quantise_v_block(1, grouped[1])
-            for b in range(V_BLOCKS):
-                if b + 1 < V_BLOCKS:
-                    silu[b + 1] = multiply_and_silu(v_codes[:, b + 1, :], v_scales[:, b + 1, :])
-                h_codes, h_scales = quantise_h(silu[b])
-                if b + 2 < V_BLOCKS:
-                    quantise_v_block(b + 2, grouped[b + 2])
-                if b + 3 < V_BLOCKS:
-                    grouped[b + 3] = group_v_block(b + 3, nc.vector.tensor_copy)
-                update_first_weight(b, h_codes, h_scales)
-
         factor_1 = norm_factor(stats_1, mean_of_1, slope[:, 0:1], offset[:, 0:1], "first")
 
         wo_grouped = keep.tile([P, E, PACK], BF16, align_bytes=64)
@@ -335,13 +353,11 @@ def tile_retentionmechanism_pc_t_kernel(
 
         for c in range(PACK):
             for half in range(HALVES):
+                blocks = slice(half * BLOCKS_PER_HALF, (half + 1) * BLOCKS_PER_HALF)
+                scaled = outbound.tile([P, BLOCKS_PER_HALF, BLOCK], F32)
                 nc.vector.tensor_scalar(
-                    out=z1[:, c, half, :],
-                    in0=z1[:, c, half, :],
-                    scalar1=factor_1[:],
-                    scalar2=None,
-                    op0=ALU.mult,
+                    out=scaled[:], in0=z1[:, blocks, c, :], scalar1=factor_1[:], scalar2=None, op0=ALU.mult
                 )
-                nc.sync.dma_start(out=out1_dram[:, c, half, :], in_=z1[:, c, half, :])
+                nc.sync.dma_start(out=out1_dram[:, c, half, :], in_=scaled[:].rearrange("p k j -> p (k j)"))
         nc.scalar.activation(out=z2[:], in_=z2[:], func=ACT.Copy, scale=factor_2[:])
         nc.sync.dma_start(out=out2_dram, in_=z2[:])

@@ -149,7 +149,6 @@ def tile_retentionmechanism_pc_t_kernel(
             )
 
         def update_first_weight(b, h_codes, h_scales):
-            last = b == V_BLOCKS - 1
             for c in range(PACK):
                 n_slice = slice(c * P, (c + 1) * P)
                 product = psum_second.tile([P, BLOCK], F32)
@@ -163,10 +162,6 @@ def tile_retentionmechanism_pc_t_kernel(
                     stop=True,
                 )
                 add_weight(z1[:, b, c, :], product[:], v_sb[:, b, c, :], stats_1, b * PACK + c)
-                if last:
-                    sum_squares(z1[:, b, c : c + 1, :], 1, stats_1, b * PACK + c)
-            if not last:
-                sum_squares(z1[:, b, :, :], PACK, stats_1, b * PACK)
 
         def update_second_weight(h_codes, h_scales):
             for c in range(PACK):
@@ -306,6 +301,10 @@ def tile_retentionmechanism_pc_t_kernel(
                 if b + 3 < V_BLOCKS:
                     grouped[b + 3] = group_v_block(b + 3)
                 update_first_weight(b, h_codes, h_scales)
+                if b > 0:
+                    sum_squares(z1[:, b - 1, :, :], PACK, stats_1, (b - 1) * PACK)
+            for c in range(PACK):
+                sum_squares(z1[:, V_BLOCKS - 1, c : c + 1, :], 1, stats_1, (V_BLOCKS - 1) * PACK + c)
 
             gate = keep.tile([P, 2], F32)
             inv_gate = keep.tile([P, 2], F32)

@@ -22,6 +22,8 @@ BLOCKS_PER_HALF = Q // BLOCK
 V_BLOCKS = HALVES * BLOCKS_PER_HALF
 COUNT_1 = E * HALVES * Q
 COUNT_2 = E * E
+GRAM_SLICE = PACK - 1
+GRAM_PART = 1
 PARTS = V_BLOCKS * PACK
 EPS_RMS = 1.1920929e-07
 EPS_STD = 1e-08
@@ -45,7 +47,8 @@ def tile_retentionmechanism_pc_t_kernel(
         unread = ctx.enter_context(tc.tile_pool(name="unread", bufs=2))
         outbound = ctx.enter_context(tc.tile_pool(name="outbound", bufs=4))
         psum_first = ctx.enter_context(tc.psum_pool(name="psum_first", bufs=4))
-        psum_second = ctx.enter_context(tc.psum_pool(name="psum_second", bufs=4))
+        psum_second = ctx.enter_context(tc.psum_pool(name="psum_second", bufs=3))
+        psum_gram = ctx.enter_context(tc.psum_pool(name="psum_gram", bufs=1))
 
         ao_sb = keep.tile([P, PACK, E], BF16)
         v_sb = keep.tile([P, V_BLOCKS, PACK, BLOCK], BF16)
@@ -148,6 +151,19 @@ def tile_retentionmechanism_pc_t_kernel(
                 out=squares[:, 0:slices, :], in_=z, func=ACT.Square, accum_out=stats[:, 1, part : part + 1]
             )
 
+        gram = psum_gram.tile([P, P], F32)
+
+        def gram_squares(b):
+            for s in range(BLOCK // P):
+                x = z1[:, b, GRAM_SLICE, s * P : (s + 1) * P]
+                nc.tensor.matmul(
+                    out=gram[:],
+                    lhsT=x,
+                    rhs=x,
+                    start=(b == 0 and s == 0),
+                    stop=(b == V_BLOCKS - 2 and s == BLOCK // P - 1),
+                )
+
         def update_first_weight(b, h_codes, h_scales):
             for c in range(PACK):
                 n_slice = slice(c * P, (c + 1) * P)
@@ -228,6 +244,8 @@ def tile_retentionmechanism_pc_t_kernel(
             nc.gpsimd.memset(mean_of_2[:], 1.0 / COUNT_2)
             ident = keep.tile([P, P], BF16)
             make_identity(nc, ident[:])
+            ident_f32 = keep.tile([P, P], F32)
+            make_identity(nc, ident_f32[:])
 
             for t in range(PACK):
                 nc.sync.dma_start(out=ao_sb[:, t, :], in_=ao_dram[:, t, :])
@@ -295,6 +313,8 @@ def tile_retentionmechanism_pc_t_kernel(
             for b in range(V_BLOCKS):
                 if b + 1 < V_BLOCKS:
                     silu[b + 1] = multiply_and_silu(v_codes[:, b + 1, :], v_scales[:, b + 1, :])
+                if b > 0:
+                    gram_squares(b - 1)
                 h_codes, h_scales = quantise_h(silu[b])
                 if b + 2 < V_BLOCKS:
                     quantise_v_block(b + 2, grouped[b + 2])
@@ -302,9 +322,20 @@ def tile_retentionmechanism_pc_t_kernel(
                     grouped[b + 3] = group_v_block(b + 3)
                 update_first_weight(b, h_codes, h_scales)
                 if b > 0:
-                    sum_squares(z1[:, b - 1, :, :], PACK, stats_1, (b - 1) * PACK)
+                    sum_squares(z1[:, b - 1, 0:GRAM_SLICE, :], GRAM_SLICE, stats_1, (b - 1) * PACK)
             for c in range(PACK):
                 sum_squares(z1[:, V_BLOCKS - 1, c : c + 1, :], 1, stats_1, (V_BLOCKS - 1) * PACK + c)
+
+            diagonal = keep.tile([P, P], F32)
+            nc.vector.scalar_tensor_tensor(
+                out=diagonal[:],
+                in0=gram[:],
+                scalar=1.0,
+                in1=ident_f32[:],
+                op0=ALU.mult,
+                op1=ALU.mult,
+                accum_out=stats_1[:, 1, GRAM_PART : GRAM_PART + 1],
+            )
 
             gate = keep.tile([P, 2], F32)
             inv_gate = keep.tile([P, 2], F32)

@@ -22,8 +22,10 @@ BLOCKS_PER_HALF = Q // BLOCK
 V_BLOCKS = HALVES * BLOCKS_PER_HALF
 COUNT_1 = E * HALVES * Q
 COUNT_2 = E * E
-GRAM_SLICE = PACK - 1
-GRAM_PART = 1
+GRAM_BLOCKS = V_BLOCKS - 1
+VECTOR_SLICE = PACK - 2
+GATE_BLOCK = V_BLOCKS - 3
+GRAM_PART = 0
 PARTS = V_BLOCKS * PACK
 EPS_RMS = 1.1920929e-07
 EPS_STD = 1e-08
@@ -64,8 +66,13 @@ def tile_retentionmechanism_pc_t_kernel(
         wo_scales = keep.tile([P, E], U8, align_bytes=64)
         z1 = keep.tile([P, V_BLOCKS, PACK, BLOCK], F32)
         z2 = keep.tile([P, PACK, E], F32)
-        stats_1 = keep.tile([P, 2, PARTS], F32)
-        stats_2 = keep.tile([P, 2, PARTS], F32)
+        sums_1 = keep.tile([P, PARTS], F32)
+        squares_1 = keep.tile([P, PARTS], F32)
+        sums_2 = keep.tile([P, PACK], F32)
+        squares_2 = keep.tile([P, PACK], F32)
+
+        behind = keep.tile([P, PACK], BF16)
+        grouped = {}
 
         def columns_of(b):
             q0 = (b % BLOCKS_PER_HALF) * BLOCK
@@ -79,11 +86,20 @@ def tile_retentionmechanism_pc_t_kernel(
             v_grouped = stage.tile([P, BLOCK, PACK], BF16, align_bytes=64)
             rows = v_sb[:, b, :, :]
             if b == 0:
-                nc.scalar.copy(
+                for s in range(BLOCK // P):
+                    cols_s = slice(s * P, (s + 1) * P)
+                    nc.scalar.copy(
+                        out=v_grouped[:, cols_s, :].rearrange("p (c i) t -> p c t i", i=4),
+                        in_=rows[:, :, cols_s].rearrange("p t (c i) -> p c t i", i=4),
+                    )
+            elif b == 1:
+                nc.vector.tensor_copy(
                     out=v_grouped[:].rearrange("p (c i) t -> p c t i", i=4),
                     in_=rows.rearrange("p t (c i) -> p c t i", i=4),
                 )
             else:
+                if b == 2:
+                    nc.gpsimd.tensor_copy(out=behind[:], in_=grouped[1][:, BLOCK - 1, :])
                 for s in range(BLOCK // P):
                     cols_s = slice(s * P, (s + 1) * P)
                     nc.gpsimd.tensor_scalar(
@@ -134,7 +150,7 @@ def tile_retentionmechanism_pc_t_kernel(
             )
             return h_codes, h_scales
 
-        def add_weight(z, product, weight, stats, part):
+        def add_weight(z, product, weight, sums, part):
             nc.vector.scalar_tensor_tensor(
                 out=z,
                 in0=product,
@@ -142,27 +158,69 @@ def tile_retentionmechanism_pc_t_kernel(
                 in1=weight,
                 op0=ALU.mult,
                 op1=ALU.add,
-                accum_out=stats[:, 0, part : part + 1],
+                accum_out=sums[:, part : part + 1],
             )
 
-        def sum_squares(z, slices, stats, part):
-            squares = unread.tile([P, PACK, BLOCK], BF16)
+        def sum_squares(z, squares, part):
+            slices, columns = z.shape[1], z.shape[2]
+            each_square = unread.tile([P, PACK, BLOCK], BF16)
             nc.scalar.activation(
-                out=squares[:, 0:slices, :], in_=z, func=ACT.Square, accum_out=stats[:, 1, part : part + 1]
+                out=each_square[:, 0:slices, 0:columns], in_=z, func=ACT.Square, accum_out=squares[:, part : part + 1]
             )
 
         gram = psum_gram.tile([P, P], F32)
 
         def gram_squares(b):
             for s in range(BLOCK // P):
-                x = z1[:, b, GRAM_SLICE, s * P : (s + 1) * P]
+                x = z1[:, b, 0, s * P : (s + 1) * P]
                 nc.tensor.matmul(
                     out=gram[:],
                     lhsT=x,
                     rhs=x,
                     start=(b == 0 and s == 0),
-                    stop=(b == V_BLOCKS - 2 and s == BLOCK // P - 1),
+                    stop=(b == GRAM_BLOCKS - 1 and s == BLOCK // P - 1),
                 )
+
+        gate = keep.tile([P, 2], F32)
+        inv_gate = keep.tile([P, 2], F32)
+        slope = keep.tile([P, 2], F32)
+        offset = keep.tile([P, 2], F32)
+
+        def prepare_gates():
+            nc.scalar.activation(out=gate[:], in_=tao_sb[:], func=ACT.Abs)
+            nc.gpsimd.tensor_scalar(
+                out=gate[:], in0=gate[:], scalar1=1e-08, scalar2=1.0, op0=ALU.max, op1=ALU.min
+            )
+            nc.gpsimd.tensor_scalar(
+                out=gate[:], in0=gate[:], scalar1=TARGET_STD, scalar2=0.0, op0=ALU.mult, op1=ALU.add
+            )
+
+        def prepare_factors():
+            nc.vector.reciprocal(out=inv_gate[:], in_=gate[:])
+            for w, count in enumerate((COUNT_1, COUNT_2)):
+                nc.gpsimd.tensor_scalar(
+                    out=slope[:, w : w + 1],
+                    in0=inv_gate[:, w : w + 1],
+                    scalar1=(count / (count - 1.0)) ** 0.5,
+                    scalar2=0.0,
+                    op0=ALU.mult,
+                    op1=ALU.add,
+                )
+            nc.gpsimd.tensor_scalar(
+                out=offset[:], in0=inv_gate[:], scalar1=EPS_STD, scalar2=0.0, op0=ALU.mult, op1=ALU.add
+            )
+
+        def read_gram():
+            diagonal = unread.tile([P, P], F32)
+            nc.vector.scalar_tensor_tensor(
+                out=diagonal[:],
+                in0=gram[:],
+                scalar=1.0,
+                in1=ident_f32[:],
+                op0=ALU.mult,
+                op1=ALU.mult,
+                accum_out=squares_1[:, GRAM_PART : GRAM_PART + 1],
+            )
 
         def update_first_weight(b, h_codes, h_scales):
             for c in range(PACK):
@@ -177,7 +235,7 @@ def tile_retentionmechanism_pc_t_kernel(
                     start=True,
                     stop=True,
                 )
-                add_weight(z1[:, b, c, :], product[:], v_sb[:, b, c, :], stats_1, b * PACK + c)
+                add_weight(z1[:, b, c, :], product[:], v_sb[:, b, c, :], sums_1, b * PACK + c)
 
         def update_second_weight(h_codes, h_scales):
             for c in range(PACK):
@@ -192,50 +250,51 @@ def tile_retentionmechanism_pc_t_kernel(
                     start=True,
                     stop=True,
                 )
-                add_weight(z2[:, c, :], product[:], wo_sb[:, c, :], stats_2, c)
-                sum_squares(z2[:, c : c + 1, :], 1, stats_2, c)
+                add_weight(z2[:, c, :], product[:], wo_sb[:, c, :], sums_2, c)
+                sum_squares(z2[:, c : c + 1, :], squares_2, c)
 
-        def norm_factor(stats, mean_of, slope, offset, name):
-            spread = psum_second.tile([P, 2 * PARTS], F32, tag="product")
-            nc.tensor.matmul(
-                out=spread[:],
-                lhsT=mean_of[:],
-                rhs=stats[:].rearrange("p s k -> p (s k)"),
-                start=True,
-                stop=True,
+        def mean_square(sums, mean_of, name):
+            parts = sums.shape[1]
+            spread = psum_second.tile([P, parts], F32, tag="product")
+            nc.tensor.matmul(out=spread[:], lhsT=mean_of[:], rhs=sums[:], start=True, stop=True)
+            mean = keep.tile([P, 1], F32, name=name + "_mean")
+            nc.vector.tensor_reduce(out=mean[:], in_=spread[:], axis=mybir.AxisListType.X, op=ALU.add)
+            share = keep.tile([P, 1], F32, name=name + "_share")
+            nc.vector.tensor_scalar(
+                out=share[:], in0=mean[:], scalar1=mean[:], scalar2=-1.0 / parts, op0=ALU.mult, op1=ALU.mult
             )
-            moments = keep.tile([P, 2], F32, name=name + "_moments")
-            nc.vector.tensor_reduce(
-                out=moments[:],
-                in_=spread[:].rearrange("p (s k) -> p s k", s=2),
-                axis=mybir.AxisListType.X,
-                op=ALU.add,
-            )
-            spread_of_z = keep.tile([P, 1], F32, name=name + "_spread")
+            return share
+
+        def norm_factor(squares, mean_of, share, slope, offset, name):
+            parts = squares.shape[1]
+            spread = psum_second.tile([P, parts], F32, tag="product")
+            nc.tensor.matmul(out=spread[:], lhsT=mean_of[:], rhs=squares[:], start=True, stop=True)
+            terms = keep.tile([P, parts], F32, name=name + "_terms")
+            variance = keep.tile([P, 1], F32, name=name + "_variance")
             nc.vector.scalar_tensor_tensor(
-                out=spread_of_z[:],
-                in0=moments[:, 0:1],
-                scalar=moments[:, 0:1],
-                in1=moments[:, 1:2],
+                out=terms[:],
+                in0=spread[:],
+                scalar=1.0,
+                in1=share[:].to_broadcast([P, parts]),
                 op0=ALU.mult,
-                op1=ALU.subtract,
-                reverse1=True,
+                op1=ALU.add,
+                accum_out=variance[:],
             )
-            nc.gpsimd.tensor_tensor(out=spread_of_z[:], in0=spread_of_z[:], in1=half_power[:], op=ALU.pow)
+            nc.gpsimd.tensor_tensor(out=variance[:], in0=variance[:], in1=half_power[:], op=ALU.pow)
             factor = keep.tile([P, 1], F32, name=name + "_factor")
             nc.vector.tensor_scalar(
-                out=factor[:], in0=spread_of_z[:], scalar1=slope, scalar2=offset, op0=ALU.mult, op1=ALU.add
+                out=factor[:], in0=variance[:], scalar1=slope, scalar2=offset, op0=ALU.mult, op1=ALU.add
             )
             nc.vector.reciprocal(out=factor[:], in_=factor[:])
             return factor
 
         with tc.manual_schedule():
             nc.vector.memset(w_scales[:].bitcast(I32), 0)
-            nc.vector.memset(stats_1[:], 0.0)
-            nc.vector.memset(stats_2[:], 0.0)
+            nc.vector.memset(sums_1[:], 0.0)
+            nc.vector.memset(squares_1[:], 0.0)
             one = keep.tile([P, 1], F32)
             nc.vector.memset(one[:], 1.0)
-            nc.scalar.activation(out=one[:], in_=one[:], func=ACT.Sqrt)
+            nc.scalar.activation(out=one[:], in_=one[:], func=ACT.Abs_reciprocal_sqrt)
             half_power = keep.tile([P, 1], F32)
             nc.gpsimd.memset(half_power[:], 0.5)
             mean_of_1 = keep.tile([P, P], F32)
@@ -265,12 +324,11 @@ def tile_retentionmechanism_pc_t_kernel(
             nc.sync.dma_start(out=wo_sb[:], in_=w_out.rearrange("(c p) d -> p c d", p=P))
             nc.sync.dma_start(out=tao_sb[:], in_=tao.rearrange("a b -> (a b)").partition_broadcast(P))
 
-            sum_sq_s = keep.tile([P, 2], F32)
-            sum_sq_v = keep.tile([P, 2], F32)
+            sum_sq = keep.tile([P, PACK], F32)
             for t in range(2):
                 squares_s = unread.tile([P, BLOCK], BF16)
                 nc.scalar.activation(
-                    out=squares_s[:], in_=ao_sb[:, t, :], func=ACT.Square, accum_out=sum_sq_s[:, t : t + 1]
+                    out=squares_s[:], in_=ao_sb[:, t, :], func=ACT.Square, accum_out=sum_sq[:, t : t + 1]
                 )
                 squares_v = unread.tile([P, BLOCK], F32)
                 nc.vector.scalar_tensor_tensor(
@@ -280,89 +338,86 @@ def tile_retentionmechanism_pc_t_kernel(
                     in1=ao_sb[:, 2 + t, :],
                     op0=ALU.mult,
                     op1=ALU.mult,
-                    accum_out=sum_sq_v[:, t : t + 1],
+                    accum_out=sum_sq[:, 2 + t : 3 + t],
                 )
-            rms = keep.tile([P, PACK], F32)
-            nc.vector.tensor_scalar(
-                out=rms[:, 0:2], in0=sum_sq_s[:], scalar1=1.0 / E, scalar2=EPS_RMS, op0=ALU.mult, op1=ALU.add
-            )
-            nc.vector.tensor_scalar(
-                out=rms[:, 2:4], in0=sum_sq_v[:], scalar1=1.0 / E, scalar2=EPS_RMS, op0=ALU.mult, op1=ALU.add
-            )
-            nc.scalar.activation(out=rms[:], in_=rms[:], func=ACT.Sqrt)
             inv_rms = keep.tile([P, PACK], F32)
-            nc.vector.reciprocal(out=inv_rms[:], in_=rms[:])
-            grouped = {0: group_v_block(0), 1: group_v_block(1), 2: group_v_block(2)}
-            a_grouped = keep.tile([P, E, PACK], BF16, align_bytes=64)
-            for u in range(PACK):
-                nc.vector.tensor_tensor(
-                    out=a_grouped[:, u * P : (u + 1) * P, :],
-                    in0=ao_sb[:, :, u:E:PACK].rearrange("p t c -> p c t"),
-                    in1=inv_rms[:].unsqueeze(1).to_broadcast([P, P, PACK]),
-                    op=ALU.mult,
-                )
-            nc.vector.quantize_mx(
-                out=a_codes[:].bitcast(FP8X4),
-                scales=a_scales[:],
-                in_=a_grouped[:].rearrange("p c t -> p (c t)"),
+            nc.scalar.activation(
+                out=inv_rms[:], in_=sum_sq[:], func=ACT.Abs_reciprocal_sqrt, scale=1.0 / E, bias=EPS_RMS
             )
-            quantise_v_block(0, grouped[0])
+            nc.scalar.activation(out=one[:], in_=one[:], func=ACT.Silu)
+            a_scaled = keep.tile([P, PACK, E], BF16)
+            for t in range(PACK):
+                nc.vector.tensor_scalar(
+                    out=a_scaled[:, t, :],
+                    in0=ao_sb[:, t, :],
+                    scalar1=inv_rms[:, t : t + 1],
+                    scalar2=None,
+                    op0=ALU.mult,
+                )
+            a_grouped = keep.tile([P, E, PACK], BF16, align_bytes=64)
+            u_halves = [(u, u + 2) for u in (0, 2)]
+            for u0, u1 in u_halves:
+                nc.vector.tensor_copy(
+                    out=a_grouped[:, u0 * P : u1 * P, :].rearrange("p (u c) t -> p u c t", c=P),
+                    in_=a_scaled[:].rearrange("p t (c u) -> p u c t", u=PACK)[:, u0:u1, :, :],
+                )
+            grouped[0] = group_v_block(0)
+            for u0, u1 in u_halves:
+                nc.vector.quantize_mx(
+                    out=a_codes[:, u0 * P : u1 * P].bitcast(FP8X4),
+                    scales=a_scales[:, u0 * P : u1 * P],
+                    in_=a_grouped[:, u0 * P : u1 * P, :].rearrange("p c t -> p (c t)"),
+                )
+            for s in range(BLOCK // P):
+                cols = slice(s * P, (s + 1) * P)
+                nc.vector.quantize_mx(
+                    out=v_codes[:, 0, cols].bitcast(FP8X4),
+                    scales=v_scales[:, 0, cols],
+                    in_=grouped[0][:, cols, :].rearrange("p j t -> p (j t)"),
+                )
+            grouped[1] = group_v_block(1)
 
+            grouped[2] = group_v_block(2)
             silu = {0: multiply_and_silu(v_codes[:, 0, :], v_scales[:, 0, :])}
             quantise_v_block(1, grouped[1])
             for b in range(V_BLOCKS):
                 if b + 1 < V_BLOCKS:
                     silu[b + 1] = multiply_and_silu(v_codes[:, b + 1, :], v_scales[:, b + 1, :])
-                if b > 0:
-                    gram_squares(b - 1)
                 h_codes, h_scales = quantise_h(silu[b])
-                if b + 2 < V_BLOCKS:
+                if 0 < b < V_BLOCKS - 2:
                     quantise_v_block(b + 2, grouped[b + 2])
                 if b + 3 < V_BLOCKS:
                     grouped[b + 3] = group_v_block(b + 3)
+                if b == GATE_BLOCK:
+                    prepare_gates()
+                if b == GATE_BLOCK + 1:
+                    prepare_factors()
                 update_first_weight(b, h_codes, h_scales)
+                if b == 0:
+                    quantise_v_block(2, grouped[2])
                 if b > 0:
-                    sum_squares(z1[:, b - 1, 0:GRAM_SLICE, :], GRAM_SLICE, stats_1, (b - 1) * PACK)
+                    gram_squares(b - 1)
+                    sum_squares(z1[:, b - 1, 1:PACK, :], squares_1, (b - 1) * PACK + 1)
+            b = V_BLOCKS - 1
             for c in range(PACK):
-                sum_squares(z1[:, V_BLOCKS - 1, c : c + 1, :], 1, stats_1, (V_BLOCKS - 1) * PACK + c)
+                z, part = z1[:, b, c, :], b * PACK + c
+                if c == VECTOR_SLICE:
+                    last_square = unread.tile([P, BLOCK], F32)
+                    nc.vector.scalar_tensor_tensor(
+                        out=last_square[:],
+                        in0=z,
+                        scalar=1.0,
+                        in1=z,
+                        op0=ALU.mult,
+                        op1=ALU.mult,
+                        accum_out=squares_1[:, part : part + 1],
+                    )
+                else:
+                    sum_squares(z1[:, b, c : c + 1, :], squares_1, part)
+            read_gram()
 
-            diagonal = keep.tile([P, P], F32)
-            nc.vector.scalar_tensor_tensor(
-                out=diagonal[:],
-                in0=gram[:],
-                scalar=1.0,
-                in1=ident_f32[:],
-                op0=ALU.mult,
-                op1=ALU.mult,
-                accum_out=stats_1[:, 1, GRAM_PART : GRAM_PART + 1],
-            )
-
-            gate = keep.tile([P, 2], F32)
-            inv_gate = keep.tile([P, 2], F32)
-            slope = keep.tile([P, 2], F32)
-            offset = keep.tile([P, 2], F32)
-            nc.vector.tensor_scalar(out=gate[:], in0=tao_sb[:], scalar1=-1.0, scalar2=None, op0=ALU.mult)
-            nc.vector.tensor_tensor(out=gate[:], in0=gate[:], in1=tao_sb[:], op=ALU.max)
-            nc.vector.tensor_scalar(
-                out=gate[:], in0=gate[:], scalar1=1e-08, scalar2=1.0, op0=ALU.max, op1=ALU.min
-            )
-            nc.vector.tensor_scalar(
-                out=gate[:], in0=gate[:], scalar1=TARGET_STD, scalar2=None, op0=ALU.mult
-            )
-            nc.vector.reciprocal(out=inv_gate[:], in_=gate[:])
-            for w, count in enumerate((COUNT_1, COUNT_2)):
-                nc.vector.tensor_scalar(
-                    out=slope[:, w : w + 1],
-                    in0=inv_gate[:, w : w + 1],
-                    scalar1=(count / (count - 1.0)) ** 0.5,
-                    scalar2=None,
-                    op0=ALU.mult,
-                )
-            nc.vector.tensor_scalar(
-                out=offset[:], in0=inv_gate[:], scalar1=EPS_STD, scalar2=None, op0=ALU.mult
-            )
-
-        factor_1 = norm_factor(stats_1, mean_of_1, slope[:, 0:1], offset[:, 0:1], "first")
+            share_1 = mean_square(sums_1, mean_of_1, "first")
+            factor_1 = norm_factor(squares_1, mean_of_1, share_1, slope[:, 0:1], offset[:, 0:1], "first")
 
         wo_grouped = keep.tile([P, E, PACK], BF16, align_bytes=64)
         for c in range(PACK):
@@ -379,15 +434,25 @@ def tile_retentionmechanism_pc_t_kernel(
         )
         h_codes, h_scales = quantise_h(multiply_and_silu(wo_codes, wo_scales))
         update_second_weight(h_codes, h_scales)
-        factor_2 = norm_factor(stats_2, mean_of_2, slope[:, 1:2], offset[:, 1:2], "second")
+        share_2 = mean_square(sums_2, mean_of_2, "second")
+        factor_2 = norm_factor(squares_2, mean_of_2, share_2, slope[:, 1:2], offset[:, 1:2], "second")
 
         for c in range(PACK):
             for half in range(HALVES):
-                blocks = slice(half * BLOCKS_PER_HALF, (half + 1) * BLOCKS_PER_HALF)
                 scaled = outbound.tile([P, BLOCKS_PER_HALF, BLOCK], F32)
-                nc.vector.tensor_scalar(
-                    out=scaled[:], in0=z1[:, blocks, c, :], scalar1=factor_1[:], scalar2=None, op0=ALU.mult
-                )
-                nc.sync.dma_start(out=out1_dram[:, c, half, :], in_=scaled[:].rearrange("p k j -> p (k j)"))
+                step = 1 if c == 0 and half == 0 else BLOCKS_PER_HALF
+                for k in range(0, BLOCKS_PER_HALF, step):
+                    b = half * BLOCKS_PER_HALF + k
+                    nc.vector.tensor_scalar(
+                        out=scaled[:, k : k + step, :],
+                        in0=z1[:, b : b + step, c, :],
+                        scalar1=factor_1[:],
+                        scalar2=None,
+                        op0=ALU.mult,
+                    )
+                    nc.sync.dma_start(
+                        out=out1_dram[:, c, half, k * BLOCK : (k + step) * BLOCK],
+                        in_=scaled[:, k : k + step, :].rearrange("p k j -> p (k j)"),
+                    )
         nc.scalar.activation(out=z2[:], in_=z2[:], func=ACT.Copy, scale=factor_2[:])
         nc.sync.dma_start(out=out2_dram, in_=z2[:])

@@ -18,6 +18,7 @@ E = P * PACK
 HALVES = 2
 Q = 2048
 BLOCK = 512
+HALF = BLOCK // 2
 BLOCKS_PER_HALF = Q // BLOCK
 V_BLOCKS = HALVES * BLOCKS_PER_HALF
 COUNT_1 = E * HALVES * Q
@@ -46,6 +47,7 @@ def tile_retentionmechanism_pc_t_kernel(
     with ExitStack() as ctx:
         keep = ctx.enter_context(tc.tile_pool(name="keep", bufs=1))
         stage = ctx.enter_context(tc.tile_pool(name="stage", bufs=3))
+        singles = ctx.enter_context(tc.tile_pool(name="singles", bufs=2))
         unread = ctx.enter_context(tc.tile_pool(name="unread", bufs=2))
         outbound = ctx.enter_context(tc.tile_pool(name="outbound", bufs=4))
         psum_first = ctx.enter_context(tc.psum_pool(name="psum_first", bufs=4))
@@ -60,8 +62,8 @@ def tile_retentionmechanism_pc_t_kernel(
         w_scales = keep.tile([P, E], U8, align_bytes=64)
         a_codes = keep.tile([P, E], U32, align_bytes=64)
         a_scales = keep.tile([P, E], U8, align_bytes=64)
-        v_codes = keep.tile([P, V_BLOCKS, BLOCK], U32, align_bytes=64)
-        v_scales = keep.tile([P, V_BLOCKS, BLOCK], U8, align_bytes=64)
+        v_codes = keep.tile([P, 2, BLOCK], U32, align_bytes=64)
+        v_scales = keep.tile([P, 2, BLOCK], U8, align_bytes=64)
         wo_codes = keep.tile([P, E], U32, align_bytes=64)
         wo_scales = keep.tile([P, E], U8, align_bytes=64)
         z1 = keep.tile([P, V_BLOCKS, PACK, BLOCK], F32)
@@ -72,7 +74,20 @@ def tile_retentionmechanism_pc_t_kernel(
         squares_2 = keep.tile([P, PACK], F32)
 
         behind = keep.tile([P, PACK], BF16)
-        grouped = {}
+        pairs = {}
+        pair_codes = {}
+        pair_scales = {}
+        v_grouped = {}
+        h_grouped = {}
+        v_quantised = {}
+        h_quantised = {}
+
+        def new_pair(b):
+            pair = stage.tile([P, 2, BLOCK, PACK], BF16, align_bytes=64)
+            pairs[b] = pair
+            h_grouped[b] = pair[:, 0, :, :]
+            if b + 2 < V_BLOCKS:
+                v_grouped[b + 2] = pair[:, 1, :, :]
 
         def columns_of(b):
             q0 = (b % BLOCKS_PER_HALF) * BLOCK
@@ -83,44 +98,48 @@ def tile_retentionmechanism_pc_t_kernel(
             nc.sync.dma_start(out=v_sb[:, b, :, :], in_=v_dram[:, :, half, cols])
 
         def group_v_block(b):
-            v_grouped = stage.tile([P, BLOCK, PACK], BF16, align_bytes=64)
             rows = v_sb[:, b, :, :]
+            if b < 2:
+                alone = singles.tile([P, BLOCK, PACK], BF16, align_bytes=64)
+                v_grouped[b] = alone[:]
+            else:
+                new_pair(b - 2)
             if b == 0:
                 for s in range(BLOCK // P):
                     cols_s = slice(s * P, (s + 1) * P)
                     nc.scalar.copy(
-                        out=v_grouped[:, cols_s, :].rearrange("p (c i) t -> p c t i", i=4),
+                        out=v_grouped[b][:, cols_s, :].rearrange("p (c i) t -> p c t i", i=4),
                         in_=rows[:, :, cols_s].rearrange("p t (c i) -> p c t i", i=4),
                     )
             elif b == 1:
                 nc.vector.tensor_copy(
-                    out=v_grouped[:].rearrange("p (c i) t -> p c t i", i=4),
+                    out=v_grouped[b].rearrange("p (c i) t -> p c t i", i=4),
                     in_=rows.rearrange("p t (c i) -> p c t i", i=4),
                 )
             else:
                 if b == 2:
-                    nc.gpsimd.tensor_copy(out=behind[:], in_=grouped[1][:, BLOCK - 1, :])
-                for s in range(BLOCK // P):
+                    nc.gpsimd.tensor_copy(out=behind[:], in_=v_grouped[1][:, BLOCK - 1, :])
+                for s in range((BLOCK if b > 2 else HALF) // P):
                     cols_s = slice(s * P, (s + 1) * P)
                     nc.gpsimd.tensor_scalar(
-                        out=v_grouped[:, cols_s, :],
+                        out=v_grouped[b][:, cols_s, :],
                         in0=rows[:, :, cols_s].rearrange("p t j -> p j t"),
                         scalar1=1.0,
                         scalar2=0.0,
                         op0=ALU.mult,
                         op1=ALU.add,
                     )
-            return v_grouped
 
-        def quantise_v_block(b, v_grouped):
-            nc.vector.quantize_mx(
-                out=v_codes[:, b, :].bitcast(FP8X4),
-                scales=v_scales[:, b, :],
-                in_=v_grouped[:].rearrange("p j t -> p (j t)"),
+        def group_rest(b):
+            nc.vector.tensor_copy(
+                out=v_grouped[b][:, HALF:, :].rearrange("p (c i) t -> p c t i", i=4),
+                in_=v_sb[:, b, :, HALF:].rearrange("p t (c i) -> p c t i", i=4),
             )
 
-        def multiply_and_silu(x_codes, x_scales):
-            h_grouped = stage.tile([P, BLOCK, PACK], BF16, align_bytes=64)
+        def quantise(codes, scales, values):
+            nc.vector.quantize_mx(out=codes.bitcast(FP8X4), scales=scales, in_=values)
+
+        def multiply_and_silu(x_codes, x_scales, silu):
             for s in range(BLOCK // P):
                 cols = slice(s * P, (s + 1) * P)
                 bank = psum_first.tile([P, PACK, P], F32)
@@ -136,19 +155,22 @@ def tile_retentionmechanism_pc_t_kernel(
                         stop=True,
                     )
                 nc.scalar.activation(
-                    out=h_grouped[:, cols, :], in_=bank[:].rearrange("p t j -> p j t"), func=ACT.Silu
+                    out=silu[:, cols, :], in_=bank[:].rearrange("p t j -> p j t"), func=ACT.Silu
                 )
-            return h_grouped
 
-        def quantise_h(h_grouped):
-            h_codes = stage.tile([P, BLOCK], U32, align_bytes=64)
-            h_scales = stage.tile([P, BLOCK], U8, align_bytes=64)
-            nc.vector.quantize_mx(
-                out=h_codes[:].bitcast(FP8X4),
-                scales=h_scales[:],
-                in_=h_grouped[:].rearrange("p j t -> p (j t)"),
+        def quantise_pair(b, members):
+            if b not in pair_codes:
+                codes = stage.tile([P, 2, BLOCK], U32, align_bytes=64)
+                scales = stage.tile([P, 2, BLOCK], U8, align_bytes=64)
+                pair_codes[b] = codes
+                pair_scales[b] = scales
+                h_quantised[b] = (codes[:, 0, :], scales[:, 0, :])
+                v_quantised[b + 2] = (codes[:, 1, :], scales[:, 1, :])
+            quantise(
+                pair_codes[b][:, members, :].rearrange("p w j -> p (w j)"),
+                pair_scales[b][:, members, :].rearrange("p w j -> p (w j)"),
+                pairs[b][:, members, :, :].rearrange("p w j t -> p (w j t)"),
             )
-            return h_codes, h_scales
 
         def add_weight(z, product, weight, sums, part):
             nc.vector.scalar_tensor_tensor(
@@ -222,7 +244,10 @@ def tile_retentionmechanism_pc_t_kernel(
                 accum_out=squares_1[:, GRAM_PART : GRAM_PART + 1],
             )
 
-        def update_first_weight(b, h_codes, h_scales):
+        products = {}
+
+        def multiply_by_w(b):
+            codes, scales = h_quantised[b]
             for c in range(PACK):
                 n_slice = slice(c * P, (c + 1) * P)
                 product = psum_second.tile([P, BLOCK], F32)
@@ -230,12 +255,19 @@ def tile_retentionmechanism_pc_t_kernel(
                     out=product[:],
                     lhsT=w_codes[:, n_slice].bitcast(FP8X4),
                     lhsT_scale=w_scales[:, n_slice],
-                    rhs=h_codes[:].bitcast(FP8X4),
-                    rhs_scale=h_scales[:],
+                    rhs=codes.bitcast(FP8X4),
+                    rhs_scale=scales,
                     start=True,
                     stop=True,
                 )
-                add_weight(z1[:, b, c, :], product[:], v_sb[:, b, c, :], sums_1, b * PACK + c)
+                products[b, c] = product
+                if c < PACK - 1:
+                    update_slice(b, c)
+                if b == 0 and c == 0:
+                    quantise_pair(0, slice(1, 2))
+
+        def update_slice(b, c):
+            add_weight(z1[:, b, c, :], products[b, c][:], v_sb[:, b, c, :], sums_1, b * PACK + c)
 
         def update_second_weight(h_codes, h_scales):
             for c in range(PACK):
@@ -361,7 +393,7 @@ def tile_retentionmechanism_pc_t_kernel(
                     out=a_grouped[:, u0 * P : u1 * P, :].rearrange("p (u c) t -> p u c t", c=P),
                     in_=a_scaled[:].rearrange("p t (c u) -> p u c t", u=PACK)[:, u0:u1, :, :],
                 )
-            grouped[0] = group_v_block(0)
+            group_v_block(0)
             for u0, u1 in u_halves:
                 nc.vector.quantize_mx(
                     out=a_codes[:, u0 * P : u1 * P].bitcast(FP8X4),
@@ -370,34 +402,36 @@ def tile_retentionmechanism_pc_t_kernel(
                 )
             for s in range(BLOCK // P):
                 cols = slice(s * P, (s + 1) * P)
-                nc.vector.quantize_mx(
-                    out=v_codes[:, 0, cols].bitcast(FP8X4),
-                    scales=v_scales[:, 0, cols],
-                    in_=grouped[0][:, cols, :].rearrange("p j t -> p (j t)"),
-                )
-            grouped[1] = group_v_block(1)
+                quantise(v_codes[:, 0, cols], v_scales[:, 0, cols], v_grouped[0][:, cols, :].rearrange("p j t -> p (j t)"))
+            group_v_block(1)
+            quantise(v_codes[:, 1, :], v_scales[:, 1, :], v_grouped[1].rearrange("p j t -> p (j t)"))
+            for b in range(2):
+                v_quantised[b] = (v_codes[:, b, :], v_scales[:, b, :])
 
-            grouped[2] = group_v_block(2)
-            silu = {0: multiply_and_silu(v_codes[:, 0, :], v_scales[:, 0, :])}
-            quantise_v_block(1, grouped[1])
+            group_v_block(2)
+            multiply_and_silu(*v_quantised[0], h_grouped[0])
             for b in range(V_BLOCKS):
-                if b + 1 < V_BLOCKS:
-                    silu[b + 1] = multiply_and_silu(v_codes[:, b + 1, :], v_scales[:, b + 1, :])
-                h_codes, h_scales = quantise_h(silu[b])
-                if 0 < b < V_BLOCKS - 2:
-                    quantise_v_block(b + 2, grouped[b + 2])
                 if b + 3 < V_BLOCKS:
-                    grouped[b + 3] = group_v_block(b + 3)
+                    group_v_block(b + 3)
+                elif b + 1 < V_BLOCKS:
+                    new_pair(b + 1)
+                if b + 1 < V_BLOCKS:
+                    multiply_and_silu(*v_quantised[b + 1], h_grouped[b + 1])
+                together = 0 < b < V_BLOCKS - 2
+                quantise_pair(b, slice(0, 2 if together else 1))
+                if b == 0:
+                    group_rest(2)
+                else:
+                    update_slice(b - 1, PACK - 1)
                 if b == GATE_BLOCK:
                     prepare_gates()
                 if b == GATE_BLOCK + 1:
                     prepare_factors()
-                update_first_weight(b, h_codes, h_scales)
-                if b == 0:
-                    quantise_v_block(2, grouped[2])
+                multiply_by_w(b)
                 if b > 0:
                     gram_squares(b - 1)
                     sum_squares(z1[:, b - 1, 1:PACK, :], squares_1, (b - 1) * PACK + 1)
+            update_slice(V_BLOCKS - 1, PACK - 1)
             b = V_BLOCKS - 1
             for c in range(PACK):
                 z, part = z1[:, b, c, :], b * PACK + c
@@ -419,7 +453,7 @@ def tile_retentionmechanism_pc_t_kernel(
             share_1 = mean_square(sums_1, mean_of_1, "first")
             factor_1 = norm_factor(squares_1, mean_of_1, share_1, slope[:, 0:1], offset[:, 0:1], "first")
 
-        wo_grouped = keep.tile([P, E, PACK], BF16, align_bytes=64)
+        wo_grouped = singles.tile([P, E, PACK], BF16, align_bytes=64, tag="alone")
         for c in range(PACK):
             flipped = psum_first.tile([P, PACK, P], BF16, tag="bank")
             for t in range(PACK):
@@ -427,13 +461,13 @@ def tile_retentionmechanism_pc_t_kernel(
             nc.scalar.copy(
                 out=wo_grouped[:, c * P : (c + 1) * P, :], in_=flipped[:].rearrange("p t i -> p i t")
             )
-        nc.vector.quantize_mx(
-            out=wo_codes[:].bitcast(FP8X4),
-            scales=wo_scales[:],
-            in_=wo_grouped[:].rearrange("p i t -> p (i t)"),
-        )
-        h_codes, h_scales = quantise_h(multiply_and_silu(wo_codes, wo_scales))
-        update_second_weight(h_codes, h_scales)
+        quantise(wo_codes[:], wo_scales[:], wo_grouped[:].rearrange("p i t -> p (i t)"))
+        silu_wo = singles.tile([P, E, PACK], BF16, align_bytes=64, tag="alone")
+        multiply_and_silu(wo_codes, wo_scales, silu_wo)
+        silu_wo_codes = keep.tile([P, E], U32, align_bytes=64)
+        silu_wo_scales = keep.tile([P, E], U8, align_bytes=64)
+        quantise(silu_wo_codes[:], silu_wo_scales[:], silu_wo[:].rearrange("p i t -> p (i t)"))
+        update_second_weight(silu_wo_codes, silu_wo_scales)
         share_2 = mean_square(sums_2, mean_of_2, "second")
         factor_2 = norm_factor(squares_2, mean_of_2, share_2, slope[:, 1:2], offset[:, 1:2], "second")
 

@@ -21,12 +21,14 @@ BLOCK = 512
 HALF = BLOCK // 2
 BLOCKS_PER_HALF = Q // BLOCK
 V_BLOCKS = HALVES * BLOCKS_PER_HALF
-COUNT_1 = E * HALVES * Q
+J = HALVES * Q
+COUNT_1 = E * J
 COUNT_2 = E * E
 GRAM_BLOCKS = V_BLOCKS - 1
+GRAM_SLICE = PACK - 1
 VECTOR_SLICE = PACK - 2
 GATE_BLOCK = V_BLOCKS - 3
-GRAM_PART = 0
+GRAM_PART = GRAM_SLICE
 PARTS = V_BLOCKS * PACK
 EPS_RMS = 1.1920929e-07
 EPS_STD = 1e-08
@@ -41,7 +43,7 @@ def tile_retentionmechanism_pc_t_kernel(
     nc = tc.nc
     ao_dram = ao.rearrange("(t p) e -> p t e", p=P)
     v_dram = w_swiglu.rearrange("(t p h) q -> p t h q", p=P, h=HALVES)
-    out1_dram = out_0.rearrange("(t p h) q -> p t h q", p=P, h=HALVES)
+    out1_dram = out_0.rearrange("(t p h) q -> p t (h q)", p=P, h=HALVES)
     out2_dram = out_1.rearrange("(c p) n -> p c n", p=P)
 
     with ExitStack() as ctx:
@@ -49,7 +51,6 @@ def tile_retentionmechanism_pc_t_kernel(
         stage = ctx.enter_context(tc.tile_pool(name="stage", bufs=3))
         singles = ctx.enter_context(tc.tile_pool(name="singles", bufs=2))
         unread = ctx.enter_context(tc.tile_pool(name="unread", bufs=2))
-        outbound = ctx.enter_context(tc.tile_pool(name="outbound", bufs=4))
         psum_first = ctx.enter_context(tc.psum_pool(name="psum_first", bufs=4))
         psum_second = ctx.enter_context(tc.psum_pool(name="psum_second", bufs=3))
         psum_gram = ctx.enter_context(tc.psum_pool(name="psum_gram", bufs=1))
@@ -66,7 +67,7 @@ def tile_retentionmechanism_pc_t_kernel(
         v_scales = keep.tile([P, 2, BLOCK], U8, align_bytes=64)
         wo_codes = keep.tile([P, E], U32, align_bytes=64)
         wo_scales = keep.tile([P, E], U8, align_bytes=64)
-        z1 = keep.tile([P, V_BLOCKS, PACK, BLOCK], F32)
+        z1 = keep.tile([P, PACK, J], F32)
         z2 = keep.tile([P, PACK, E], F32)
         sums_1 = keep.tile([P, PARTS], F32)
         squares_1 = keep.tile([P, PARTS], F32)
@@ -88,6 +89,9 @@ def tile_retentionmechanism_pc_t_kernel(
             h_grouped[b] = pair[:, 0, :, :]
             if b + 2 < V_BLOCKS:
                 v_grouped[b + 2] = pair[:, 1, :, :]
+
+        def z1_block(b):
+            return z1[:, :, b * BLOCK : (b + 1) * BLOCK]
 
         def columns_of(b):
             q0 = (b % BLOCKS_PER_HALF) * BLOCK
@@ -194,7 +198,7 @@ def tile_retentionmechanism_pc_t_kernel(
 
         def gram_squares(b):
             for s in range(BLOCK // P):
-                x = z1[:, b, 0, s * P : (s + 1) * P]
+                x = z1_block(b)[:, GRAM_SLICE, s * P : (s + 1) * P]
                 nc.tensor.matmul(
                     out=gram[:],
                     lhsT=x,
@@ -267,7 +271,7 @@ def tile_retentionmechanism_pc_t_kernel(
                     quantise_pair(0, slice(1, 2))
 
         def update_slice(b, c):
-            add_weight(z1[:, b, c, :], products[b, c][:], v_sb[:, b, c, :], sums_1, b * PACK + c)
+            add_weight(z1_block(b)[:, c, :], products[b, c][:], v_sb[:, b, c, :], sums_1, b * PACK + c)
 
         def update_second_weight(h_codes, h_scales):
             for c in range(PACK):
@@ -357,7 +361,7 @@ def tile_retentionmechanism_pc_t_kernel(
             nc.sync.dma_start(out=tao_sb[:], in_=tao.rearrange("a b -> (a b)").partition_broadcast(P))
 
             sum_sq = keep.tile([P, PACK], F32)
-            for t in range(2):
+            for t in range(0, PACK, 2):
                 squares_s = unread.tile([P, BLOCK], BF16)
                 nc.scalar.activation(
                     out=squares_s[:], in_=ao_sb[:, t, :], func=ACT.Square, accum_out=sum_sq[:, t : t + 1]
@@ -365,12 +369,12 @@ def tile_retentionmechanism_pc_t_kernel(
                 squares_v = unread.tile([P, BLOCK], F32)
                 nc.vector.scalar_tensor_tensor(
                     out=squares_v[:],
-                    in0=ao_sb[:, 2 + t, :],
+                    in0=ao_sb[:, t + 1, :],
                     scalar=1.0,
-                    in1=ao_sb[:, 2 + t, :],
+                    in1=ao_sb[:, t + 1, :],
                     op0=ALU.mult,
                     op1=ALU.mult,
-                    accum_out=sum_sq[:, 2 + t : 3 + t],
+                    accum_out=sum_sq[:, t + 1 : t + 2],
                 )
             inv_rms = keep.tile([P, PACK], F32)
             nc.scalar.activation(
@@ -430,11 +434,11 @@ def tile_retentionmechanism_pc_t_kernel(
                 multiply_by_w(b)
                 if b > 0:
                     gram_squares(b - 1)
-                    sum_squares(z1[:, b - 1, 1:PACK, :], squares_1, (b - 1) * PACK + 1)
+                    sum_squares(z1_block(b - 1)[:, 0:GRAM_SLICE, :], squares_1, (b - 1) * PACK)
             update_slice(V_BLOCKS - 1, PACK - 1)
             b = V_BLOCKS - 1
             for c in range(PACK):
-                z, part = z1[:, b, c, :], b * PACK + c
+                z, part = z1_block(b)[:, c, :], b * PACK + c
                 if c == VECTOR_SLICE:
                     last_square = unread.tile([P, BLOCK], F32)
                     nc.vector.scalar_tensor_tensor(
@@ -447,7 +451,7 @@ def tile_retentionmechanism_pc_t_kernel(
                         accum_out=squares_1[:, part : part + 1],
                     )
                 else:
-                    sum_squares(z1[:, b, c : c + 1, :], squares_1, part)
+                    sum_squares(z1_block(b)[:, c : c + 1, :], squares_1, part)
             read_gram()
 
             share_1 = mean_square(sums_1, mean_of_1, "first")
@@ -472,21 +476,13 @@ def tile_retentionmechanism_pc_t_kernel(
         factor_2 = norm_factor(squares_2, mean_of_2, share_2, slope[:, 1:2], offset[:, 1:2], "second")
 
         for c in range(PACK):
-            for half in range(HALVES):
-                scaled = outbound.tile([P, BLOCKS_PER_HALF, BLOCK], F32)
-                step = 1 if c == 0 and half == 0 else BLOCKS_PER_HALF
-                for k in range(0, BLOCKS_PER_HALF, step):
-                    b = half * BLOCKS_PER_HALF + k
-                    nc.vector.tensor_scalar(
-                        out=scaled[:, k : k + step, :],
-                        in0=z1[:, b : b + step, c, :],
-                        scalar1=factor_1[:],
-                        scalar2=None,
-                        op0=ALU.mult,
-                    )
-                    nc.sync.dma_start(
-                        out=out1_dram[:, c, half, k * BLOCK : (k + step) * BLOCK],
-                        in_=scaled[:, k : k + step, :].rearrange("p k j -> p (k j)"),
-                    )
+            edges = [0, BLOCK, 2 * BLOCK, Q, J] if c == 0 else [0, Q, J]
+            for start, stop in zip(edges[:-1], edges[1:]):
+                piece = z1[:, c, start:stop]
+                nc.vector.tensor_scalar(out=piece, in0=piece, scalar1=factor_1[:], scalar2=None, op0=ALU.mult)
+                if c < 2:
+                    nc.sync.dma_start(out=out1_dram[:, c, start:stop], in_=piece)
+            if c >= 2:
+                nc.sync.dma_start(out=out1_dram[:, c, :], in_=z1[:, c, :])
         nc.scalar.activation(out=z2[:], in_=z2[:], func=ACT.Copy, scale=factor_2[:])
         nc.sync.dma_start(out=out2_dram, in_=z2[:])

@@ -18,6 +18,7 @@ E = P * PACK
 HALVES = 2
 Q = 2048
 BLOCK = 512
+STRIP = 64
 HALF = BLOCK // 2
 BLOCKS_PER_HALF = Q // BLOCK
 V_BLOCKS = HALVES * BLOCKS_PER_HALF
@@ -123,8 +124,8 @@ def tile_retentionmechanism_pc_t_kernel(
             else:
                 if b == 2:
                     nc.gpsimd.tensor_copy(out=behind[:], in_=v_grouped[1][:, BLOCK - 1, :])
-                for s in range((BLOCK if b > 2 else HALF) // P):
-                    cols_s = slice(s * P, (s + 1) * P)
+                for start in range(0, BLOCK if b > 2 else HALF, STRIP):
+                    cols_s = slice(start, start + STRIP)
                     nc.gpsimd.tensor_scalar(
                         out=v_grouped[b][:, cols_s, :],
                         in0=rows[:, :, cols_s].rearrange("p t j -> p j t"),
@@ -480,9 +481,6 @@ def tile_retentionmechanism_pc_t_kernel(
             for start, stop in zip(edges[:-1], edges[1:]):
                 piece = z1[:, c, start:stop]
                 nc.vector.tensor_scalar(out=piece, in0=piece, scalar1=factor_1[:], scalar2=None, op0=ALU.mult)
-                if c < 2:
-                    nc.sync.dma_start(out=out1_dram[:, c, start:stop], in_=piece)
-            if c >= 2:
-                nc.sync.dma_start(out=out1_dram[:, c, :], in_=z1[:, c, :])
+                nc.sync.dma_start(out=out1_dram[:, c, start:stop], in_=piece)
         nc.scalar.activation(out=z2[:], in_=z2[:], func=ACT.Copy, scale=factor_2[:])
         nc.sync.dma_start(out=out2_dram, in_=z2[:])

@@ -18,8 +18,8 @@ E = P * PACK
 HALVES = 2
 Q = 2048
 BLOCK = 512
-STRIP = 64
-HALF = BLOCK // 2
+GPSIMD_COLS = slice(0, 3 * P)
+VECTOR_COLS = slice(3 * P, BLOCK)
 BLOCKS_PER_HALF = Q // BLOCK
 V_BLOCKS = HALVES * BLOCKS_PER_HALF
 J = HALVES * Q
@@ -75,21 +75,13 @@ def tile_retentionmechanism_pc_t_kernel(
         sums_2 = keep.tile([P, PACK], F32)
         squares_2 = keep.tile([P, PACK], F32)
 
-        behind = keep.tile([P, PACK], BF16)
-        pairs = {}
-        pair_codes = {}
-        pair_scales = {}
-        v_grouped = {}
-        h_grouped = {}
+        trio = keep.tile([P, 3, BLOCK, PACK], BF16, align_bytes=64)
+        v_next = trio[:, 1, :, :]
         v_quantised = {}
         h_quantised = {}
 
-        def new_pair(b):
-            pair = stage.tile([P, 2, BLOCK, PACK], BF16, align_bytes=64)
-            pairs[b] = pair
-            h_grouped[b] = pair[:, 0, :, :]
-            if b + 2 < V_BLOCKS:
-                v_grouped[b + 2] = pair[:, 1, :, :]
+        def h_grouped(b):
+            return trio[:, 2 * (b % 2), :, :]
 
         def z1_block(b):
             return z1[:, :, b * BLOCK : (b + 1) * BLOCK]
@@ -102,43 +94,20 @@ def tile_retentionmechanism_pc_t_kernel(
             half, cols = columns_of(b)
             nc.sync.dma_start(out=v_sb[:, b, :, :], in_=v_dram[:, :, half, cols])
 
-        def group_v_block(b):
-            rows = v_sb[:, b, :, :]
-            if b < 2:
-                alone = singles.tile([P, BLOCK, PACK], BF16, align_bytes=64)
-                v_grouped[b] = alone[:]
-            else:
-                new_pair(b - 2)
-            if b == 0:
-                for s in range(BLOCK // P):
-                    cols_s = slice(s * P, (s + 1) * P)
-                    nc.scalar.copy(
-                        out=v_grouped[b][:, cols_s, :].rearrange("p (c i) t -> p c t i", i=4),
-                        in_=rows[:, :, cols_s].rearrange("p t (c i) -> p c t i", i=4),
-                    )
-            elif b == 1:
-                nc.vector.tensor_copy(
-                    out=v_grouped[b].rearrange("p (c i) t -> p c t i", i=4),
-                    in_=rows.rearrange("p t (c i) -> p c t i", i=4),
-                )
-            else:
-                if b == 2:
-                    nc.gpsimd.tensor_copy(out=behind[:], in_=v_grouped[1][:, BLOCK - 1, :])
-                for start in range(0, BLOCK if b > 2 else HALF, STRIP):
-                    cols_s = slice(start, start + STRIP)
-                    nc.gpsimd.tensor_scalar(
-                        out=v_grouped[b][:, cols_s, :],
-                        in0=rows[:, :, cols_s].rearrange("p t j -> p j t"),
-                        scalar1=1.0,
-                        scalar2=0.0,
-                        op0=ALU.mult,
-                        op1=ALU.add,
-                    )
+        def group_on(engine_copy, out, b, cols):
+            engine_copy(
+                out=out[:, cols, :].rearrange("p (c i) t -> p c t i", i=4),
+                in_=v_sb[:, b, :, cols].rearrange("p t (c i) -> p c t i", i=4),
+            )
 
-        def group_rest(b):
-            nc.vector.tensor_copy(
-                out=v_grouped[b][:, HALF:, :].rearrange("p (c i) t -> p c t i", i=4),
-                in_=v_sb[:, b, :, HALF:].rearrange("p t (c i) -> p c t i", i=4),
+        def group_on_gpsimd(b):
+            nc.gpsimd.tensor_scalar(
+                out=v_next[:, GPSIMD_COLS, :],
+                in0=v_sb[:, b, :, GPSIMD_COLS].rearrange("p t j -> p j t"),
+                scalar1=1.0,
+                scalar2=0.0,
+                op0=ALU.mult,
+                op1=ALU.add,
             )
 
         def quantise(codes, scales, values):
@@ -163,19 +132,21 @@ def tile_retentionmechanism_pc_t_kernel(
                     out=silu[:, cols, :], in_=bank[:].rearrange("p t j -> p j t"), func=ACT.Silu
                 )
 
-        def quantise_pair(b, members):
-            if b not in pair_codes:
-                codes = stage.tile([P, 2, BLOCK], U32, align_bytes=64)
-                scales = stage.tile([P, 2, BLOCK], U8, align_bytes=64)
-                pair_codes[b] = codes
-                pair_scales[b] = scales
-                h_quantised[b] = (codes[:, 0, :], scales[:, 0, :])
-                v_quantised[b + 2] = (codes[:, 1, :], scales[:, 1, :])
-            quantise(
-                pair_codes[b][:, members, :].rearrange("p w j -> p (w j)"),
-                pair_scales[b][:, members, :].rearrange("p w j -> p (w j)"),
-                pairs[b][:, members, :, :].rearrange("p w j t -> p (w j t)"),
-            )
+        def quantise_round(b):
+            h_member, v_member = (0, 1) if b % 2 == 0 else (1, 0)
+            codes = stage.tile([P, 2, BLOCK], U32, align_bytes=64)
+            scales = stage.tile([P, 2, BLOCK], U8, align_bytes=64)
+            h_quantised[b] = (codes[:, h_member, :], scales[:, h_member, :])
+            if b + 2 < V_BLOCKS:
+                v_quantised[b + 2] = (codes[:, v_member, :], scales[:, v_member, :])
+                pair = trio[:, b % 2 : b % 2 + 2, :, :]
+                quantise(
+                    codes[:].rearrange("p w j -> p (w j)"),
+                    scales[:].rearrange("p w j -> p (w j)"),
+                    pair.rearrange("p w j t -> p (w j t)"),
+                )
+            else:
+                quantise(*h_quantised[b], h_grouped(b).rearrange("p j t -> p (j t)"))
 
         def add_weight(z, product, weight, sums, part):
             nc.vector.scalar_tensor_tensor(
@@ -268,8 +239,6 @@ def tile_retentionmechanism_pc_t_kernel(
                 products[b, c] = product
                 if c < PACK - 1:
                     update_slice(b, c)
-                if b == 0 and c == 0:
-                    quantise_pair(0, slice(1, 2))
 
         def update_slice(b, c):
             add_weight(z1_block(b)[:, c, :], products[b, c][:], v_sb[:, b, c, :], sums_1, b * PACK + c)
@@ -398,7 +367,13 @@ def tile_retentionmechanism_pc_t_kernel(
                     out=a_grouped[:, u0 * P : u1 * P, :].rearrange("p (u c) t -> p u c t", c=P),
                     in_=a_scaled[:].rearrange("p t (c u) -> p u c t", u=PACK)[:, u0:u1, :, :],
                 )
-            group_v_block(0)
+            first_two = []
+            for b in range(2):
+                alone = singles.tile([P, BLOCK, PACK], BF16, align_bytes=64)
+                first_two.append(alone)
+                v_quantised[b] = (v_codes[:, b, :], v_scales[:, b, :])
+            for s in range(BLOCK // P):
+                group_on(nc.scalar.copy, first_two[0], 0, slice(s * P, (s + 1) * P))
             for u0, u1 in u_halves:
                 nc.vector.quantize_mx(
                     out=a_codes[:, u0 * P : u1 * P].bitcast(FP8X4),
@@ -407,26 +382,23 @@ def tile_retentionmechanism_pc_t_kernel(
                 )
             for s in range(BLOCK // P):
                 cols = slice(s * P, (s + 1) * P)
-                quantise(v_codes[:, 0, cols], v_scales[:, 0, cols], v_grouped[0][:, cols, :].rearrange("p j t -> p (j t)"))
-            group_v_block(1)
-            quantise(v_codes[:, 1, :], v_scales[:, 1, :], v_grouped[1].rearrange("p j t -> p (j t)"))
-            for b in range(2):
-                v_quantised[b] = (v_codes[:, b, :], v_scales[:, b, :])
+                quantise(
+                    v_codes[:, 0, cols], v_scales[:, 0, cols], first_two[0][:, cols, :].rearrange("p j t -> p (j t)")
+                )
+            group_on(nc.vector.tensor_copy, first_two[1], 1, slice(0, BLOCK))
+            quantise(*v_quantised[1], first_two[1][:].rearrange("p j t -> p (j t)"))
+            group_on(nc.vector.tensor_copy, v_next, 2, slice(0, BLOCK))
 
-            group_v_block(2)
-            multiply_and_silu(*v_quantised[0], h_grouped[0])
+            multiply_and_silu(*v_quantised[0], h_grouped(0))
             for b in range(V_BLOCKS):
-                if b + 3 < V_BLOCKS:
-                    group_v_block(b + 3)
-                elif b + 1 < V_BLOCKS:
-                    new_pair(b + 1)
                 if b + 1 < V_BLOCKS:
-                    multiply_and_silu(*v_quantised[b + 1], h_grouped[b + 1])
-                together = 0 < b < V_BLOCKS - 2
-                quantise_pair(b, slice(0, 2 if together else 1))
-                if b == 0:
-                    group_rest(2)
-                else:
+                    multiply_and_silu(*v_quantised[b + 1], h_grouped(b + 1))
+                if 0 < b < V_BLOCKS - 2:
+                    group_on(nc.vector.tensor_copy, v_next, b + 2, VECTOR_COLS)
+                quantise_round(b)
+                if b + 3 < V_BLOCKS:
+                    group_on_gpsimd(b + 3)
+                if b > 0:
                     update_slice(b - 1, PACK - 1)
                 if b == GATE_BLOCK:
                     prepare_gates()

@@ -18,8 +18,6 @@ E = P * PACK
 HALVES = 2
 Q = 2048
 BLOCK = 512
-GPSIMD_COLS = slice(0, 3 * P)
-VECTOR_COLS = slice(3 * P, BLOCK)
 BLOCKS_PER_HALF = Q // BLOCK
 V_BLOCKS = HALVES * BLOCKS_PER_HALF
 J = HALVES * Q
@@ -102,8 +100,8 @@ def tile_retentionmechanism_pc_t_kernel(
 
         def group_on_gpsimd(b):
             nc.gpsimd.tensor_scalar(
-                out=v_next[:, GPSIMD_COLS, :],
-                in0=v_sb[:, b, :, GPSIMD_COLS].rearrange("p t j -> p j t"),
+                out=v_next.rearrange("p (c i) t -> p c t i", i=4),
+                in0=v_sb[:, b, :, :].rearrange("p t (c i) -> p c t i", i=4),
                 scalar1=1.0,
                 scalar2=0.0,
                 op0=ALU.mult,
@@ -393,8 +391,6 @@ def tile_retentionmechanism_pc_t_kernel(
             for b in range(V_BLOCKS):
                 if b + 1 < V_BLOCKS:
                     multiply_and_silu(*v_quantised[b + 1], h_grouped(b + 1))
-                if 0 < b < V_BLOCKS - 2:
-                    group_on(nc.vector.tensor_copy, v_next, b + 2, VECTOR_COLS)
                 quantise_round(b)
                 if b + 3 < V_BLOCKS:
                     group_on_gpsimd(b + 3)

@@ -137,6 +137,10 @@ def tile_retentionmechanism_pc_t_kernel(
             h_quantised[b] = (codes[:, h_member, :], scales[:, h_member, :])
             if b + 2 < V_BLOCKS:
                 v_quantised[b + 2] = (codes[:, v_member, :], scales[:, v_member, :])
+            if b == 0:
+                quantise(*h_quantised[b], h_grouped(b).rearrange("p j t -> p (j t)"))
+                quantise(*v_quantised[b + 2], v_next.rearrange("p j t -> p (j t)"))
+            elif b + 2 < V_BLOCKS:
                 pair = trio[:, b % 2 : b % 2 + 2, :, :]
                 quantise(
                     codes[:].rearrange("p w j -> p (w j)"),
@@ -348,7 +352,6 @@ def tile_retentionmechanism_pc_t_kernel(
             nc.scalar.activation(
                 out=inv_rms[:], in_=sum_sq[:], func=ACT.Abs_reciprocal_sqrt, scale=1.0 / E, bias=EPS_RMS
             )
-            nc.scalar.activation(out=one[:], in_=one[:], func=ACT.Silu)
             a_scaled = keep.tile([P, PACK, E], BF16)
             for t in range(PACK):
                 nc.vector.tensor_scalar(
@@ -372,17 +375,14 @@ def tile_retentionmechanism_pc_t_kernel(
                 v_quantised[b] = (v_codes[:, b, :], v_scales[:, b, :])
             for s in range(BLOCK // P):
                 group_on(nc.scalar.copy, first_two[0], 0, slice(s * P, (s + 1) * P))
+            nc.scalar.activation(out=one[:], in_=one[:], func=ACT.Silu)
             for u0, u1 in u_halves:
                 nc.vector.quantize_mx(
                     out=a_codes[:, u0 * P : u1 * P].bitcast(FP8X4),
                     scales=a_scales[:, u0 * P : u1 * P],
                     in_=a_grouped[:, u0 * P : u1 * P, :].rearrange("p c t -> p (c t)"),
                 )
-            for s in range(BLOCK // P):
-                cols = slice(s * P, (s + 1) * P)
-                quantise(
-                    v_codes[:, 0, cols], v_scales[:, 0, cols], first_two[0][:, cols, :].rearrange("p j t -> p (j t)")
-                )
+            quantise(*v_quantised[0], first_two[0][:].rearrange("p j t -> p (j t)"))
             group_on(nc.vector.tensor_copy, first_two[1], 1, slice(0, BLOCK))
             quantise(*v_quantised[1], first_two[1][:].rearrange("p j t -> p (j t)"))
             group_on(nc.vector.tensor_copy, v_next, 2, slice(0, BLOCK))

@@ -18,6 +18,7 @@ E = P * PACK
 HALVES = 2
 Q = 2048
 BLOCK = 512
+HALF_BLOCKS = (slice(0, BLOCK // 2), slice(BLOCK // 2, BLOCK))
 BLOCKS_PER_HALF = Q // BLOCK
 V_BLOCKS = HALVES * BLOCKS_PER_HALF
 J = HALVES * Q
@@ -98,10 +99,10 @@ def tile_retentionmechanism_pc_t_kernel(
                 in_=v_sb[:, b, :, cols].rearrange("p t (c i) -> p c t i", i=4),
             )
 
-        def group_on_gpsimd(b):
+        def group_on_gpsimd(b, cols):
             nc.gpsimd.tensor_scalar(
-                out=v_next.rearrange("p (c i) t -> p c t i", i=4),
-                in0=v_sb[:, b, :, :].rearrange("p t (c i) -> p c t i", i=4),
+                out=v_next[:, cols, :].rearrange("p (c i) t -> p c t i", i=4),
+                in0=v_sb[:, b, :, cols].rearrange("p t (c i) -> p c t i", i=4),
                 scalar1=1.0,
                 scalar2=0.0,
                 op0=ALU.mult,
@@ -137,18 +138,9 @@ def tile_retentionmechanism_pc_t_kernel(
             h_quantised[b] = (codes[:, h_member, :], scales[:, h_member, :])
             if b + 2 < V_BLOCKS:
                 v_quantised[b + 2] = (codes[:, v_member, :], scales[:, v_member, :])
-            if b == 0:
-                quantise(*h_quantised[b], h_grouped(b).rearrange("p j t -> p (j t)"))
+            quantise(*h_quantised[b], h_grouped(b).rearrange("p j t -> p (j t)"))
+            if b + 2 < V_BLOCKS:
                 quantise(*v_quantised[b + 2], v_next.rearrange("p j t -> p (j t)"))
-            elif b + 2 < V_BLOCKS:
-                pair = trio[:, b % 2 : b % 2 + 2, :, :]
-                quantise(
-                    codes[:].rearrange("p w j -> p (w j)"),
-                    scales[:].rearrange("p w j -> p (w j)"),
-                    pair.rearrange("p w j t -> p (w j t)"),
-                )
-            else:
-                quantise(*h_quantised[b], h_grouped(b).rearrange("p j t -> p (j t)"))
 
         def add_weight(z, product, weight, sums, part):
             nc.vector.scalar_tensor_tensor(
@@ -170,8 +162,8 @@ def tile_retentionmechanism_pc_t_kernel(
 
         gram = psum_gram.tile([P, P], F32)
 
-        def gram_squares(b):
-            for s in range(BLOCK // P):
+        def gram_squares(b, pieces):
+            for s in pieces:
                 x = z1_block(b)[:, GRAM_SLICE, s * P : (s + 1) * P]
                 nc.tensor.matmul(
                     out=gram[:],
@@ -241,6 +233,10 @@ def tile_retentionmechanism_pc_t_kernel(
                 products[b, c] = product
                 if c < PACK - 1:
                     update_slice(b, c)
+                if c == PACK - 2 and b > 0:
+                    gram_squares(b - 1, range(1))
+            if b > 0:
+                gram_squares(b - 1, range(1, BLOCK // P))
 
         def update_slice(b, c):
             add_weight(z1_block(b)[:, c, :], products[b, c][:], v_sb[:, b, c, :], sums_1, b * PACK + c)
@@ -352,6 +348,7 @@ def tile_retentionmechanism_pc_t_kernel(
             nc.scalar.activation(
                 out=inv_rms[:], in_=sum_sq[:], func=ACT.Abs_reciprocal_sqrt, scale=1.0 / E, bias=EPS_RMS
             )
+            nc.scalar.activation(out=one[:], in_=one[:], func=ACT.Silu)
             a_scaled = keep.tile([P, PACK, E], BF16)
             for t in range(PACK):
                 nc.vector.tensor_scalar(
@@ -375,15 +372,21 @@ def tile_retentionmechanism_pc_t_kernel(
                 v_quantised[b] = (v_codes[:, b, :], v_scales[:, b, :])
             for s in range(BLOCK // P):
                 group_on(nc.scalar.copy, first_two[0], 0, slice(s * P, (s + 1) * P))
-            nc.scalar.activation(out=one[:], in_=one[:], func=ACT.Silu)
             for u0, u1 in u_halves:
                 nc.vector.quantize_mx(
                     out=a_codes[:, u0 * P : u1 * P].bitcast(FP8X4),
                     scales=a_scales[:, u0 * P : u1 * P],
                     in_=a_grouped[:, u0 * P : u1 * P, :].rearrange("p c t -> p (c t)"),
                 )
-            quantise(*v_quantised[0], first_two[0][:].rearrange("p j t -> p (j t)"))
+
+            def quantise_half_of_block_0(cols):
+                quantise(
+                    v_codes[:, 0, cols], v_scales[:, 0, cols], first_two[0][:, cols, :].rearrange("p j t -> p (j t)")
+                )
+
+            quantise_half_of_block_0(HALF_BLOCKS[0])
             group_on(nc.vector.tensor_copy, first_two[1], 1, slice(0, BLOCK))
+            quantise_half_of_block_0(HALF_BLOCKS[1])
             quantise(*v_quantised[1], first_two[1][:].rearrange("p j t -> p (j t)"))
             group_on(nc.vector.tensor_copy, v_next, 2, slice(0, BLOCK))
 
@@ -392,8 +395,11 @@ def tile_retentionmechanism_pc_t_kernel(
                 if b + 1 < V_BLOCKS:
                     multiply_and_silu(*v_quantised[b + 1], h_grouped(b + 1))
                 quantise_round(b)
-                if b + 3 < V_BLOCKS:
-                    group_on_gpsimd(b + 3)
+                if b == 0:
+                    group_on(nc.scalar.copy, v_next, 3, HALF_BLOCKS[0])
+                    group_on_gpsimd(3, HALF_BLOCKS[1])
+                elif b + 3 < V_BLOCKS:
+                    group_on_gpsimd(b + 3, slice(0, BLOCK))
                 if b > 0:
                     update_slice(b - 1, PACK - 1)
                 if b == GATE_BLOCK:
@@ -402,7 +408,6 @@ def tile_retentionmechanism_pc_t_kernel(
                     prepare_factors()
                 multiply_by_w(b)
                 if b > 0:
-                    gram_squares(b - 1)
                     sum_squares(z1_block(b - 1)[:, 0:GRAM_SLICE, :], squares_1, (b - 1) * PACK)
             update_slice(V_BLOCKS - 1, PACK - 1)
             b = V_BLOCKS - 1

@@ -24,9 +24,11 @@ V_BLOCKS = HALVES * BLOCKS_PER_HALF
 J = HALVES * Q
 COUNT_1 = E * J
 COUNT_2 = E * E
-GRAM_BLOCKS = V_BLOCKS - 1
+GRAM_BLOCKS = range(1, V_BLOCKS - 1)
 GRAM_SLICE = PACK - 1
 VECTOR_SLICE = PACK - 2
+IDLE_ROUND = V_BLOCKS - 2
+VECTOR_BLOCKS = (IDLE_ROUND - 2, V_BLOCKS - 1)
 GATE_BLOCK = V_BLOCKS - 3
 GRAM_PART = GRAM_SLICE
 PARTS = V_BLOCKS * PACK
@@ -44,11 +46,11 @@ def tile_retentionmechanism_pc_t_kernel(
     ao_dram = ao.rearrange("(t p) e -> p t e", p=P)
     v_dram = w_swiglu.rearrange("(t p h) q -> p t h q", p=P, h=HALVES)
     out1_dram = out_0.rearrange("(t p h) q -> p t (h q)", p=P, h=HALVES)
-    out2_dram = out_1.rearrange("(c p) n -> p c n", p=P)
+    out2_dram = out_1.rearrange("(p c) n -> p c n", p=P)
 
     with ExitStack() as ctx:
         keep = ctx.enter_context(tc.tile_pool(name="keep", bufs=1))
-        stage = ctx.enter_context(tc.tile_pool(name="stage", bufs=3))
+        stage = ctx.enter_context(tc.tile_pool(name="stage", bufs=6))
         singles = ctx.enter_context(tc.tile_pool(name="singles", bufs=2))
         unread = ctx.enter_context(tc.tile_pool(name="unread", bufs=2))
         psum_first = ctx.enter_context(tc.psum_pool(name="psum_first", bufs=4))
@@ -63,8 +65,8 @@ def tile_retentionmechanism_pc_t_kernel(
         w_scales = keep.tile([P, E], U8, align_bytes=64)
         a_codes = keep.tile([P, E], U32, align_bytes=64)
         a_scales = keep.tile([P, E], U8, align_bytes=64)
-        v_codes = keep.tile([P, 2, BLOCK], U32, align_bytes=64)
-        v_scales = keep.tile([P, 2, BLOCK], U8, align_bytes=64)
+        v0_codes = keep.tile([P, BLOCK], U32, align_bytes=64)
+        v0_scales = keep.tile([P, BLOCK], U8, align_bytes=64)
         wo_codes = keep.tile([P, E], U32, align_bytes=64)
         wo_scales = keep.tile([P, E], U8, align_bytes=64)
         z1 = keep.tile([P, PACK, J], F32)
@@ -74,13 +76,12 @@ def tile_retentionmechanism_pc_t_kernel(
         sums_2 = keep.tile([P, PACK], F32)
         squares_2 = keep.tile([P, PACK], F32)
 
-        trio = keep.tile([P, 3, BLOCK, PACK], BF16, align_bytes=64)
-        v_next = trio[:, 1, :, :]
+        grouped = keep.tile([P, 3, BLOCK, PACK], BF16, align_bytes=64)
         v_quantised = {}
         h_quantised = {}
 
-        def h_grouped(b):
-            return trio[:, 2 * (b % 2), :, :]
+        def buffer_of(b):
+            return grouped[:, b % 3, :, :]
 
         def z1_block(b):
             return z1[:, :, b * BLOCK : (b + 1) * BLOCK]
@@ -93,15 +94,15 @@ def tile_retentionmechanism_pc_t_kernel(
             half, cols = columns_of(b)
             nc.sync.dma_start(out=v_sb[:, b, :, :], in_=v_dram[:, :, half, cols])
 
-        def group_on(engine_copy, out, b, cols):
+        def group_on(engine_copy, b, cols):
             engine_copy(
-                out=out[:, cols, :].rearrange("p (c i) t -> p c t i", i=4),
+                out=buffer_of(b)[:, cols, :].rearrange("p (c i) t -> p c t i", i=4),
                 in_=v_sb[:, b, :, cols].rearrange("p t (c i) -> p c t i", i=4),
             )
 
         def group_on_gpsimd(b, cols):
             nc.gpsimd.tensor_scalar(
-                out=v_next[:, cols, :].rearrange("p (c i) t -> p c t i", i=4),
+                out=buffer_of(b)[:, cols, :].rearrange("p (c i) t -> p c t i", i=4),
                 in0=v_sb[:, b, :, cols].rearrange("p t (c i) -> p c t i", i=4),
                 scalar1=1.0,
                 scalar2=0.0,
@@ -131,16 +132,11 @@ def tile_retentionmechanism_pc_t_kernel(
                     out=silu[:, cols, :], in_=bank[:].rearrange("p t j -> p j t"), func=ACT.Silu
                 )
 
-        def quantise_round(b):
-            h_member, v_member = (0, 1) if b % 2 == 0 else (1, 0)
-            codes = stage.tile([P, 2, BLOCK], U32, align_bytes=64)
-            scales = stage.tile([P, 2, BLOCK], U8, align_bytes=64)
-            h_quantised[b] = (codes[:, h_member, :], scales[:, h_member, :])
-            if b + 2 < V_BLOCKS:
-                v_quantised[b + 2] = (codes[:, v_member, :], scales[:, v_member, :])
-            quantise(*h_quantised[b], h_grouped(b).rearrange("p j t -> p (j t)"))
-            if b + 2 < V_BLOCKS:
-                quantise(*v_quantised[b + 2], v_next.rearrange("p j t -> p (j t)"))
+        def quantise_block(b):
+            codes = stage.tile([P, BLOCK], U32, align_bytes=64)
+            scales = stage.tile([P, BLOCK], U8, align_bytes=64)
+            quantise(codes[:], scales[:], buffer_of(b).rearrange("p j t -> p (j t)"))
+            return codes[:], scales[:]
 
         def add_weight(z, product, weight, sums, part):
             nc.vector.scalar_tensor_tensor(
@@ -160,6 +156,19 @@ def tile_retentionmechanism_pc_t_kernel(
                 out=each_square[:, 0:slices, 0:columns], in_=z, func=ACT.Square, accum_out=squares[:, part : part + 1]
             )
 
+        def sum_squares_on_vector(b):
+            z, part = z1_block(b)[:, VECTOR_SLICE, :], b * PACK + VECTOR_SLICE
+            vector_square = unread.tile([P, BLOCK], F32)
+            nc.vector.scalar_tensor_tensor(
+                out=vector_square[:],
+                in0=z,
+                scalar=1.0,
+                in1=z,
+                op0=ALU.mult,
+                op1=ALU.mult,
+                accum_out=squares_1[:, part : part + 1],
+            )
+
         gram = psum_gram.tile([P, P], F32)
 
         def gram_squares(b, pieces):
@@ -169,8 +178,8 @@ def tile_retentionmechanism_pc_t_kernel(
                     out=gram[:],
                     lhsT=x,
                     rhs=x,
-                    start=(b == 0 and s == 0),
-                    stop=(b == GRAM_BLOCKS - 1 and s == BLOCK // P - 1),
+                    start=(b == GRAM_BLOCKS[0] and s == 0),
+                    stop=(b == GRAM_BLOCKS[-1] and s == BLOCK // P - 1),
                 )
 
         gate = keep.tile([P, 2], F32)
@@ -233,9 +242,9 @@ def tile_retentionmechanism_pc_t_kernel(
                 products[b, c] = product
                 if c < PACK - 1:
                     update_slice(b, c)
-                if c == PACK - 2 and b > 0:
+                if c == PACK - 2 and b - 1 in GRAM_BLOCKS:
                     gram_squares(b - 1, range(1))
-            if b > 0:
+            if b - 1 in GRAM_BLOCKS:
                 gram_squares(b - 1, range(1, BLOCK // P))
 
         def update_slice(b, c):
@@ -325,7 +334,7 @@ def tile_retentionmechanism_pc_t_kernel(
                 )
             for b in range(2, V_BLOCKS):
                 load_v_block(b)
-            nc.sync.dma_start(out=wo_sb[:], in_=w_out.rearrange("(c p) d -> p c d", p=P))
+            nc.sync.dma_start(out=wo_sb[:], in_=w_out.rearrange("(p c) d -> p c d", p=P))
             nc.sync.dma_start(out=tao_sb[:], in_=tao.rearrange("a b -> (a b)").partition_broadcast(P))
 
             sum_sq = keep.tile([P, PACK], F32)
@@ -365,13 +374,8 @@ def tile_retentionmechanism_pc_t_kernel(
                     out=a_grouped[:, u0 * P : u1 * P, :].rearrange("p (u c) t -> p u c t", c=P),
                     in_=a_scaled[:].rearrange("p t (c u) -> p u c t", u=PACK)[:, u0:u1, :, :],
                 )
-            first_two = []
-            for b in range(2):
-                alone = singles.tile([P, BLOCK, PACK], BF16, align_bytes=64)
-                first_two.append(alone)
-                v_quantised[b] = (v_codes[:, b, :], v_scales[:, b, :])
             for s in range(BLOCK // P):
-                group_on(nc.scalar.copy, first_two[0], 0, slice(s * P, (s + 1) * P))
+                group_on(nc.scalar.copy, 0, slice(s * P, (s + 1) * P))
             for u0, u1 in u_halves:
                 nc.vector.quantize_mx(
                     out=a_codes[:, u0 * P : u1 * P].bitcast(FP8X4),
@@ -380,53 +384,50 @@ def tile_retentionmechanism_pc_t_kernel(
                 )
 
             def quantise_half_of_block_0(cols):
-                quantise(
-                    v_codes[:, 0, cols], v_scales[:, 0, cols], first_two[0][:, cols, :].rearrange("p j t -> p (j t)")
-                )
+                quantise(v0_codes[:, cols], v0_scales[:, cols], buffer_of(0)[:, cols, :].rearrange("p j t -> p (j t)"))
 
             quantise_half_of_block_0(HALF_BLOCKS[0])
-            group_on(nc.vector.tensor_copy, first_two[1], 1, slice(0, BLOCK))
+            group_on(nc.vector.tensor_copy, 1, slice(0, BLOCK))
             quantise_half_of_block_0(HALF_BLOCKS[1])
-            quantise(*v_quantised[1], first_two[1][:].rearrange("p j t -> p (j t)"))
-            group_on(nc.vector.tensor_copy, v_next, 2, slice(0, BLOCK))
+            v_quantised[0] = (v0_codes[:], v0_scales[:])
+            v_quantised[1] = quantise_block(1)
+            group_on(nc.vector.tensor_copy, 2, slice(0, BLOCK))
 
-            multiply_and_silu(*v_quantised[0], h_grouped(0))
+            multiply_and_silu(*v_quantised[0], buffer_of(0))
             for b in range(V_BLOCKS):
                 if b + 1 < V_BLOCKS:
-                    multiply_and_silu(*v_quantised[b + 1], h_grouped(b + 1))
-                quantise_round(b)
+                    multiply_and_silu(*v_quantised[b + 1], buffer_of(b + 1))
+                h_quantised[b] = quantise_block(b)
+                if b + 2 < V_BLOCKS:
+                    v_quantised[b + 2] = quantise_block(b + 2)
                 if b == 0:
-                    group_on(nc.scalar.copy, v_next, 3, HALF_BLOCKS[0])
+                    group_on(nc.scalar.copy, 3, HALF_BLOCKS[0])
                     group_on_gpsimd(3, HALF_BLOCKS[1])
                 elif b + 3 < V_BLOCKS:
                     group_on_gpsimd(b + 3, slice(0, BLOCK))
                 if b > 0:
                     update_slice(b - 1, PACK - 1)
+                if b == IDLE_ROUND:
+                    sum_squares_on_vector(IDLE_ROUND - 2)
                 if b == GATE_BLOCK:
                     prepare_gates()
                 if b == GATE_BLOCK + 1:
                     prepare_factors()
                 multiply_by_w(b)
                 if b > 0:
-                    sum_squares(z1_block(b - 1)[:, 0:GRAM_SLICE, :], squares_1, (b - 1) * PACK)
+                    if b - 1 in VECTOR_BLOCKS:
+                        scalar_slices = VECTOR_SLICE
+                    else:
+                        scalar_slices = GRAM_SLICE if b - 1 in GRAM_BLOCKS else PACK
+                    sum_squares(z1_block(b - 1)[:, 0:scalar_slices, :], squares_1, (b - 1) * PACK)
             update_slice(V_BLOCKS - 1, PACK - 1)
+            read_gram()
             b = V_BLOCKS - 1
             for c in range(PACK):
-                z, part = z1_block(b)[:, c, :], b * PACK + c
                 if c == VECTOR_SLICE:
-                    last_square = unread.tile([P, BLOCK], F32)
-                    nc.vector.scalar_tensor_tensor(
-                        out=last_square[:],
-                        in0=z,
-                        scalar=1.0,
-                        in1=z,
-                        op0=ALU.mult,
-                        op1=ALU.mult,
-                        accum_out=squares_1[:, part : part + 1],
-                    )
+                    sum_squares_on_vector(b)
                 else:
-                    sum_squares(z1_block(b)[:, c : c + 1, :], squares_1, part)
-            read_gram()
+                    sum_squares(z1_block(b)[:, c : c + 1, :], squares_1, b * PACK + c)
 
             share_1 = mean_square(sums_1, mean_of_1, "first")
             factor_1 = norm_factor(squares_1, mean_of_1, share_1, slope[:, 0:1], offset[:, 0:1], "first")
@@ -450,7 +451,7 @@ def tile_retentionmechanism_pc_t_kernel(
         factor_2 = norm_factor(squares_2, mean_of_2, share_2, slope[:, 1:2], offset[:, 1:2], "second")
 
         for c in range(PACK):
-            edges = [0, BLOCK, 2 * BLOCK, Q, J] if c == 0 else [0, Q, J]
+            edges = [0, BLOCK // 2, BLOCK, 2 * BLOCK, Q, J] if c == 0 else [0, Q, J]
             for start, stop in zip(edges[:-1], edges[1:]):
                 piece = z1[:, c, start:stop]
                 nc.vector.tensor_scalar(out=piece, in0=piece, scalar1=factor_1[:], scalar2=None, op0=ALU.mult)

@@ -18,6 +18,8 @@ E = P * PACK
 HALVES = 2
 Q = 2048
 BLOCK = 512
+SCALAR_COLS = slice(0, P)
+PIECES = BLOCK // P
 HALF_BLOCKS = (slice(0, BLOCK // 2), slice(BLOCK // 2, BLOCK))
 BLOCKS_PER_HALF = Q // BLOCK
 V_BLOCKS = HALVES * BLOCKS_PER_HALF
@@ -27,11 +29,13 @@ COUNT_2 = E * E
 GRAM_BLOCKS = range(1, V_BLOCKS - 1)
 GRAM_SLICE = PACK - 1
 VECTOR_SLICE = PACK - 2
+FIRST_AFTER_SECOND = ((), (0, 1), (2,), (3,))
 IDLE_ROUND = V_BLOCKS - 2
 VECTOR_BLOCKS = (IDLE_ROUND - 2, V_BLOCKS - 1)
 GATE_BLOCK = V_BLOCKS - 3
 GRAM_PART = GRAM_SLICE
 PARTS = V_BLOCKS * PACK
+WARM_UP = 10
 EPS_RMS = 1.1920929e-07
 EPS_STD = 1e-08
 TARGET_STD = 2048.0**-0.5
@@ -113,24 +117,35 @@ def tile_retentionmechanism_pc_t_kernel(
         def quantise(codes, scales, values):
             nc.vector.quantize_mx(out=codes.bitcast(FP8X4), scales=scales, in_=values)
 
-        def multiply_and_silu(x_codes, x_scales, silu):
-            for s in range(BLOCK // P):
-                cols = slice(s * P, (s + 1) * P)
-                bank = psum_first.tile([P, PACK, P], F32)
-                for t in range(PACK):
-                    e_slice = slice(t * P, (t + 1) * P)
-                    nc.tensor.matmul_mx(
-                        out=bank[:, t, :],
-                        lhsT=a_codes[:, e_slice].bitcast(FP8X4),
-                        lhsT_scale=a_scales[:, e_slice],
-                        rhs=x_codes[:, cols].bitcast(FP8X4),
-                        rhs_scale=x_scales[:, cols],
-                        start=True,
-                        stop=True,
-                    )
-                nc.scalar.activation(
-                    out=silu[:, cols, :], in_=bank[:].rearrange("p t j -> p j t"), func=ACT.Silu
+        def multiply_by_a(x_codes, x_scales, s):
+            cols = slice(s * P, (s + 1) * P)
+            bank = psum_first.tile([P, PACK, P], F32)
+            for t in range(PACK):
+                e_slice = slice(t * P, (t + 1) * P)
+                nc.tensor.matmul_mx(
+                    out=bank[:, t, :],
+                    lhsT=a_codes[:, e_slice].bitcast(FP8X4),
+                    lhsT_scale=a_scales[:, e_slice],
+                    rhs=x_codes[:, cols].bitcast(FP8X4),
+                    rhs_scale=x_scales[:, cols],
+                    start=True,
+                    stop=True,
                 )
+            return bank
+
+        def silu_of(bank, silu, s):
+            nc.scalar.activation(
+                out=silu[:, s * P : (s + 1) * P, :], in_=bank[:].rearrange("p t j -> p j t"), func=ACT.Silu
+            )
+
+        first_products = {}
+
+        def first_stage(b, s):
+            first_products[b, s] = multiply_by_a(*v_quantised[b], s)
+
+        def silu_block(b):
+            for s in range(PIECES):
+                silu_of(first_products[b, s], buffer_of(b), s)
 
         def quantise_block(b):
             codes = stage.tile([P, BLOCK], U32, align_bytes=64)
@@ -179,7 +194,7 @@ def tile_retentionmechanism_pc_t_kernel(
                     lhsT=x,
                     rhs=x,
                     start=(b == GRAM_BLOCKS[0] and s == 0),
-                    stop=(b == GRAM_BLOCKS[-1] and s == BLOCK // P - 1),
+                    stop=(b == GRAM_BLOCKS[-1] and s == PIECES - 1),
                 )
 
         gate = keep.tile([P, 2], F32)
@@ -242,10 +257,11 @@ def tile_retentionmechanism_pc_t_kernel(
                 products[b, c] = product
                 if c < PACK - 1:
                     update_slice(b, c)
-                if c == PACK - 2 and b - 1 in GRAM_BLOCKS:
-                    gram_squares(b - 1, range(1))
+                if b + 2 < V_BLOCKS:
+                    for s in FIRST_AFTER_SECOND[c]:
+                        first_stage(b + 2, s)
             if b - 1 in GRAM_BLOCKS:
-                gram_squares(b - 1, range(1, BLOCK // P))
+                gram_squares(b - 1, range(PIECES))
 
         def update_slice(b, c):
             add_weight(z1_block(b)[:, c, :], products[b, c][:], v_sb[:, b, c, :], sums_1, b * PACK + c)
@@ -353,6 +369,9 @@ def tile_retentionmechanism_pc_t_kernel(
                     op1=ALU.mult,
                     accum_out=sum_sq[:, t + 1 : t + 2],
                 )
+            warm = psum_second.tile([P, E], F32, tag="product")
+            for i in range(WARM_UP):
+                nc.tensor.matmul(out=warm[:], lhsT=ident[:], rhs=ao_sb[:, i % PACK, :], start=True, stop=True)
             inv_rms = keep.tile([P, PACK], F32)
             nc.scalar.activation(
                 out=inv_rms[:], in_=sum_sq[:], func=ACT.Abs_reciprocal_sqrt, scale=1.0 / E, bias=EPS_RMS
@@ -374,7 +393,7 @@ def tile_retentionmechanism_pc_t_kernel(
                     out=a_grouped[:, u0 * P : u1 * P, :].rearrange("p (u c) t -> p u c t", c=P),
                     in_=a_scaled[:].rearrange("p t (c u) -> p u c t", u=PACK)[:, u0:u1, :, :],
                 )
-            for s in range(BLOCK // P):
+            for s in range(PIECES):
                 group_on(nc.scalar.copy, 0, slice(s * P, (s + 1) * P))
             for u0, u1 in u_halves:
                 nc.vector.quantize_mx(
@@ -393,16 +412,20 @@ def tile_retentionmechanism_pc_t_kernel(
             v_quantised[1] = quantise_block(1)
             group_on(nc.vector.tensor_copy, 2, slice(0, BLOCK))
 
-            multiply_and_silu(*v_quantised[0], buffer_of(0))
+            for s in range(PIECES):
+                first_stage(0, s)
+            silu_block(0)
+            for s in range(PIECES):
+                first_stage(1, s)
             for b in range(V_BLOCKS):
                 if b + 1 < V_BLOCKS:
-                    multiply_and_silu(*v_quantised[b + 1], buffer_of(b + 1))
+                    silu_block(b + 1)
                 h_quantised[b] = quantise_block(b)
                 if b + 2 < V_BLOCKS:
                     v_quantised[b + 2] = quantise_block(b + 2)
                 if b == 0:
-                    group_on(nc.scalar.copy, 3, HALF_BLOCKS[0])
-                    group_on_gpsimd(3, HALF_BLOCKS[1])
+                    group_on(nc.scalar.copy, 3, SCALAR_COLS)
+                    group_on_gpsimd(3, slice(SCALAR_COLS.stop, BLOCK))
                 elif b + 3 < V_BLOCKS:
                     group_on_gpsimd(b + 3, slice(0, BLOCK))
                 if b > 0:
@@ -442,7 +465,8 @@ def tile_retentionmechanism_pc_t_kernel(
             )
         quantise(wo_codes[:], wo_scales[:], wo_grouped[:].rearrange("p i t -> p (i t)"))
         silu_wo = singles.tile([P, E, PACK], BF16, align_bytes=64, tag="alone")
-        multiply_and_silu(wo_codes, wo_scales, silu_wo)
+        for s in range(PIECES):
+            silu_of(multiply_by_a(wo_codes, wo_scales, s), silu_wo, s)
         silu_wo_codes = keep.tile([P, E], U32, align_bytes=64)
         silu_wo_scales = keep.tile([P, E], U8, align_bytes=64)
         quantise(silu_wo_codes[:], silu_wo_scales[:], silu_wo[:].rearrange("p i t -> p (i t)"))

@@ -35,7 +35,7 @@ VECTOR_BLOCKS = (IDLE_ROUND - 2, V_BLOCKS - 1)
 GATE_BLOCK = V_BLOCKS - 3
 GRAM_PART = GRAM_SLICE
 PARTS = V_BLOCKS * PACK
-WARM_UP = 10
+WARM_UP = 4
 EPS_RMS = 1.1920929e-07
 EPS_STD = 1e-08
 TARGET_STD = 2048.0**-0.5
@@ -393,8 +393,18 @@ def tile_retentionmechanism_pc_t_kernel(
                     out=a_grouped[:, u0 * P : u1 * P, :].rearrange("p (u c) t -> p u c t", c=P),
                     in_=a_scaled[:].rearrange("p t (c u) -> p u c t", u=PACK)[:, u0:u1, :, :],
                 )
-            for s in range(PIECES):
-                group_on(nc.scalar.copy, 0, slice(s * P, (s + 1) * P))
+            for cols in HALF_BLOCKS:
+                laid_out = psum_first.tile([P, BLOCK // 2, PACK], BF16, tag="bank")
+                for s in range(PIECES // 2):
+                    piece = slice(s * P, (s + 1) * P)
+                    nc.tensor.matmul(
+                        out=laid_out[:, piece, :].rearrange("p j t -> p (j t)"),
+                        lhsT=ident[:],
+                        rhs=v_sb[:, 0, :, cols.start + s * P : cols.start + (s + 1) * P].rearrange("p t j -> p j t"),
+                        start=True,
+                        stop=True,
+                    )
+                nc.scalar.copy(out=buffer_of(0)[:, cols, :], in_=laid_out[:])
             for u0, u1 in u_halves:
                 nc.vector.quantize_mx(
                     out=a_codes[:, u0 * P : u1 * P].bitcast(FP8X4),

@@ -26,12 +26,9 @@ V_BLOCKS = HALVES * BLOCKS_PER_HALF
 J = HALVES * Q
 COUNT_1 = E * J
 COUNT_2 = E * E
-GRAM_BLOCKS = range(1, V_BLOCKS - 1)
+GRAM_BLOCKS = range(V_BLOCKS - 1)
 GRAM_SLICE = PACK - 1
-VECTOR_SLICE = PACK - 2
 FIRST_AFTER_SECOND = ((), (0, 1), (2,), (3,))
-IDLE_ROUND = V_BLOCKS - 2
-VECTOR_BLOCKS = (IDLE_ROUND - 2, V_BLOCKS - 1)
 GATE_BLOCK = V_BLOCKS - 3
 GRAM_PART = GRAM_SLICE
 PARTS = V_BLOCKS * PACK
@@ -57,7 +54,7 @@ def tile_retentionmechanism_pc_t_kernel(
         stage = ctx.enter_context(tc.tile_pool(name="stage", bufs=6))
         singles = ctx.enter_context(tc.tile_pool(name="singles", bufs=2))
         unread = ctx.enter_context(tc.tile_pool(name="unread", bufs=2))
-        psum_first = ctx.enter_context(tc.psum_pool(name="psum_first", bufs=4))
+        psum_first = ctx.enter_context(tc.psum_pool(name="psum_first", bufs=1))
         psum_second = ctx.enter_context(tc.psum_pool(name="psum_second", bufs=3))
         psum_gram = ctx.enter_context(tc.psum_pool(name="psum_gram", bufs=1))
 
@@ -119,7 +116,7 @@ def tile_retentionmechanism_pc_t_kernel(
 
         def multiply_by_a(x_codes, x_scales, s):
             cols = slice(s * P, (s + 1) * P)
-            bank = psum_first.tile([P, PACK, P], F32)
+            bank = psum_first.tile([P, PACK, P], F32, tag="bank%d" % s)
             for t in range(PACK):
                 e_slice = slice(t * P, (t + 1) * P)
                 nc.tensor.matmul_mx(
@@ -138,13 +135,19 @@ def tile_retentionmechanism_pc_t_kernel(
                 out=silu[:, s * P : (s + 1) * P, :], in_=bank[:].rearrange("p t j -> p j t"), func=ACT.Silu
             )
 
+        def silu_order(b):
+            return range(PIECES - 1, -1, -1) if b % 2 == 1 else range(PIECES)
+
+        def product_order(b):
+            return silu_order(b - 1) if b > 0 else range(PIECES)
+
         first_products = {}
 
         def first_stage(b, s):
             first_products[b, s] = multiply_by_a(*v_quantised[b], s)
 
         def silu_block(b):
-            for s in range(PIECES):
+            for s in silu_order(b):
                 silu_of(first_products[b, s], buffer_of(b), s)
 
         def quantise_block(b):
@@ -171,19 +174,6 @@ def tile_retentionmechanism_pc_t_kernel(
                 out=each_square[:, 0:slices, 0:columns], in_=z, func=ACT.Square, accum_out=squares[:, part : part + 1]
             )
 
-        def sum_squares_on_vector(b):
-            z, part = z1_block(b)[:, VECTOR_SLICE, :], b * PACK + VECTOR_SLICE
-            vector_square = unread.tile([P, BLOCK], F32)
-            nc.vector.scalar_tensor_tensor(
-                out=vector_square[:],
-                in0=z,
-                scalar=1.0,
-                in1=z,
-                op0=ALU.mult,
-                op1=ALU.mult,
-                accum_out=squares_1[:, part : part + 1],
-            )
-
         gram = psum_gram.tile([P, P], F32)
 
         def gram_squares(b, pieces):
@@ -203,7 +193,8 @@ def tile_retentionmechanism_pc_t_kernel(
         offset = keep.tile([P, 2], F32)
 
         def prepare_gates():
-            nc.scalar.activation(out=gate[:], in_=tao_sb[:], func=ACT.Abs)
+            nc.gpsimd.tensor_tensor(out=gate[:], in0=tao_sb[:], in1=tao_sb[:], op=ALU.mult)
+            nc.gpsimd.tensor_tensor(out=gate[:], in0=gate[:], in1=half_powers[:], op=ALU.pow)
             nc.gpsimd.tensor_scalar(
                 out=gate[:], in0=gate[:], scalar1=1e-08, scalar2=1.0, op0=ALU.max, op1=ALU.min
             )
@@ -258,8 +249,8 @@ def tile_retentionmechanism_pc_t_kernel(
                 if c < PACK - 1:
                     update_slice(b, c)
                 if b + 2 < V_BLOCKS:
-                    for s in FIRST_AFTER_SECOND[c]:
-                        first_stage(b + 2, s)
+                    for i in FIRST_AFTER_SECOND[c]:
+                        first_stage(b + 2, product_order(b + 2)[i])
             if b - 1 in GRAM_BLOCKS:
                 gram_squares(b - 1, range(PIECES))
 
@@ -309,7 +300,7 @@ def tile_retentionmechanism_pc_t_kernel(
                 op1=ALU.add,
                 accum_out=variance[:],
             )
-            nc.gpsimd.tensor_tensor(out=variance[:], in0=variance[:], in1=half_power[:], op=ALU.pow)
+            nc.gpsimd.tensor_tensor(out=variance[:], in0=variance[:], in1=half_powers[:, 0:1], op=ALU.pow)
             factor = keep.tile([P, 1], F32, name=name + "_factor")
             nc.vector.tensor_scalar(
                 out=factor[:], in0=variance[:], scalar1=slope, scalar2=offset, op0=ALU.mult, op1=ALU.add
@@ -324,8 +315,8 @@ def tile_retentionmechanism_pc_t_kernel(
             one = keep.tile([P, 1], F32)
             nc.vector.memset(one[:], 1.0)
             nc.scalar.activation(out=one[:], in_=one[:], func=ACT.Abs_reciprocal_sqrt)
-            half_power = keep.tile([P, 1], F32)
-            nc.gpsimd.memset(half_power[:], 0.5)
+            half_powers = keep.tile([P, 2], F32)
+            nc.gpsimd.memset(half_powers[:], 0.5)
             mean_of_1 = keep.tile([P, P], F32)
             nc.gpsimd.memset(mean_of_1[:], 1.0 / COUNT_1)
             mean_of_2 = keep.tile([P, P], F32)
@@ -393,8 +384,8 @@ def tile_retentionmechanism_pc_t_kernel(
                     out=a_grouped[:, u0 * P : u1 * P, :].rearrange("p (u c) t -> p u c t", c=P),
                     in_=a_scaled[:].rearrange("p t (c u) -> p u c t", u=PACK)[:, u0:u1, :, :],
                 )
-            for cols in HALF_BLOCKS:
-                laid_out = psum_first.tile([P, BLOCK // 2, PACK], BF16, tag="bank")
+            for i, cols in enumerate(HALF_BLOCKS):
+                laid_out = psum_first.tile([P, BLOCK // 2, PACK], BF16, tag="bank%d" % i)
                 for s in range(PIECES // 2):
                     piece = slice(s * P, (s + 1) * P)
                     nc.tensor.matmul(
@@ -440,34 +431,26 @@ def tile_retentionmechanism_pc_t_kernel(
                     group_on_gpsimd(b + 3, slice(0, BLOCK))
                 if b > 0:
                     update_slice(b - 1, PACK - 1)
-                if b == IDLE_ROUND:
-                    sum_squares_on_vector(IDLE_ROUND - 2)
                 if b == GATE_BLOCK:
                     prepare_gates()
                 if b == GATE_BLOCK + 1:
                     prepare_factors()
                 multiply_by_w(b)
                 if b > 0:
-                    if b - 1 in VECTOR_BLOCKS:
-                        scalar_slices = VECTOR_SLICE
-                    else:
-                        scalar_slices = GRAM_SLICE if b - 1 in GRAM_BLOCKS else PACK
+                    scalar_slices = GRAM_SLICE if b - 1 in GRAM_BLOCKS else PACK
                     sum_squares(z1_block(b - 1)[:, 0:scalar_slices, :], squares_1, (b - 1) * PACK)
             update_slice(V_BLOCKS - 1, PACK - 1)
             read_gram()
             b = V_BLOCKS - 1
             for c in range(PACK):
-                if c == VECTOR_SLICE:
-                    sum_squares_on_vector(b)
-                else:
-                    sum_squares(z1_block(b)[:, c : c + 1, :], squares_1, b * PACK + c)
+                sum_squares(z1_block(b)[:, c : c + 1, :], squares_1, b * PACK + c)
 
             share_1 = mean_square(sums_1, mean_of_1, "first")
             factor_1 = norm_factor(squares_1, mean_of_1, share_1, slope[:, 0:1], offset[:, 0:1], "first")
 
         wo_grouped = singles.tile([P, E, PACK], BF16, align_bytes=64, tag="alone")
         for c in range(PACK):
-            flipped = psum_first.tile([P, PACK, P], BF16, tag="bank")
+            flipped = psum_first.tile([P, PACK, P], BF16, tag="bank%d" % c)
             for t in range(PACK):
                 nc.tensor.transpose(flipped[:, t, :], wo_sb[:, c, t * P : (t + 1) * P], ident[:])
             nc.scalar.copy(

@@ -54,7 +54,7 @@ def tile_retentionmechanism_pc_t_kernel(
         stage = ctx.enter_context(tc.tile_pool(name="stage", bufs=6))
         singles = ctx.enter_context(tc.tile_pool(name="singles", bufs=2))
         unread = ctx.enter_context(tc.tile_pool(name="unread", bufs=2))
-        psum_first = ctx.enter_context(tc.psum_pool(name="psum_first", bufs=1))
+        psum_first = ctx.enter_context(tc.psum_pool(name="psum_first", bufs=4))
         psum_second = ctx.enter_context(tc.psum_pool(name="psum_second", bufs=3))
         psum_gram = ctx.enter_context(tc.psum_pool(name="psum_gram", bufs=1))
 
@@ -111,12 +111,25 @@ def tile_retentionmechanism_pc_t_kernel(
                 op1=ALU.add,
             )
 
+        def group_on_tensor(b, cols):
+            laid_out = psum_first.tile([P, BLOCK // 2, PACK], BF16, tag="bank")
+            width = cols.stop - cols.start
+            for k in range(0, width, P):
+                nc.tensor.matmul(
+                    out=laid_out[:, k : k + P, :].rearrange("p j t -> p (j t)"),
+                    lhsT=ident[:],
+                    rhs=v_sb[:, b, :, cols.start + k : cols.start + k + P].rearrange("p t j -> p j t"),
+                    start=True,
+                    stop=True,
+                )
+            nc.scalar.copy(out=buffer_of(b)[:, cols, :], in_=laid_out[:, 0:width, :])
+
         def quantise(codes, scales, values):
             nc.vector.quantize_mx(out=codes.bitcast(FP8X4), scales=scales, in_=values)
 
         def multiply_by_a(x_codes, x_scales, s):
             cols = slice(s * P, (s + 1) * P)
-            bank = psum_first.tile([P, PACK, P], F32, tag="bank%d" % s)
+            bank = psum_first.tile([P, PACK, P], F32)
             for t in range(PACK):
                 e_slice = slice(t * P, (t + 1) * P)
                 nc.tensor.matmul_mx(
@@ -135,19 +148,13 @@ def tile_retentionmechanism_pc_t_kernel(
                 out=silu[:, s * P : (s + 1) * P, :], in_=bank[:].rearrange("p t j -> p j t"), func=ACT.Silu
             )
 
-        def silu_order(b):
-            return range(PIECES - 1, -1, -1) if b % 2 == 1 else range(PIECES)
-
-        def product_order(b):
-            return silu_order(b - 1) if b > 0 else range(PIECES)
-
         first_products = {}
 
         def first_stage(b, s):
             first_products[b, s] = multiply_by_a(*v_quantised[b], s)
 
         def silu_block(b):
-            for s in silu_order(b):
+            for s in range(PIECES):
                 silu_of(first_products[b, s], buffer_of(b), s)
 
         def quantise_block(b):
@@ -193,8 +200,7 @@ def tile_retentionmechanism_pc_t_kernel(
         offset = keep.tile([P, 2], F32)
 
         def prepare_gates():
-            nc.gpsimd.tensor_tensor(out=gate[:], in0=tao_sb[:], in1=tao_sb[:], op=ALU.mult)
-            nc.gpsimd.tensor_tensor(out=gate[:], in0=gate[:], in1=half_powers[:], op=ALU.pow)
+            nc.scalar.activation(out=gate[:], in_=tao_sb[:], func=ACT.Abs)
             nc.gpsimd.tensor_scalar(
                 out=gate[:], in0=gate[:], scalar1=1e-08, scalar2=1.0, op0=ALU.max, op1=ALU.min
             )
@@ -249,8 +255,8 @@ def tile_retentionmechanism_pc_t_kernel(
                 if c < PACK - 1:
                     update_slice(b, c)
                 if b + 2 < V_BLOCKS:
-                    for i in FIRST_AFTER_SECOND[c]:
-                        first_stage(b + 2, product_order(b + 2)[i])
+                    for s in FIRST_AFTER_SECOND[c]:
+                        first_stage(b + 2, s)
             if b - 1 in GRAM_BLOCKS:
                 gram_squares(b - 1, range(PIECES))
 
@@ -300,7 +306,7 @@ def tile_retentionmechanism_pc_t_kernel(
                 op1=ALU.add,
                 accum_out=variance[:],
             )
-            nc.gpsimd.tensor_tensor(out=variance[:], in0=variance[:], in1=half_powers[:, 0:1], op=ALU.pow)
+            nc.gpsimd.tensor_tensor(out=variance[:], in0=variance[:], in1=half_power[:], op=ALU.pow)
             factor = keep.tile([P, 1], F32, name=name + "_factor")
             nc.vector.tensor_scalar(
                 out=factor[:], in0=variance[:], scalar1=slope, scalar2=offset, op0=ALU.mult, op1=ALU.add
@@ -315,8 +321,8 @@ def tile_retentionmechanism_pc_t_kernel(
             one = keep.tile([P, 1], F32)
             nc.vector.memset(one[:], 1.0)
             nc.scalar.activation(out=one[:], in_=one[:], func=ACT.Abs_reciprocal_sqrt)
-            half_powers = keep.tile([P, 2], F32)
-            nc.gpsimd.memset(half_powers[:], 0.5)
+            half_power = keep.tile([P, 1], F32)
+            nc.gpsimd.memset(half_power[:], 0.5)
             mean_of_1 = keep.tile([P, P], F32)
             nc.gpsimd.memset(mean_of_1[:], 1.0 / COUNT_1)
             mean_of_2 = keep.tile([P, P], F32)
@@ -364,9 +370,10 @@ def tile_retentionmechanism_pc_t_kernel(
             for i in range(WARM_UP):
                 nc.tensor.matmul(out=warm[:], lhsT=ident[:], rhs=ao_sb[:, i % PACK, :], start=True, stop=True)
             inv_rms = keep.tile([P, PACK], F32)
-            nc.scalar.activation(
-                out=inv_rms[:], in_=sum_sq[:], func=ACT.Abs_reciprocal_sqrt, scale=1.0 / E, bias=EPS_RMS
-            )
+            for rows in (slice(0, PACK - 1), slice(PACK - 1, PACK)):
+                nc.scalar.activation(
+                    out=inv_rms[:, rows], in_=sum_sq[:, rows], func=ACT.Abs_reciprocal_sqrt, scale=1.0 / E, bias=EPS_RMS
+                )
             nc.scalar.activation(out=one[:], in_=one[:], func=ACT.Silu)
             a_scaled = keep.tile([P, PACK, E], BF16)
             for t in range(PACK):
@@ -384,18 +391,8 @@ def tile_retentionmechanism_pc_t_kernel(
                     out=a_grouped[:, u0 * P : u1 * P, :].rearrange("p (u c) t -> p u c t", c=P),
                     in_=a_scaled[:].rearrange("p t (c u) -> p u c t", u=PACK)[:, u0:u1, :, :],
                 )
-            for i, cols in enumerate(HALF_BLOCKS):
-                laid_out = psum_first.tile([P, BLOCK // 2, PACK], BF16, tag="bank%d" % i)
-                for s in range(PIECES // 2):
-                    piece = slice(s * P, (s + 1) * P)
-                    nc.tensor.matmul(
-                        out=laid_out[:, piece, :].rearrange("p j t -> p (j t)"),
-                        lhsT=ident[:],
-                        rhs=v_sb[:, 0, :, cols.start + s * P : cols.start + (s + 1) * P].rearrange("p t j -> p j t"),
-                        start=True,
-                        stop=True,
-                    )
-                nc.scalar.copy(out=buffer_of(0)[:, cols, :], in_=laid_out[:])
+            for cols in HALF_BLOCKS:
+                group_on_tensor(0, cols)
             for u0, u1 in u_halves:
                 nc.vector.quantize_mx(
                     out=a_codes[:, u0 * P : u1 * P].bitcast(FP8X4),
@@ -425,7 +422,7 @@ def tile_retentionmechanism_pc_t_kernel(
                 if b + 2 < V_BLOCKS:
                     v_quantised[b + 2] = quantise_block(b + 2)
                 if b == 0:
-                    group_on(nc.scalar.copy, 3, SCALAR_COLS)
+                    group_on_tensor(3, SCALAR_COLS)
                     group_on_gpsimd(3, slice(SCALAR_COLS.stop, BLOCK))
                 elif b + 3 < V_BLOCKS:
                     group_on_gpsimd(b + 3, slice(0, BLOCK))
@@ -448,30 +445,33 @@ def tile_retentionmechanism_pc_t_kernel(
             share_1 = mean_square(sums_1, mean_of_1, "first")
             factor_1 = norm_factor(squares_1, mean_of_1, share_1, slope[:, 0:1], offset[:, 0:1], "first")
 
-        wo_grouped = singles.tile([P, E, PACK], BF16, align_bytes=64, tag="alone")
-        for c in range(PACK):
-            flipped = psum_first.tile([P, PACK, P], BF16, tag="bank%d" % c)
-            for t in range(PACK):
-                nc.tensor.transpose(flipped[:, t, :], wo_sb[:, c, t * P : (t + 1) * P], ident[:])
-            nc.scalar.copy(
-                out=wo_grouped[:, c * P : (c + 1) * P, :], in_=flipped[:].rearrange("p t i -> p i t")
-            )
-        quantise(wo_codes[:], wo_scales[:], wo_grouped[:].rearrange("p i t -> p (i t)"))
-        silu_wo = singles.tile([P, E, PACK], BF16, align_bytes=64, tag="alone")
-        for s in range(PIECES):
-            silu_of(multiply_by_a(wo_codes, wo_scales, s), silu_wo, s)
-        silu_wo_codes = keep.tile([P, E], U32, align_bytes=64)
-        silu_wo_scales = keep.tile([P, E], U8, align_bytes=64)
-        quantise(silu_wo_codes[:], silu_wo_scales[:], silu_wo[:].rearrange("p i t -> p (i t)"))
-        update_second_weight(silu_wo_codes, silu_wo_scales)
-        share_2 = mean_square(sums_2, mean_of_2, "second")
-        factor_2 = norm_factor(squares_2, mean_of_2, share_2, slope[:, 1:2], offset[:, 1:2], "second")
+            def scale_and_store(c, edges):
+                for start, stop in zip(edges[:-1], edges[1:]):
+                    piece = z1[:, c, start:stop]
+                    nc.vector.tensor_scalar(out=piece, in0=piece, scalar1=factor_1[:], scalar2=None, op0=ALU.mult)
+                    nc.sync.dma_start(out=out1_dram[:, c, start:stop], in_=piece)
 
-        for c in range(PACK):
-            edges = [0, BLOCK // 2, BLOCK, 2 * BLOCK, Q, J] if c == 0 else [0, Q, J]
-            for start, stop in zip(edges[:-1], edges[1:]):
-                piece = z1[:, c, start:stop]
-                nc.vector.tensor_scalar(out=piece, in0=piece, scalar1=factor_1[:], scalar2=None, op0=ALU.mult)
-                nc.sync.dma_start(out=out1_dram[:, c, start:stop], in_=piece)
-        nc.scalar.activation(out=z2[:], in_=z2[:], func=ACT.Copy, scale=factor_2[:])
-        nc.sync.dma_start(out=out2_dram, in_=z2[:])
+            wo_grouped = singles.tile([P, E, PACK], BF16, align_bytes=64, tag="alone")
+            for c in range(PACK):
+                flipped = psum_first.tile([P, PACK, P], BF16, tag="bank")
+                for t in range(PACK):
+                    nc.tensor.transpose(flipped[:, t, :], wo_sb[:, c, t * P : (t + 1) * P], ident[:])
+                nc.scalar.copy(
+                    out=wo_grouped[:, c * P : (c + 1) * P, :], in_=flipped[:].rearrange("p t i -> p i t")
+                )
+            scale_and_store(0, [0, BLOCK // 2, BLOCK, 2 * BLOCK, Q, J])
+            quantise(wo_codes[:], wo_scales[:], wo_grouped[:].rearrange("p i t -> p (i t)"))
+            silu_wo = singles.tile([P, E, PACK], BF16, align_bytes=64, tag="alone")
+            for s in range(PIECES):
+                silu_of(multiply_by_a(wo_codes, wo_scales, s), silu_wo, s)
+            scale_and_store(1, [0, Q, J])
+            scale_and_store(2, [0, Q, J])
+            silu_wo_codes = keep.tile([P, E], U32, align_bytes=64)
+            silu_wo_scales = keep.tile([P, E], U8, align_bytes=64)
+            quantise(silu_wo_codes[:], silu_wo_scales[:], silu_wo[:].rearrange("p i t -> p (i t)"))
+            update_second_weight(silu_wo_codes, silu_wo_scales)
+            scale_and_store(3, [0, Q, J])
+            share_2 = mean_square(sums_2, mean_of_2, "second")
+            factor_2 = norm_factor(squares_2, mean_of_2, share_2, slope[:, 1:2], offset[:, 1:2], "second")
+            nc.scalar.activation(out=z2[:], in_=z2[:], func=ACT.Copy, scale=factor_2[:])
+            nc.sync.dma_start(out=out2_dram, in_=z2[:])

@@ -200,7 +200,8 @@ def tile_retentionmechanism_pc_t_kernel(
         offset = keep.tile([P, 2], F32)
 
         def prepare_gates():
-            nc.scalar.activation(out=gate[:], in_=tao_sb[:], func=ACT.Abs)
+            nc.gpsimd.tensor_tensor(out=gate[:], in0=tao_sb[:], in1=tao_sb[:], op=ALU.mult)
+            nc.gpsimd.tensor_tensor(out=gate[:], in0=gate[:], in1=half_powers[:], op=ALU.pow)
             nc.gpsimd.tensor_scalar(
                 out=gate[:], in0=gate[:], scalar1=1e-08, scalar2=1.0, op0=ALU.max, op1=ALU.min
             )
@@ -306,7 +307,7 @@ def tile_retentionmechanism_pc_t_kernel(
                 op1=ALU.add,
                 accum_out=variance[:],
             )
-            nc.gpsimd.tensor_tensor(out=variance[:], in0=variance[:], in1=half_power[:], op=ALU.pow)
+            nc.gpsimd.tensor_tensor(out=variance[:], in0=variance[:], in1=half_powers[:, 0:1], op=ALU.pow)
             factor = keep.tile([P, 1], F32, name=name + "_factor")
             nc.vector.tensor_scalar(
                 out=factor[:], in0=variance[:], scalar1=slope, scalar2=offset, op0=ALU.mult, op1=ALU.add
@@ -321,8 +322,8 @@ def tile_retentionmechanism_pc_t_kernel(
             one = keep.tile([P, 1], F32)
             nc.vector.memset(one[:], 1.0)
             nc.scalar.activation(out=one[:], in_=one[:], func=ACT.Abs_reciprocal_sqrt)
-            half_power = keep.tile([P, 1], F32)
-            nc.gpsimd.memset(half_power[:], 0.5)
+            half_powers = keep.tile([P, 2], F32)
+            nc.gpsimd.memset(half_powers[:], 0.5)
             mean_of_1 = keep.tile([P, P], F32)
             nc.gpsimd.memset(mean_of_1[:], 1.0 / COUNT_1)
             mean_of_2 = keep.tile([P, P], F32)
@@ -465,13 +466,13 @@ def tile_retentionmechanism_pc_t_kernel(
             for s in range(PIECES):
                 silu_of(multiply_by_a(wo_codes, wo_scales, s), silu_wo, s)
             scale_and_store(1, [0, Q, J])
-            scale_and_store(2, [0, Q, J])
+            scale_and_store(2, [0, J])
             silu_wo_codes = keep.tile([P, E], U32, align_bytes=64)
             silu_wo_scales = keep.tile([P, E], U8, align_bytes=64)
             quantise(silu_wo_codes[:], silu_wo_scales[:], silu_wo[:].rearrange("p i t -> p (i t)"))
             update_second_weight(silu_wo_codes, silu_wo_scales)
-            scale_and_store(3, [0, Q, J])
+            scale_and_store(3, [0, J])
             share_2 = mean_square(sums_2, mean_of_2, "second")
             factor_2 = norm_factor(squares_2, mean_of_2, share_2, slope[:, 1:2], offset[:, 1:2], "second")
-            nc.scalar.activation(out=z2[:], in_=z2[:], func=ACT.Copy, scale=factor_2[:])
+            nc.vector.tensor_scalar(out=z2[:], in0=z2[:], scalar1=factor_2[:], scalar2=None, op0=ALU.mult)
             nc.sync.dma_start(out=out2_dram, in_=z2[:])

from contextlib import ExitStack

import concourse.mybir as mybir
from concourse.masks import make_identity

F32 = mybir.dt.float32
BF16 = mybir.dt.bfloat16
I32 = mybir.dt.int32
U32 = mybir.dt.uint32
U8 = mybir.dt.uint8
FP8X4 = mybir.dt.float8_e4m3fn_x4
ACT = mybir.ActivationFunctionType
ALU = mybir.AluOpType

P = 128
PACK = 4
E = P * PACK
HALVES = 2
Q = 2048
BLOCK = 512
SCALAR_COLS = slice(0, P)
PIECES = BLOCK // P
HALF_BLOCKS = (slice(0, BLOCK // 2), slice(BLOCK // 2, BLOCK))
BLOCKS_PER_HALF = Q // BLOCK
V_BLOCKS = HALVES * BLOCKS_PER_HALF
J = HALVES * Q
COUNT_1 = E * J
COUNT_2 = E * E
GRAM_BLOCKS = range(V_BLOCKS - 1)
GRAM_SLICE = PACK - 1
FIRST_AFTER_SECOND = ((), (0, 1), (2,), (3,))
GATE_BLOCK = V_BLOCKS - 3
GRAM_PART = GRAM_SLICE
PARTS = V_BLOCKS * PACK
WARM_UP = 4
EPS_RMS = 1.1920929e-07
EPS_STD = 1e-08
TARGET_STD = 2048.0**-0.5

FLOPS = 2 * 2 * E * E * (HALVES * Q + E)


def tile_retentionmechanism_pc_t_kernel(
    tc, ao, w_swiglu, w_out, out_w_words, out_w_scales, tao, out_0, out_1
):
    nc = tc.nc
    ao_dram = ao.rearrange("(t p) e -> p t e", p=P)
    v_dram = w_swiglu.rearrange("(t p h) q -> p t h q", p=P, h=HALVES)
    out1_dram = out_0.rearrange("(t p h) q -> p t (h q)", p=P, h=HALVES)
    out2_dram = out_1.rearrange("(p c) n -> p c n", p=P)

    with ExitStack() as ctx:
        keep = ctx.enter_context(tc.tile_pool(name="keep", bufs=1))
        stage = ctx.enter_context(tc.tile_pool(name="stage", bufs=6))
        singles = ctx.enter_context(tc.tile_pool(name="singles", bufs=2))
        unread = ctx.enter_context(tc.tile_pool(name="unread", bufs=2))
        psum_first = ctx.enter_context(tc.psum_pool(name="psum_first", bufs=4))
        psum_second = ctx.enter_context(tc.psum_pool(name="psum_second", bufs=3))
        psum_gram = ctx.enter_context(tc.psum_pool(name="psum_gram", bufs=1))

        ao_sb = keep.tile([P, PACK, E], BF16)
        v_sb = keep.tile([P, V_BLOCKS, PACK, BLOCK], BF16)
        wo_sb = keep.tile([P, PACK, E], BF16)
        tao_sb = keep.tile([P, 2], BF16)
        w_codes = keep.tile([P, E], U32, align_bytes=64)
        w_scales = keep.tile([P, E], U8, align_bytes=64)
        a_codes = keep.tile([P, E], U32, align_bytes=64)
        a_scales = keep.tile([P, E], U8, align_bytes=64)
        v0_codes = keep.tile([P, BLOCK], U32, align_bytes=64)
        v0_scales = keep.tile([P, BLOCK], U8, align_bytes=64)
        wo_codes = keep.tile([P, E], U32, align_bytes=64)
        wo_scales = keep.tile([P, E], U8, align_bytes=64)
        z1 = keep.tile([P, PACK, J], F32)
        z2 = keep.tile([P, PACK, E], F32)
        sums_1 = keep.tile([P, PARTS], F32)
        squares_1 = keep.tile([P, PARTS], F32)
        sums_2 = keep.tile([P, PACK], F32)
        squares_2 = keep.tile([P, PACK], F32)

        grouped = keep.tile([P, 3, BLOCK, PACK], BF16, align_bytes=64)
        v_quantised = {}
        h_quantised = {}

        def buffer_of(b):
            return grouped[:, b % 3, :, :]

        def z1_block(b):
            return z1[:, :, b * BLOCK : (b + 1) * BLOCK]

        def columns_of(b):
            q0 = (b % BLOCKS_PER_HALF) * BLOCK
            return b // BLOCKS_PER_HALF, slice(q0, q0 + BLOCK)

        def load_v_block(b):
            half, cols = columns_of(b)
            nc.sync.dma_start(out=v_sb[:, b, :, :], in_=v_dram[:, :, half, cols])

        def group_on(engine_copy, b, cols):
            engine_copy(
                out=buffer_of(b)[:, cols, :].rearrange("p (c i) t -> p c t i", i=4),
                in_=v_sb[:, b, :, cols].rearrange("p t (c i) -> p c t i", i=4),
            )

        def group_on_gpsimd(b, cols):
            nc.gpsimd.tensor_scalar(
                out=buffer_of(b)[:, cols, :].rearrange("p (c i) t -> p c t i", i=4),
                in0=v_sb[:, b, :, cols].rearrange("p t (c i) -> p c t i", i=4),
                scalar1=1.0,
                scalar2=0.0,
                op0=ALU.mult,
                op1=ALU.add,
            )

        def group_on_tensor(b, cols):
            laid_out = psum_first.tile([P, BLOCK // 2, PACK], BF16, tag="bank")
            width = cols.stop - cols.start
            for k in range(0, width, P):
                nc.tensor.matmul(
                    out=laid_out[:, k : k + P, :].rearrange("p j t -> p (j t)"),
                    lhsT=ident[:],
                    rhs=v_sb[:, b, :, cols.start + k : cols.start + k + P].rearrange("p t j -> p j t"),
                    start=True,
                    stop=True,
                )
            nc.scalar.copy(out=buffer_of(b)[:, cols, :], in_=laid_out[:, 0:width, :])

        def quantise(codes, scales, values):
            nc.vector.quantize_mx(out=codes.bitcast(FP8X4), scales=scales, in_=values)

        def multiply_by_a(x_codes, x_scales, s):
            cols = slice(s * P, (s + 1) * P)
            bank = psum_first.tile([P, PACK, P], F32)
            for t in range(PACK):
                e_slice = slice(t * P, (t + 1) * P)
                nc.tensor.matmul_mx(
                    out=bank[:, t, :],
                    lhsT=a_codes[:, e_slice].bitcast(FP8X4),
                    lhsT_scale=a_scales[:, e_slice],
                    rhs=x_codes[:, cols].bitcast(FP8X4),
                    rhs_scale=x_scales[:, cols],
                    start=True,
                    stop=True,
                )
            return bank

        def silu_of(bank, silu, s):
            nc.scalar.activation(
                out=silu[:, s * P : (s + 1) * P, :], in_=bank[:].rearrange("p t j -> p j t"), func=ACT.Silu
            )

        first_products = {}

        def first_stage(b, s):
            first_products[b, s] = multiply_by_a(*v_quantised[b], s)

        def silu_block(b):
            for s in range(PIECES):
                silu_of(first_products[b, s], buffer_of(b), s)

        def quantise_block(b):
            codes = stage.tile([P, BLOCK], U32, align_bytes=64)
            scales = stage.tile([P, BLOCK], U8, align_bytes=64)
            quantise(codes[:], scales[:], buffer_of(b).rearrange("p j t -> p (j t)"))
            return codes[:], scales[:]

        def add_weight(z, product, weight, sums, part):
            nc.vector.scalar_tensor_tensor(
                out=z,
                in0=product,
                scalar=1.0,
                in1=weight,
                op0=ALU.mult,
                op1=ALU.add,
                accum_out=sums[:, part : part + 1],
            )

        def sum_squares(z, squares, part):
            slices, columns = z.shape[1], z.shape[2]
            each_square = unread.tile([P, PACK, BLOCK], BF16)
            nc.scalar.activation(
                out=each_square[:, 0:slices, 0:columns], in_=z, func=ACT.Square, accum_out=squares[:, part : part + 1]
            )

        gram = psum_gram.tile([P, P], F32)

        def gram_squares(b, pieces):
            for s in pieces:
                x = z1_block(b)[:, GRAM_SLICE, s * P : (s + 1) * P]
                nc.tensor.matmul(
                    out=gram[:],
                    lhsT=x,
                    rhs=x,
                    start=(b == GRAM_BLOCKS[0] and s == 0),
                    stop=(b == GRAM_BLOCKS[-1] and s == PIECES - 1),
                )

        gate = keep.tile([P, 2], F32)
        inv_gate = keep.tile([P, 2], F32)
        slope = keep.tile([P, 2], F32)
        offset = keep.tile([P, 2], F32)

        def prepare_gates():
            nc.gpsimd.tensor_tensor(out=gate[:], in0=tao_sb[:], in1=tao_sb[:], op=ALU.mult)
            nc.gpsimd.tensor_tensor(out=gate[:], in0=gate[:], in1=half_powers[:], op=ALU.pow)
            nc.gpsimd.tensor_scalar(
                out=gate[:], in0=gate[:], scalar1=1e-08, scalar2=1.0, op0=ALU.max, op1=ALU.min
            )
            nc.gpsimd.tensor_scalar(
                out=gate[:], in0=gate[:], scalar1=TARGET_STD, scalar2=0.0, op0=ALU.mult, op1=ALU.add
            )

        def prepare_factors():
            nc.vector.reciprocal(out=inv_gate[:], in_=gate[:])
            for w, count in enumerate((COUNT_1, COUNT_2)):
                nc.gpsimd.tensor_scalar(
                    out=slope[:, w : w + 1],
                    in0=inv_gate[:, w : w + 1],
                    scalar1=(count / (count - 1.0)) ** 0.5,
                    scalar2=0.0,
                    op0=ALU.mult,
                    op1=ALU.add,
                )
            nc.gpsimd.tensor_scalar(
                out=offset[:], in0=inv_gate[:], scalar1=EPS_STD, scalar2=0.0, op0=ALU.mult, op1=ALU.add
            )

        def read_gram():
            diagonal = unread.tile([P, P], F32)
            nc.vector.scalar_tensor_tensor(
                out=diagonal[:],
                in0=gram[:],
                scalar=1.0,
                in1=ident_f32[:],
                op0=ALU.mult,
                op1=ALU.mult,
                accum_out=squares_1[:, GRAM_PART : GRAM_PART + 1],
            )

        products = {}

        def multiply_by_w(b):
            codes, scales = h_quantised[b]
            for c in range(PACK):
                n_slice = slice(c * P, (c + 1) * P)
                product = psum_second.tile([P, BLOCK], F32)
                nc.tensor.matmul_mx(
                    out=product[:],
                    lhsT=w_codes[:, n_slice].bitcast(FP8X4),
                    lhsT_scale=w_scales[:, n_slice],
                    rhs=codes.bitcast(FP8X4),
                    rhs_scale=scales,
                    start=True,
                    stop=True,
                )
                products[b, c] = product
                if c < PACK - 1:
                    update_slice(b, c)
                if b + 2 < V_BLOCKS:
                    for s in FIRST_AFTER_SECOND[c]:
                        first_stage(b + 2, s)
            if b - 1 in GRAM_BLOCKS:
                gram_squares(b - 1, range(PIECES))

        def update_slice(b, c):
            add_weight(z1_block(b)[:, c, :], products[b, c][:], v_sb[:, b, c, :], sums_1, b * PACK + c)

        def update_second_weight(h_codes, h_scales):
            for c in range(PACK):
                i_slice = slice(c * P, (c + 1) * P)
                product = psum_second.tile([P, BLOCK], F32)
                nc.tensor.matmul_mx(
                    out=product[:],
                    lhsT=h_codes[:, i_slice].bitcast(FP8X4),
                    lhsT_scale=h_scales[:, i_slice],
                    rhs=w_codes[:].bitcast(FP8X4),
                    rhs_scale=w_scales[:],
                    start=True,
                    stop=True,
                )
                add_weight(z2[:, c, :], product[:], wo_sb[:, c, :], sums_2, c)
                sum_squares(z2[:, c : c + 1, :], squares_2, c)

        def mean_square(sums, mean_of, name):
            parts = sums.shape[1]
            spread = psum_second.tile([P, parts], F32, tag="product")
            nc.tensor.matmul(out=spread[:], lhsT=mean_of[:], rhs=sums[:], start=True, stop=True)
            mean = keep.tile([P, 1], F32, name=name + "_mean")
            nc.vector.tensor_reduce(out=mean[:], in_=spread[:], axis=mybir.AxisListType.X, op=ALU.add)
            share = keep.tile([P, 1], F32, name=name + "_share")
            nc.vector.tensor_scalar(
                out=share[:], in0=mean[:], scalar1=mean[:], scalar2=-1.0 / parts, op0=ALU.mult, op1=ALU.mult
            )
            return share

        def norm_factor(squares, mean_of, share, slope, offset, name):
            parts = squares.shape[1]
            spread = psum_second.tile([P, parts], F32, tag="product")
            nc.tensor.matmul(out=spread[:], lhsT=mean_of[:], rhs=squares[:], start=True, stop=True)
            terms = keep.tile([P, parts], F32, name=name + "_terms")
            variance = keep.tile([P, 1], F32, name=name + "_variance")
            nc.vector.scalar_tensor_tensor(
                out=terms[:],
                in0=spread[:],
                scalar=1.0,
                in1=share[:].to_broadcast([P, parts]),
                op0=ALU.mult,
                op1=ALU.add,
                accum_out=variance[:],
            )
            nc.gpsimd.tensor_tensor(out=variance[:], in0=variance[:], in1=half_powers[:, 0:1], op=ALU.pow)
            factor = keep.tile([P, 1], F32, name=name + "_factor")
            nc.vector.tensor_scalar(
                out=factor[:], in0=variance[:], scalar1=slope, scalar2=offset, op0=ALU.mult, op1=ALU.add
            )
            nc.vector.reciprocal(out=factor[:], in_=factor[:])
            return factor

        with tc.manual_schedule():
            nc.vector.memset(w_scales[:].bitcast(I32), 0)
            nc.vector.memset(sums_1[:], 0.0)
            nc.vector.memset(squares_1[:], 0.0)
            one = keep.tile([P, 1], F32)
            nc.vector.memset(one[:], 1.0)
            nc.scalar.activation(out=one[:], in_=one[:], func=ACT.Abs_reciprocal_sqrt)
            half_powers = keep.tile([P, 2], F32)
            nc.gpsimd.memset(half_powers[:], 0.5)
            mean_of_1 = keep.tile([P, P], F32)
            nc.gpsimd.memset(mean_of_1[:], 1.0 / COUNT_1)
            mean_of_2 = keep.tile([P, P], F32)
            nc.gpsimd.memset(mean_of_2[:], 1.0 / COUNT_2)
            ident = keep.tile([P, P], BF16)
            make_identity(nc, ident[:])
            ident_f32 = keep.tile([P, P], F32)
            make_identity(nc, ident_f32[:])

            for t in range(PACK):
                nc.sync.dma_start(out=ao_sb[:, t, :], in_=ao_dram[:, t, :])
            load_v_block(0)
            load_v_block(1)
            nc.sync.dma_start(
                out=w_codes[:].bitcast(I32),
                in_=out_w_words.rearrange("g p n t -> (g p) (n t)").bitcast(I32),
            )
            scale_rows = out_w_scales.rearrange("g s n -> (g s) n").bitcast(I32)
            for r in range(PACK):
                nc.sync.dma_start(
                    out=w_scales[r:P:32, :].bitcast(I32), in_=scale_rows[r : 4 * PACK : PACK, :]
                )
            for b in range(2, V_BLOCKS):
                load_v_block(b)
            nc.sync.dma_start(out=wo_sb[:], in_=w_out.rearrange("(p c) d -> p c d", p=P))
            nc.sync.dma_start(out=tao_sb[:], in_=tao.rearrange("a b -> (a b)").partition_broadcast(P))

            sum_sq = keep.tile([P, PACK], F32)
            for t in range(0, PACK, 2):
                squares_s = unread.tile([P, BLOCK], BF16)
                nc.scalar.activation(
                    out=squares_s[:], in_=ao_sb[:, t, :], func=ACT.Square, accum_out=sum_sq[:, t : t + 1]
                )
                squares_v = unread.tile([P, BLOCK], F32)
                nc.vector.scalar_tensor_tensor(
                    out=squares_v[:],
                    in0=ao_sb[:, t + 1, :],
                    scalar=1.0,
                    in1=ao_sb[:, t + 1, :],
                    op0=ALU.mult,
                    op1=ALU.mult,
                    accum_out=sum_sq[:, t + 1 : t + 2],
                )
            warm = psum_second.tile([P, E], F32, tag="product")
            for i in range(WARM_UP):
                nc.tensor.matmul(out=warm[:], lhsT=ident[:], rhs=ao_sb[:, i % PACK, :], start=True, stop=True)
            inv_rms = keep.tile([P, PACK], F32)
            for rows in (slice(0, PACK - 1), slice(PACK - 1, PACK)):
                nc.scalar.activation(
                    out=inv_rms[:, rows], in_=sum_sq[:, rows], func=ACT.Abs_reciprocal_sqrt, scale=1.0 / E, bias=EPS_RMS
                )
            nc.scalar.activation(out=one[:], in_=one[:], func=ACT.Silu)
            a_scaled = keep.tile([P, PACK, E], BF16)
            for t in range(PACK):
                nc.vector.tensor_scalar(
                    out=a_scaled[:, t, :],
                    in0=ao_sb[:, t, :],
                    scalar1=inv_rms[:, t : t + 1],
                    scalar2=None,
                    op0=ALU.mult,
                )
            a_grouped = keep.tile([P, E, PACK], BF16, align_bytes=64)
            u_halves = [(u, u + 2) for u in (0, 2)]
            for u0, u1 in u_halves:
                nc.vector.tensor_copy(
                    out=a_grouped[:, u0 * P : u1 * P, :].rearrange("p (u c) t -> p u c t", c=P),
                    in_=a_scaled[:].rearrange("p t (c u) -> p u c t", u=PACK)[:, u0:u1, :, :],
                )
            for cols in HALF_BLOCKS:
                group_on_tensor(0, cols)
            for u0, u1 in u_halves:
                nc.vector.quantize_mx(
                    out=a_codes[:, u0 * P : u1 * P].bitcast(FP8X4),
                    scales=a_scales[:, u0 * P : u1 * P],
                    in_=a_grouped[:, u0 * P : u1 * P, :].rearrange("p c t -> p (c t)"),
                )

            def quantise_half_of_block_0(cols):
                quantise(v0_codes[:, cols], v0_scales[:, cols], buffer_of(0)[:, cols, :].rearrange("p j t -> p (j t)"))

            quantise_half_of_block_0(HALF_BLOCKS[0])
            group_on(nc.vector.tensor_copy, 1, slice(0, BLOCK))
            quantise_half_of_block_0(HALF_BLOCKS[1])
            v_quantised[0] = (v0_codes[:], v0_scales[:])
            v_quantised[1] = quantise_block(1)
            group_on(nc.vector.tensor_copy, 2, slice(0, BLOCK))

            for s in range(PIECES):
                first_stage(0, s)
            silu_block(0)
            for s in range(PIECES):
                first_stage(1, s)
            for b in range(V_BLOCKS):
                if b + 1 < V_BLOCKS:
                    silu_block(b + 1)
                h_quantised[b] = quantise_block(b)
                if b + 2 < V_BLOCKS:
                    v_quantised[b + 2] = quantise_block(b + 2)
                if b == 0:
                    group_on_tensor(3, SCALAR_COLS)
                    group_on_gpsimd(3, slice(SCALAR_COLS.stop, BLOCK))
                elif b + 3 < V_BLOCKS:
                    group_on_gpsimd(b + 3, slice(0, BLOCK))
                if b > 0:
                    update_slice(b - 1, PACK - 1)
                if b == GATE_BLOCK:
                    prepare_gates()
                if b == GATE_BLOCK + 1:
                    prepare_factors()
                multiply_by_w(b)
                if b > 0:
                    scalar_slices = GRAM_SLICE if b - 1 in GRAM_BLOCKS else PACK
                    sum_squares(z1_block(b - 1)[:, 0:scalar_slices, :], squares_1, (b - 1) * PACK)
            update_slice(V_BLOCKS - 1, PACK - 1)
            read_gram()
            b = V_BLOCKS - 1
            for c in range(PACK):
                sum_squares(z1_block(b)[:, c : c + 1, :], squares_1, b * PACK + c)

            share_1 = mean_square(sums_1, mean_of_1, "first")
            factor_1 = norm_factor(squares_1, mean_of_1, share_1, slope[:, 0:1], offset[:, 0:1], "first")

            def scale_and_store(c, edges):
                for start, stop in zip(edges[:-1], edges[1:]):
                    piece = z1[:, c, start:stop]
                    nc.vector.tensor_scalar(out=piece, in0=piece, scalar1=factor_1[:], scalar2=None, op0=ALU.mult)
                    nc.sync.dma_start(out=out1_dram[:, c, start:stop], in_=piece)

            wo_grouped = singles.tile([P, E, PACK], BF16, align_bytes=64, tag="alone")
            for c in range(PACK):
                flipped = psum_first.tile([P, PACK, P], BF16, tag="bank")
                for t in range(PACK):
                    nc.tensor.transpose(flipped[:, t, :], wo_sb[:, c, t * P : (t + 1) * P], ident[:])
                nc.scalar.copy(
                    out=wo_grouped[:, c * P : (c + 1) * P, :], in_=flipped[:].rearrange("p t i -> p i t")
                )
            scale_and_store(0, [0, BLOCK // 2, BLOCK, 2 * BLOCK, Q, J])
            quantise(wo_codes[:], wo_scales[:], wo_grouped[:].rearrange("p i t -> p (i t)"))
            silu_wo = singles.tile([P, E, PACK], BF16, align_bytes=64, tag="alone")
            for s in range(PIECES):
                silu_of(multiply_by_a(wo_codes, wo_scales, s), silu_wo, s)
            scale_and_store(1, [0, Q, J])
            scale_and_store(2, [0, J])
            silu_wo_codes = keep.tile([P, E], U32, align_bytes=64)
            silu_wo_scales = keep.tile([P, E], U8, align_bytes=64)
            quantise(silu_wo_codes[:], silu_wo_scales[:], silu_wo[:].rearrange("p i t -> p (i t)"))
            update_second_weight(silu_wo_codes, silu_wo_scales)
            scale_and_store(3, [0, J])
            share_2 = mean_square(sums_2, mean_of_2, "second")
            factor_2 = norm_factor(squares_2, mean_of_2, share_2, slope[:, 1:2], offset[:, 1:2], "second")
            nc.vector.tensor_scalar(out=z2[:], in0=z2[:], scalar1=factor_2[:], scalar2=None, op0=ALU.mult)
            nc.sync.dma_start(out=out2_dram, in_=z2[:])
